import numpy as np
import ml_dtypes


def mxq(x, axis, fmt="e4m3"):
    dtype, down = {"e4m3": (ml_dtypes.float8_e4m3fn, 7), "e5m2": (ml_dtypes.float8_e5m2, 14)}[fmt]
    v = np.moveaxis(np.asarray(x, np.float32).astype(ml_dtypes.bfloat16).astype(np.float64), axis, -1)
    blocks = v.reshape(v.shape[:-1] + (-1, 32))
    amax = np.abs(blocks).max(-1, keepdims=True)
    byte = np.maximum(np.where(amax > 0, np.frexp(amax)[1] - 1 + 127, 0) - down, 1)
    scale = np.exp2(byte - 127.0)
    codes = (blocks / scale).astype(np.float32).astype(dtype).astype(np.float64)
    return np.moveaxis((codes * scale).reshape(v.shape), -1, axis)


WIDE = False


def mx_kscale(k):
    if not WIDE:
        return np.ones(k)
    levels = np.array([10, -10, 5, -5, 0])
    a = np.random.permutation(np.resize(levels, k // 512 * 4)).reshape(k // 512, 4)
    idx = np.arange(k)
    return np.exp2(a[idx // 512, idx % 128 // 32])


BF16 = ml_dtypes.bfloat16


def bf(x):
    return np.asarray(x, np.float32).astype(BF16)


def f64(x):
    return np.asarray(x).astype(np.float64)


S, B, ND, NS, HN, BT, C, Hd, Wd = 8, 64, 32, 96, 512, 512, 3, 64, 64
P = C * Hd * Wd
EPS = 1e-9
SELU_ALPHA = 1.6732632423543772848170429916717
SELU_SCALE = 1.0507009873554804934193349852946


def selu(v):
    return SELU_SCALE * np.where(v > 0, v, SELU_ALPHA * np.expm1(np.minimum(v, 0.0)))


def sigmoid(v):
    return 1.0 / (1.0 + np.exp(-v))


def setup_inputs():
    t = mx_kscale(HN)
    return {"digits": bf(np.random.random_sample((S, B, ND))),
            "styles": bf(np.random.standard_normal((S, B, NS))),
            "images": bf(np.random.random_sample((S, B, C, Hd, Wd))),
            "W_h": bf(np.random.standard_normal((ND + NS, HN)) / np.sqrt(ND + NS) * t),
            "b_h": bf(np.random.standard_normal(HN) * 0.5 * t),
            "W1": bf(np.random.standard_normal((HN, BT)) * 1.4 / np.sqrt(HN) / t[:, None]),
            "b1": bf(np.random.standard_normal(BT) * 0.5),
            "W2": bf(np.random.standard_normal((BT, P)) / np.sqrt(BT)),
            "b2": bf(np.random.standard_normal(P) * 0.5)}


def reference(digits, styles, images, W_h, b_h, W1, b1, W2, b2):
    h = np.maximum(np.concatenate([f64(digits), f64(styles)], axis=-1) @ f64(W_h) + f64(b_h), 0.0)
    t = selu((mxq(h, 2, "e4m3") @ mxq(f64(W1), 0, "e4m3")) + f64(b1))
    x_hat = sigmoid((mxq(t, 2, "e4m3") @ mxq(f64(W2), 0, "e4m3")) + f64(b2))
    images_mean = x_hat.reshape(x_hat.shape[0], x_hat.shape[1], C, Hd, Wd)
    img = f64(images)
    loss = -(np.log(images_mean + EPS) * img + np.log(1.0 - images_mean + EPS) * (1.0 - img)).sum(-1)
    return loss

@@ -1,0 +1,337 @@
+import math
+from contextlib import ExitStack
+
+import concourse.masks as masks
+import concourse.mybir as mybir
+
+F32 = mybir.dt.float32
+BF16 = mybir.dt.bfloat16
+U32 = mybir.dt.uint32
+U8 = mybir.dt.uint8
+FP8X4 = mybir.dt.float8_e4m3fn_x4
+ACT = mybir.ActivationFunctionType
+ALU = mybir.AluOpType
+AX = mybir.AxisListType
+
+P = 128
+TOK = 512
+NT = 4
+HN = 512
+CH = 12288
+BLK = 512
+NBLK = CH // BLK
+BB = 6
+NBATCH = NBLK // BB
+CHUNK = 1024
+NCHUNK = CH // CHUNK
+EPS = 1e-9
+LOG_EPS = math.log(EPS)
+SELU_ALPHA = 1.6732632423543772848170429916717
+SELU_SCALE = 1.0507009873554804934193349852946
+SA = SELU_SCALE * SELU_ALPHA
+
+FLOPS = 2 * TOK * (128 * HN + HN * HN + HN * CH)
+
+
+def tile_decoder_kernel(tc, digits, styles, images, W_h, b_h, W1, b1, W2, b2, out):
+    nc = tc.nc
+    dig_v = digits.rearrange("s b c -> (s b) c").rearrange("(t p) c -> p t c", p=P)
+    sty_v = styles.rearrange("s b c -> (s b) c").rearrange("(t p) c -> p t c", p=P)
+    img_v = images.rearrange("s b c h w -> (s b) (c h w)").rearrange("(t p) n -> p t n", p=P)
+    out_v = out.rearrange("s b c h -> (s b) (c h)").rearrange("(t p) g -> p t g", p=P)
+    w1_v = W1.rearrange("(j p) n -> p j n", p=P)
+    w2_v = W2.rearrange("(j p) n -> p j n", p=P)
+
+    with ExitStack() as ctx:
+        ctx.enter_context(tc.manual_schedule())
+        const = ctx.enter_context(tc.tile_pool(name="const", bufs=1))
+        yp = ctx.enter_context(tc.tile_pool(name="yp", bufs=9))
+        bp = ctx.enter_context(tc.tile_pool(name="bp", bufs=5))
+        rawp = ctx.enter_context(tc.tile_pool(name="rawp", bufs=3))
+        gp = ctx.enter_context(tc.tile_pool(name="gp", bufs=2))
+        cp = ctx.enter_context(tc.tile_pool(name="cp", bufs=2 * BB))
+        imp = ctx.enter_context(tc.tile_pool(name="imp", bufs=3))
+        pu = ctx.enter_context(tc.psum_pool(name="pu", bufs=3))
+        pi = ctx.enter_context(tc.psum_pool(name="pi", bufs=4))
+        ps = ctx.enter_context(tc.psum_pool(name="ps", bufs=1))
+
+        raws = {}
+        imgs = {}
+        grouped = {}
+        codes = {}
+        planes = {}
+        ubank = {}
+        ytile = {}
+        btile = {}
+        itile = {}
+        stile = {}
+
+        ident_bf = const.tile([P, P], BF16, name="ident_bf")
+        masks.make_identity(nc, ident_bf[:])
+        ident_f = const.tile([P, P], F32, name="ident_f")
+        masks.make_identity(nc, ident_f[:])
+        brow = const.tile([P, P], BF16, name="brow")
+        nc.vector.memset(brow[:], 0.0)
+        b2rows = const.tile([P, BLK], BF16, name="b2rows")
+        nc.vector.memset(b2rows[:], 0.0)
+        eps_b = const.tile([P, 1], F32, name="eps_b")
+        nc.vector.memset(eps_b[:], EPS)
+        one_eps_b = const.tile([P, 1], F32, name="one_eps_b")
+        nc.vector.memset(one_eps_b[:], 1.0)
+        nc.vector.tensor_scalar_add(out=one_eps_b[:], in0=one_eps_b[:], scalar1=EPS)
+
+        cat = const.tile([P, NT, P], BF16, name="cat")
+        nc.sync.dma_start(out=cat[:, :, 0:32], in_=dig_v)
+        nc.sync.dma_start(out=cat[:, :, 32:128], in_=sty_v)
+        wh = const.tile([P, HN], BF16, name="wh")
+        nc.sync.dma_start(out=wh[:], in_=W_h)
+        nc.sync.dma_start(out=brow[0:4, :], in_=b_h.rearrange("(j p) -> j p", p=P))
+        nc.sync.dma_start(out=brow[4:8, :], in_=b1.rearrange("(j p) -> j p", p=P))
+        raw1 = const.tile([P, 4, HN], BF16, name="raw1")
+        nc.sync.dma_start(out=raw1[:], in_=w1_v)
+        nc.sync.dma_start(out=b2rows[0:NBLK, :], in_=b2.rearrange("(b x) -> b x", x=BLK))
+
+        def load_w2(c):
+            raw = rawp.tile([P, 4, CHUNK], BF16, name="raw", tag="raw")
+            nc.sync.dma_start(out=raw[:], in_=w2_v[:, :, c * CHUNK:(c + 1) * CHUNK])
+            raws[c] = raw
+
+        def load_img(c):
+            im = imp.tile([P, NT, CHUNK], BF16, name="im", tag="im")
+            nc.sync.dma_start(out=im[:], in_=img_v[:, :, c * CHUNK:(c + 1) * CHUNK])
+            imgs[c] = im
+
+        for c in range(3):
+            load_w2(c)
+        for c in range(3):
+            load_img(c)
+
+        def prep_copy(b):
+            g2 = gp.tile([P, 4 * BLK], BF16, name="g2", tag="g2", align_bytes=64)
+            lo = (b % 2) * BLK
+            nc.vector.tensor_copy(
+                out=g2[:].rearrange("p (r q j) -> p r q j", r=4, j=4),
+                in_=raws[b // 2][:, :, lo:lo + BLK].rearrange("p j (q r) -> p r q j", r=4),
+            )
+            grouped[b] = g2
+            if b % 2 == 1 and b // 2 + 3 < NCHUNK:
+                load_w2(b // 2 + 3)
+
+        def prep_quant(b):
+            cd = cp.tile([P, BLK], U32, name="cd", tag="cd", align_bytes=64)
+            pl = cp.tile([P, BLK], U8, name="pl", tag="pl", align_bytes=64)
+            nc.vector.quantize_mx(out=cd[:].bitcast(FP8X4), scales=pl[:], in_=grouped[b][:])
+            codes[b] = cd
+            planes[b] = pl
+
+        def mx(b, r):
+            u = pu.tile([P, TOK], F32, name="u", tag="u")
+            nc.tensor.matmul_mx(
+                out=u[:],
+                lhsT=codes[b][:, r * P:(r + 1) * P].bitcast(FP8X4),
+                lhsT_scale=planes[b][:, r * P:(r + 1) * P],
+                rhs=t_codes[:].bitcast(FP8X4),
+                rhs_scale=t_plane[:],
+                start=True,
+                stop=True,
+            )
+            ubank[(b, r)] = u
+
+        def sig(b, r):
+            if r == 0:
+                ytile[b] = yp.tile([P, 4, TOK], F32, name="y", tag="y")
+            nc.scalar.activation(
+                out=ytile[b][:, r, :], in_=ubank[(b, r)][:], func=ACT.Sigmoid,
+                bias=nb2[:, 4 * b + r:4 * b + r + 1], scale=-1.0,
+            )
+
+        def logs(b):
+            btile[b] = bp.tile([P, 4, TOK], F32, name="bt", tag="bt")
+            nc.scalar.activation(out=btile[b][:], in_=ytile[b][:], func=ACT.Ln,
+                                 bias=eps_b[:, 0:1], scale=1.0)
+            nc.scalar.activation(out=ytile[b][:], in_=ytile[b][:], func=ACT.Ln,
+                                 bias=one_eps_b[:, 0:1], scale=-1.0)
+
+        def imgt(b):
+            lo = (b % 2) * BLK
+            for s in range(2):
+                it = pi.tile([P, TOK], F32, name="it", tag="it")
+                for t in range(NT):
+                    words = imgs[b // 2][:, t, lo:lo + BLK].bitcast(F32)
+                    nc.tensor.transpose(
+                        out=it[:, t * P:(t + 1) * P],
+                        in_=words.rearrange("p (q s) -> p s q", s=2)[:, s, :],
+                        identity=ident_f[:],
+                    )
+                itile[(b, s)] = it
+            if b % 2 == 1 and b // 2 + 3 < NCHUNK:
+                load_img(b // 2 + 3)
+
+        def uv(b):
+            for s in range(2):
+                iv = itile[(b, s)][:].bitcast(BF16).rearrange("p (t e) -> p e t", e=2)
+                a_s = ytile[b][:, 2 * s:2 * s + 2, :]
+                b_s = btile[b][:, 2 * s:2 * s + 2, :]
+                nc.vector.scalar_tensor_tensor(out=a_s, in0=a_s, scalar=LOG_EPS, in1=iv,
+                                               op0=ALU.max, op1=ALU.mult)
+                nc.vector.scalar_tensor_tensor(out=b_s, in0=iv, scalar=1.0, in1=b_s,
+                                               op0=ALU.subtract, op1=ALU.mult)
+
+        def zed(b):
+            nc.gpsimd.tensor_tensor(out=ytile[b][:], in0=btile[b][:], in1=ytile[b][:],
+                                    op=ALU.subtract)
+
+        def summ(b):
+            st = ps.tile([P, TOK], F32, name="st", tag="st")
+            for t in range(NT):
+                for r in range(4):
+                    nc.tensor.matmul(
+                        out=st[:, t * P:(t + 1) * P],
+                        lhsT=ytile[b][:, r, t * P:(t + 1) * P],
+                        rhs=ident_f[:],
+                        is_transpose=True,
+                        start=(r == 0),
+                        stop=(r == 3),
+                    )
+            stile[b] = st
+
+        def red(b):
+            nc.vector.tensor_reduce(
+                out=res[:, :, 8 * b:8 * b + 8],
+                in_=stile[b][:].rearrange("p (t g w) -> p t g w", t=NT, g=8),
+                axis=AX.X, op=ALU.add,
+            )
+
+        cat_ps = pi.tile([P, TOK], BF16, name="cat_ps", tag="it")
+        for t in range(NT):
+            nc.tensor.transpose(out=cat_ps[:, t * P:(t + 1) * P], in_=cat[:, t, :],
+                                identity=ident_bf[:])
+        cat_t = const.tile([P, TOK], BF16, name="cat_t")
+        nc.vector.tensor_copy(out=cat_t[:], in_=cat_ps[:])
+        bias_ps = pi.tile([P, P], BF16, name="bias_ps", tag="it")
+        nc.tensor.transpose(out=bias_ps[:], in_=brow[:], identity=ident_bf[:])
+        bh = const.tile([P, 4], F32, name="bh")
+        nc.vector.tensor_copy(out=bh[:], in_=bias_ps[:, 0:4])
+        b1e = const.tile([P, 4], F32, name="b1e")
+        nc.vector.tensor_scalar_add(out=b1e[:], in0=bias_ps[:, 4:8], scalar1=math.log(SA))
+        b1s = const.tile([P, 4], F32, name="b1s")
+        nc.vector.tensor_scalar_mul(out=b1s[:], in0=bias_ps[:, 4:8], scalar1=SELU_SCALE)
+
+        h_sb = bp.tile([P, 4, TOK], BF16, name="h_sb", tag="bt")
+        for j in range(4):
+            hp = pu.tile([P, TOK], F32, name="hp", tag="u")
+            nc.tensor.matmul(out=hp[:], lhsT=wh[:, j * P:(j + 1) * P], rhs=cat_t[:],
+                             start=True, stop=True)
+            nc.scalar.activation(out=h_sb[:, j, :], in_=hp[:], func=ACT.Relu,
+                                 bias=bh[:, j:j + 1], scale=1.0)
+
+        b2_ps = pi.tile([P, 2 * P], F32, name="b2_ps", tag="it")
+        for s in range(2):
+            nc.tensor.transpose(
+                out=b2_ps[:, s * P:(s + 1) * P],
+                in_=b2rows[:].bitcast(F32).rearrange("p (q s) -> p s q", s=2)[:, s, :],
+                identity=ident_f[:],
+            )
+
+        def regroup(dst, src):
+            nc.vector.tensor_copy(
+                out=dst[:].rearrange("p (c i t) -> p c t i", i=4, t=4),
+                in_=src[:].rearrange("p t (c i) -> p c t i", i=4),
+            )
+
+        w1g = gp.tile([P, 4 * HN], BF16, name="w1g", tag="g2", align_bytes=64)
+        regroup(w1g, raw1)
+        nb2 = const.tile([P, 4 * NBLK], F32, name="nb2")
+        nb2_v = nb2[:].rearrange("p (b s e) -> p b s e", s=2, e=2)
+        for s in range(2):
+            nc.vector.tensor_scalar_mul(
+                out=nb2_v[:, :, s, :],
+                in0=b2_ps[:, s * P:s * P + NBLK].bitcast(BF16).rearrange("p (b e) -> p b e", e=2),
+                scalar1=-1.0,
+            )
+        w1_codes = const.tile([P, HN], U32, name="w1_codes", align_bytes=64)
+        w1_plane = const.tile([P, HN], U8, name="w1_plane", align_bytes=64)
+        nc.vector.quantize_mx(out=w1_codes[:].bitcast(FP8X4), scales=w1_plane[:], in_=w1g[:])
+
+        hg = gp.tile([P, 4 * TOK], BF16, name="hg", tag="g2", align_bytes=64)
+        regroup(hg, h_sb)
+        h_codes = const.tile([P, TOK], U32, name="h_codes", align_bytes=64)
+        h_plane = const.tile([P, TOK], U8, name="h_plane", align_bytes=64)
+        nc.vector.quantize_mx(out=h_codes[:].bitcast(FP8X4), scales=h_plane[:], in_=hg[:])
+
+        prep_copy(0)
+        prep_copy(1)
+        prep_quant(0)
+        prep_quant(1)
+        e_sb = yp.tile([P, 4, TOK], F32, name="e_sb", tag="y")
+        r_sb = bp.tile([P, 4, TOK], F32, name="r_sb", tag="bt")
+        t_sb = bp.tile([P, 4, TOK], BF16, name="t_sb", tag="bt")
+        for m in range(4):
+            tp = pu.tile([P, TOK], F32, name="tp", tag="u")
+            nc.tensor.matmul_mx(
+                out=tp[:],
+                lhsT=w1_codes[:, m * P:(m + 1) * P].bitcast(FP8X4),
+                lhsT_scale=w1_plane[:, m * P:(m + 1) * P],
+                rhs=h_codes[:].bitcast(FP8X4),
+                rhs_scale=h_plane[:],
+                start=True,
+                stop=True,
+            )
+            nc.scalar.activation(out=e_sb[:, m, :], in_=tp[:], func=ACT.Exp,
+                                 bias=b1e[:, m:m + 1], scale=1.0)
+            nc.scalar.activation(out=r_sb[:, m, :], in_=tp[:], func=ACT.Relu,
+                                 bias=b1s[:, m:m + 1], scale=SELU_SCALE)
+            nc.vector.tensor_scalar(out=e_sb[:, m, :], in0=e_sb[:, m, :], scalar1=SA,
+                                    scalar2=-SA, op0=ALU.min, op1=ALU.add)
+            nc.vector.tensor_tensor(out=t_sb[:, m, :], in0=e_sb[:, m, :], in1=r_sb[:, m, :],
+                                    op=ALU.add)
+        tg = gp.tile([P, 4 * TOK], BF16, name="tg", tag="g2", align_bytes=64)
+        regroup(tg, t_sb)
+        prep_copy(2)
+        t_codes = const.tile([P, TOK], U32, name="t_codes", align_bytes=64)
+        t_plane = const.tile([P, TOK], U8, name="t_plane", align_bytes=64)
+        nc.vector.quantize_mx(out=t_codes[:].bitcast(FP8X4), scales=t_plane[:], in_=tg[:])
+        prep_quant(2)
+        for b in range(3, BB):
+            prep_copy(b)
+            prep_quant(b)
+
+        res = const.tile([P, NT, CH // 64], F32, name="res")
+
+        early = 3
+        for n in range(early):
+            mx(n // 4, n % 4)
+        for i in range(NBATCH):
+            first = i * BB
+            for n in range(4 * BB):
+                b = first + n // 4
+                r = n % 4
+                if n >= early:
+                    mx(b, r)
+                sig(b, r)
+                if r == 3 and b + BB < NBLK:
+                    prep_copy(b + BB)
+                    if n // 4 > 0:
+                        prep_quant(b + BB - 1)
+            if first + BB < NBLK:
+                prep_quant(first + 2 * BB - 1)
+            if i == 0:
+                imgt(0)
+            for k in range(BB):
+                g = first + k
+                logs(g)
+                if k == BB - 2 and g + 2 < NBLK:
+                    for n in range(early):
+                        mx(g + 2 + n // 4, n % 4)
+                if g >= 3:
+                    summ(g - 3)
+                uv(g)
+                if g >= 3:
+                    red(g - 3)
+                zed(g)
+                if g + 1 < NBLK:
+                    imgt(g + 1)
+        for g in range(NBLK - 3, NBLK):
+            summ(g)
+            red(g)
+        nc.sync.dma_start(out=out_v, in_=res[:])

@@ -25,10 +25,13 @@ NBATCH = NBLK // BB
 CHUNK = 1024
 NCHUNK = CH // CHUNK
 EPS = 1e-9
-LOG_EPS = math.log(EPS)
+D_MIN = math.log(EPS) - 1e-3
 SELU_ALPHA = 1.6732632423543772848170429916717
 SELU_SCALE = 1.0507009873554804934193349852946
 SA = SELU_SCALE * SELU_ALPHA
+
+LAST = ((0, 1, "g"), (1, 2, "g"), (2, 3, "g"), (3, 4, "g"))
+LAST_MUL = LAST
 
 FLOPS = 2 * TOK * (128 * HN + HN * HN + HN * CH)
 
@@ -45,7 +48,7 @@ def tile_decoder_kernel(tc, digits, styles, images, W_h, b_h, W1, b1, W2, b2, ou
     with ExitStack() as ctx:
         ctx.enter_context(tc.manual_schedule())
         const = ctx.enter_context(tc.tile_pool(name="const", bufs=1))
-        yp = ctx.enter_context(tc.tile_pool(name="yp", bufs=9))
+        yp = ctx.enter_context(tc.tile_pool(name="yp", bufs=8))
         bp = ctx.enter_context(tc.tile_pool(name="bp", bufs=5))
         rawp = ctx.enter_context(tc.tile_pool(name="rawp", bufs=3))
         gp = ctx.enter_context(tc.tile_pool(name="gp", bufs=2))
@@ -65,6 +68,7 @@ def tile_decoder_kernel(tc, digits, styles, images, W_h, b_h, W1, b1, W2, b2, ou
         btile = {}
         itile = {}
         stile = {}
+        done = {}
 
         ident_bf = const.tile([P, P], BF16, name="ident_bf")
         masks.make_identity(nc, ident_bf[:])
@@ -79,6 +83,8 @@ def tile_decoder_kernel(tc, digits, styles, images, W_h, b_h, W1, b1, W2, b2, ou
         one_eps_b = const.tile([P, 1], F32, name="one_eps_b")
         nc.vector.memset(one_eps_b[:], 1.0)
         nc.vector.tensor_scalar_add(out=one_eps_b[:], in0=one_eps_b[:], scalar1=EPS)
+        warm = const.tile([P, 1], F32, name="warm")
+        nc.scalar.activation(out=warm[:], in_=eps_b[:], func=ACT.Relu)
 
         cat = const.tile([P, NT, P], BF16, name="cat")
         nc.sync.dma_start(out=cat[:, :, 0:32], in_=dig_v)
@@ -106,13 +112,15 @@ def tile_decoder_kernel(tc, digits, styles, images, W_h, b_h, W1, b1, W2, b2, ou
         for c in range(3):
             load_img(c)
 
-        def prep_copy(b):
+        def prep_copy(b, on_scalar=False):
             g2 = gp.tile([P, 4 * BLK], BF16, name="g2", tag="g2", align_bytes=64)
             lo = (b % 2) * BLK
-            nc.vector.tensor_copy(
-                out=g2[:].rearrange("p (r q j) -> p r q j", r=4, j=4),
-                in_=raws[b // 2][:, :, lo:lo + BLK].rearrange("p j (q r) -> p r q j", r=4),
-            )
+            dst = g2[:].rearrange("p (r q j) -> p r q j", r=4, j=4)
+            src = raws[b // 2][:, :, lo:lo + BLK].rearrange("p j (q r) -> p r q j", r=4)
+            if on_scalar:
+                nc.scalar.copy(out=dst, in_=src)
+            else:
+                nc.vector.tensor_copy(out=dst, in_=src)
             grouped[b] = g2
             if b % 2 == 1 and b // 2 + 3 < NCHUNK:
                 load_w2(b // 2 + 3)
@@ -145,11 +153,12 @@ def tile_decoder_kernel(tc, digits, styles, images, W_h, b_h, W1, b1, W2, b2, ou
                 bias=nb2[:, 4 * b + r:4 * b + r + 1], scale=-1.0,
             )
 
-        def logs(b):
-            btile[b] = bp.tile([P, 4, TOK], F32, name="bt", tag="bt")
-            nc.scalar.activation(out=btile[b][:], in_=ytile[b][:], func=ACT.Ln,
+        def logs(b, r0=0, r1=4):
+            if r0 == 0:
+                btile[b] = bp.tile([P, 4, TOK], F32, name="bt", tag="bt")
+            nc.scalar.activation(out=btile[b][:, r0:r1, :], in_=ytile[b][:, r0:r1, :], func=ACT.Ln,
                                  bias=eps_b[:, 0:1], scale=1.0)
-            nc.scalar.activation(out=ytile[b][:], in_=ytile[b][:], func=ACT.Ln,
+            nc.scalar.activation(out=ytile[b][:, r0:r1, :], in_=ytile[b][:, r0:r1, :], func=ACT.Ln,
                                  bias=one_eps_b[:, 0:1], scale=-1.0)
 
         def imgt(b):
@@ -167,39 +176,46 @@ def tile_decoder_kernel(tc, digits, styles, images, W_h, b_h, W1, b1, W2, b2, ou
             if b % 2 == 1 and b // 2 + 3 < NCHUNK:
                 load_img(b // 2 + 3)
 
-        def uv(b):
+        def dsub(b, r0=0, r1=4, eng=None):
+            (eng or nc.gpsimd).tensor_tensor(out=ytile[b][:, r0:r1, :], in0=ytile[b][:, r0:r1, :],
+                                             in1=btile[b][:, r0:r1, :], op=ALU.subtract)
+
+        def mul(b, r0=0, r1=4):
             for s in range(2):
-                iv = itile[(b, s)][:].bitcast(BF16).rearrange("p (t e) -> p e t", e=2)
-                a_s = ytile[b][:, 2 * s:2 * s + 2, :]
-                b_s = btile[b][:, 2 * s:2 * s + 2, :]
-                nc.vector.scalar_tensor_tensor(out=a_s, in0=a_s, scalar=LOG_EPS, in1=iv,
-                                               op0=ALU.max, op1=ALU.mult)
-                nc.vector.scalar_tensor_tensor(out=b_s, in0=iv, scalar=1.0, in1=b_s,
-                                               op0=ALU.subtract, op1=ALU.mult)
+                lo = max(r0, 2 * s)
+                hi = min(r1, 2 * s + 2)
+                if lo < hi:
+                    iv = itile[(b, s)][:].bitcast(BF16).rearrange("p (t e) -> p e t", e=2)
+                    d_s = ytile[b][:, lo:hi, :]
+                    nc.vector.scalar_tensor_tensor(out=d_s, in0=d_s, scalar=D_MIN,
+                                                   in1=iv[:, lo - 2 * s:hi - 2 * s, :],
+                                                   op0=ALU.max, op1=ALU.mult)
 
-        def zed(b):
-            nc.gpsimd.tensor_tensor(out=ytile[b][:], in0=btile[b][:], in1=ytile[b][:],
-                                    op=ALU.subtract)
-
-        def summ(b):
-            st = ps.tile([P, TOK], F32, name="st", tag="st")
-            for t in range(NT):
-                for r in range(4):
+        def summ(b, r0=0, r1=8):
+            if b not in stile:
+                if b >= NBLK - BB:
+                    stile[b] = pu.tile([P, TOK], F32, name="st_u", tag="u")
+                else:
+                    stile[b] = ps.tile([P, TOK], F32, name="st", tag="st")
+                done[b] = 0
+            for r in range(r0, r1):
+                src = btile[b] if r < 4 else ytile[b]
+                for t in range(NT):
                     nc.tensor.matmul(
-                        out=st[:, t * P:(t + 1) * P],
-                        lhsT=ytile[b][:, r, t * P:(t + 1) * P],
+                        out=stile[b][:, t * P:(t + 1) * P],
+                        lhsT=src[:, r % 4, t * P:(t + 1) * P],
                         rhs=ident_f[:],
                         is_transpose=True,
-                        start=(r == 0),
-                        stop=(r == 3),
+                        start=(done[b] == 0),
+                        stop=(done[b] == 8 * NT - 1),
                     )
-            stile[b] = st
+                    done[b] = done[b] + 1
 
         def red(b):
             nc.vector.tensor_reduce(
                 out=res[:, :, 8 * b:8 * b + 8],
                 in_=stile[b][:].rearrange("p (t g w) -> p t g w", t=NT, g=8),
-                axis=AX.X, op=ALU.add,
+                axis=AX.X, op=ALU.add, negate=True,
             )
 
         cat_ps = pi.tile([P, TOK], BF16, name="cat_ps", tag="it")
@@ -259,10 +275,9 @@ def tile_decoder_kernel(tc, digits, styles, images, W_h, b_h, W1, b1, W2, b2, ou
         h_plane = const.tile([P, TOK], U8, name="h_plane", align_bytes=64)
         nc.vector.quantize_mx(out=h_codes[:].bitcast(FP8X4), scales=h_plane[:], in_=hg[:])
 
-        prep_copy(0)
+        prep_copy(0, on_scalar=True)
         prep_copy(1)
         prep_quant(0)
-        prep_quant(1)
         e_sb = yp.tile([P, 4, TOK], F32, name="e_sb", tag="y")
         r_sb = bp.tile([P, 4, TOK], F32, name="r_sb", tag="bt")
         t_sb = bp.tile([P, 4, TOK], BF16, name="t_sb", tag="bt")
@@ -287,14 +302,16 @@ def tile_decoder_kernel(tc, digits, styles, images, W_h, b_h, W1, b1, W2, b2, ou
                                     op=ALU.add)
         tg = gp.tile([P, 4 * TOK], BF16, name="tg", tag="g2", align_bytes=64)
         regroup(tg, t_sb)
-        prep_copy(2)
+        nc.scalar.activation(out=warm[:], in_=eps_b[:], func=ACT.Sigmoid)
+        prep_quant(1)
         t_codes = const.tile([P, TOK], U32, name="t_codes", align_bytes=64)
         t_plane = const.tile([P, TOK], U8, name="t_plane", align_bytes=64)
         nc.vector.quantize_mx(out=t_codes[:].bitcast(FP8X4), scales=t_plane[:], in_=tg[:])
-        prep_quant(2)
-        for b in range(3, BB):
+        for b in range(2, BB):
             prep_copy(b)
-            prep_quant(b)
+            if b > 2:
+                prep_quant(b - 1)
+        prep_quant(BB - 1)
 
         res = const.tile([P, NT, CH // 64], F32, name="res")
 
@@ -315,23 +332,49 @@ def tile_decoder_kernel(tc, digits, styles, images, W_h, b_h, W1, b1, W2, b2, ou
                         prep_quant(b + BB - 1)
             if first + BB < NBLK:
                 prep_quant(first + 2 * BB - 1)
-            if i == 0:
-                imgt(0)
+            imgt(first)
+            if i > 0:
+                for late in (first - 2, first - 1):
+                    summ(late)
+                    red(late)
+            last_batch = first + BB >= NBLK
             for k in range(BB):
                 g = first + k
-                logs(g)
-                if k == BB - 2 and g + 2 < NBLK:
-                    for n in range(early):
-                        mx(g + 2 + n // 4, n % 4)
-                if g >= 3:
-                    summ(g - 3)
-                uv(g)
-                if g >= 3:
-                    red(g - 3)
-                zed(g)
-                if g + 1 < NBLK:
+                if not last_batch:
+                    logs(g)
+                    dsub(g)
+                    if k == BB - 3:
+                        for n in range(early):
+                            mx(first + BB + n // 4, n % 4)
+                    if k < BB - 1:
+                        imgt(g + 1)
+                    mul(g)
+                    if 0 < k < BB - 1:
+                        red(g - 1)
+                    if k < BB - 2:
+                        summ(g)
+                elif k < BB - 1:
+                    logs(g, 0, 2)
+                    dsub(g, 0, 2)
+                    logs(g, 2, 4)
+                    dsub(g, 2, 4, nc.vector)
                     imgt(g + 1)
-        for g in range(NBLK - 3, NBLK):
-            summ(g)
-            red(g)
+                    summ(g, 0, 4)
+                    mul(g, 2, 4)
+                    summ(g, 6, 8)
+                    mul(g, 0, 2)
+                    summ(g, 4, 6)
+                    if k > 0:
+                        red(g - 1)
+                else:
+                    summ(g, 0, 0)
+                    for (r0, r1, where) in LAST:
+                        logs(g, r0, r1)
+                        dsub(g, r0, r1, nc.vector if where == "v" else nc.gpsimd)
+                        summ(g, r0, r1)
+                    red(g - 1)
+                    for (r0, r1, where) in LAST_MUL:
+                        mul(g, r0, r1)
+                        summ(g, 4 + r0, 4 + r1)
+                    red(g)
         nc.sync.dma_start(out=out_v, in_=res[:])

@@ -30,8 +30,12 @@ SELU_ALPHA = 1.6732632423543772848170429916717
 SELU_SCALE = 1.0507009873554804934193349852946
 SA = SELU_SCALE * SELU_ALPHA
 
-LAST = ((0, 1, "g"), (1, 2, "g"), (2, 3, "g"), (3, 4, "g"))
-LAST_MUL = LAST
+UV_HALVES = (0,)
+UV_LAST = ()
+NLAST = 2
+SL = 0
+DEFER = 2
+SBANKS = 2
 
 FLOPS = 2 * TOK * (128 * HN + HN * HN + HN * CH)
 
@@ -52,11 +56,11 @@ def tile_decoder_kernel(tc, digits, styles, images, W_h, b_h, W1, b1, W2, b2, ou
         bp = ctx.enter_context(tc.tile_pool(name="bp", bufs=5))
         rawp = ctx.enter_context(tc.tile_pool(name="rawp", bufs=3))
         gp = ctx.enter_context(tc.tile_pool(name="gp", bufs=2))
-        cp = ctx.enter_context(tc.tile_pool(name="cp", bufs=2 * BB))
+        cp = ctx.enter_context(tc.tile_pool(name="cp", bufs=BB + 2))
         imp = ctx.enter_context(tc.tile_pool(name="imp", bufs=3))
         pu = ctx.enter_context(tc.psum_pool(name="pu", bufs=3))
-        pi = ctx.enter_context(tc.psum_pool(name="pi", bufs=4))
-        ps = ctx.enter_context(tc.psum_pool(name="ps", bufs=1))
+        pi = ctx.enter_context(tc.psum_pool(name="pi", bufs=3))
+        ps = ctx.enter_context(tc.psum_pool(name="ps", bufs=2))
 
         raws = {}
         imgs = {}
@@ -176,9 +180,15 @@ def tile_decoder_kernel(tc, digits, styles, images, W_h, b_h, W1, b1, W2, b2, ou
             if b % 2 == 1 and b // 2 + 3 < NCHUNK:
                 load_img(b // 2 + 3)
 
+        def is_uv(b, r):
+            return r // 2 in (UV_LAST if b >= NBLK - NLAST else UV_HALVES)
+
         def dsub(b, r0=0, r1=4, eng=None):
-            (eng or nc.gpsimd).tensor_tensor(out=ytile[b][:, r0:r1, :], in0=ytile[b][:, r0:r1, :],
-                                             in1=btile[b][:, r0:r1, :], op=ALU.subtract)
+            for r in range(r0, r1, 2 if r1 - r0 > 1 else 1):
+                hi = min(r1, r + 2)
+                if not is_uv(b, r):
+                    (eng or nc.gpsimd).tensor_tensor(out=ytile[b][:, r:hi, :], in0=ytile[b][:, r:hi, :],
+                                                     in1=btile[b][:, r:hi, :], op=ALU.subtract)
 
         def mul(b, r0=0, r1=4):
             for s in range(2):
@@ -186,28 +196,42 @@ def tile_decoder_kernel(tc, digits, styles, images, W_h, b_h, W1, b1, W2, b2, ou
                 hi = min(r1, 2 * s + 2)
                 if lo < hi:
                     iv = itile[(b, s)][:].bitcast(BF16).rearrange("p (t e) -> p e t", e=2)
-                    d_s = ytile[b][:, lo:hi, :]
-                    nc.vector.scalar_tensor_tensor(out=d_s, in0=d_s, scalar=D_MIN,
-                                                   in1=iv[:, lo - 2 * s:hi - 2 * s, :],
+                    iv = iv[:, lo - 2 * s:hi - 2 * s, :]
+                    a_s = ytile[b][:, lo:hi, :]
+                    b_s = btile[b][:, lo:hi, :]
+                    nc.vector.scalar_tensor_tensor(out=a_s, in0=a_s, scalar=D_MIN, in1=iv,
                                                    op0=ALU.max, op1=ALU.mult)
+                    if is_uv(b, lo):
+                        nc.vector.scalar_tensor_tensor(out=b_s, in0=iv, scalar=1.0, in1=b_s,
+                                                       op0=ALU.subtract, op1=ALU.mult)
 
-        def summ(b, r0=0, r1=8):
+        def zsub(b, r0=0, r1=4, eng=None):
+            for r in range(r0, r1, 2 if r1 - r0 > 1 else 1):
+                hi = min(r1, r + 2)
+                if is_uv(b, r):
+                    (eng or nc.gpsimd).tensor_tensor(out=ytile[b][:, r:hi, :], in0=ytile[b][:, r:hi, :],
+                                                     in1=btile[b][:, r:hi, :], op=ALU.subtract)
+
+        def arrays(b):
+            return ([("b", r) for r in range(4) if not is_uv(b, r)]
+                    + [("y", r) for r in range(4) if not is_uv(b, r)]
+                    + [("y", r) for r in range(4) if is_uv(b, r)])
+
+        def summ(b, picks=None):
             if b not in stile:
-                if b >= NBLK - BB:
-                    stile[b] = pu.tile([P, TOK], F32, name="st_u", tag="u")
-                else:
-                    stile[b] = ps.tile([P, TOK], F32, name="st", tag="st")
+                stile[b] = ps.tile([P, TOK], F32, name="st", tag="st")
                 done[b] = 0
-            for r in range(r0, r1):
-                src = btile[b] if r < 4 else ytile[b]
+            total = len(arrays(b)) * NT
+            for (which, r) in (arrays(b) if picks is None else picks):
+                src = btile[b] if which == "b" else ytile[b]
                 for t in range(NT):
                     nc.tensor.matmul(
                         out=stile[b][:, t * P:(t + 1) * P],
-                        lhsT=src[:, r % 4, t * P:(t + 1) * P],
+                        lhsT=src[:, r, t * P:(t + 1) * P],
                         rhs=ident_f[:],
-                        is_transpose=True,
+                        is_transpose=(done[b] % 6 != 6 - 1),
                         start=(done[b] == 0),
-                        stop=(done[b] == 8 * NT - 1),
+                        stop=(done[b] == total - 1),
                     )
                     done[b] = done[b] + 1
 
@@ -316,10 +340,20 @@ def tile_decoder_kernel(tc, digits, styles, images, W_h, b_h, W1, b1, W2, b2, ou
         res = const.tile([P, NT, CH // 64], F32, name="res")
 
         early = 3
+        pending = []
+
+        def sum_red(h, picks=None, new=True):
+            if new:
+                if len(pending) >= SBANKS:
+                    red(pending.pop(0))
+                pending.append(h)
+            summ(h, picks)
+
         for n in range(early):
             mx(n // 4, n % 4)
         for i in range(NBATCH):
             first = i * BB
+            last_batch = first + BB >= NBLK
             for n in range(4 * BB):
                 b = first + n // 4
                 r = n % 4
@@ -330,51 +364,41 @@ def tile_decoder_kernel(tc, digits, styles, images, W_h, b_h, W1, b1, W2, b2, ou
                     prep_copy(b + BB)
                     if n // 4 > 0:
                         prep_quant(b + BB - 1)
-            if first + BB < NBLK:
+            if not last_batch:
                 prep_quant(first + 2 * BB - 1)
             imgt(first)
             if i > 0:
-                for late in (first - 2, first - 1):
-                    summ(late)
-                    red(late)
-            last_batch = first + BB >= NBLK
+                for late in range(first - DEFER, first):
+                    sum_red(late)
             for k in range(BB):
                 g = first + k
-                if not last_batch:
-                    logs(g)
-                    dsub(g)
-                    if k == BB - 3:
-                        for n in range(early):
-                            mx(first + BB + n // 4, n % 4)
-                    if k < BB - 1:
-                        imgt(g + 1)
-                    mul(g)
-                    if 0 < k < BB - 1:
-                        red(g - 1)
-                    if k < BB - 2:
-                        summ(g)
-                elif k < BB - 1:
-                    logs(g, 0, 2)
-                    dsub(g, 0, 2)
-                    logs(g, 2, 4)
-                    dsub(g, 2, 4, nc.vector)
+                if g >= NBLK - NLAST:
+                    continue
+                logs(g)
+                dsub(g)
+                if k == BB - 3 and not last_batch:
+                    for n in range(early):
+                        mx(first + BB + n // 4, n % 4)
+                if k < BB - 1:
                     imgt(g + 1)
-                    summ(g, 0, 4)
-                    mul(g, 2, 4)
-                    summ(g, 6, 8)
-                    mul(g, 0, 2)
-                    summ(g, 4, 6)
-                    if k > 0:
-                        red(g - 1)
-                else:
-                    summ(g, 0, 0)
-                    for (r0, r1, where) in LAST:
-                        logs(g, r0, r1)
-                        dsub(g, r0, r1, nc.vector if where == "v" else nc.gpsimd)
-                        summ(g, r0, r1)
-                    red(g - 1)
-                    for (r0, r1, where) in LAST_MUL:
-                        mul(g, r0, r1)
-                        summ(g, 4 + r0, 4 + r1)
-                    red(g)
+                mul(g)
+                zsub(g)
+                h = g - SL
+                if h >= first and (last_batch or h < first + BB - DEFER):
+                    sum_red(h)
+        for h in range(NBLK - NLAST - SL, NBLK - NLAST):
+            sum_red(h)
+        for g in range(NBLK - NLAST, NBLK):
+            pieces = ((0, 1), (1, 2), (2, 3), (3, 4)) if g == NBLK - 1 else ((0, 2), (2, 4))
+            for j, (r0, r1) in enumerate(pieces):
+                logs(g, r0, r1)
+                dsub(g, r0, r1, nc.vector if (j % 2 == 1 and g < NBLK - 1) else nc.gpsimd)
+                sum_red(g, [("b", r) for r in range(r0, r1)], new=(j == 0))
+            if g + 1 < NBLK:
+                imgt(g + 1)
+            for (r0, r1) in (pieces if g == NBLK - 1 else pieces[::-1]):
+                mul(g, r0, r1)
+                sum_red(g, [("y", r) for r in range(r0, r1)], new=False)
+        while pending:
+            red(pending.pop(0))
         nc.sync.dma_start(out=out_v, in_=res[:])

@@ -20,7 +20,7 @@ HN = 512
 CH = 12288
 BLK = 512
 NBLK = CH // BLK
-BB = 6
+BB = 8
 NBATCH = NBLK // BB
 CHUNK = 1024
 NCHUNK = CH // CHUNK
@@ -30,9 +30,9 @@ SELU_ALPHA = 1.6732632423543772848170429916717
 SELU_SCALE = 1.0507009873554804934193349852946
 SA = SELU_SCALE * SELU_ALPHA
 
-UV_HALVES = (0,)
+UV_HALVES = ()
 UV_LAST = ()
-NLAST = 2
+NLAST = 1
 SL = 0
 DEFER = 2
 SBANKS = 2
@@ -52,7 +52,7 @@ def tile_decoder_kernel(tc, digits, styles, images, W_h, b_h, W1, b1, W2, b2, ou
     with ExitStack() as ctx:
         ctx.enter_context(tc.manual_schedule())
         const = ctx.enter_context(tc.tile_pool(name="const", bufs=1))
-        yp = ctx.enter_context(tc.tile_pool(name="yp", bufs=8))
+        yp = ctx.enter_context(tc.tile_pool(name="yp", bufs=10))
         bp = ctx.enter_context(tc.tile_pool(name="bp", bufs=5))
         rawp = ctx.enter_context(tc.tile_pool(name="rawp", bufs=3))
         gp = ctx.enter_context(tc.tile_pool(name="gp", bufs=2))
@@ -214,7 +214,7 @@ def tile_decoder_kernel(tc, digits, styles, images, W_h, b_h, W1, b1, W2, b2, ou
 
         def arrays(b):
             return ([("b", r) for r in range(4) if not is_uv(b, r)]
-                    + [("y", r) for r in range(4) if not is_uv(b, r)]
+                    + [("y", r) for r in (2, 3, 0, 1) if not is_uv(b, r)]
                     + [("y", r) for r in range(4) if is_uv(b, r)])
 
         def summ(b, picks=None):
@@ -375,14 +375,15 @@ def tile_decoder_kernel(tc, digits, styles, images, W_h, b_h, W1, b1, W2, b2, ou
                 if g >= NBLK - NLAST:
                     continue
                 logs(g)
-                dsub(g)
+                dsub(g, 0, 2)
+                dsub(g, 2, 4, nc.vector)
                 if k == BB - 3 and not last_batch:
                     for n in range(early):
                         mx(first + BB + n // 4, n % 4)
                 if k < BB - 1:
                     imgt(g + 1)
-                mul(g)
-                zsub(g)
+                mul(g, 2, 4)
+                mul(g, 0, 2)
                 h = g - SL
                 if h >= first and (last_batch or h < first + BB - DEFER):
                     sum_red(h)
@@ -392,7 +393,7 @@ def tile_decoder_kernel(tc, digits, styles, images, W_h, b_h, W1, b1, W2, b2, ou
             pieces = ((0, 1), (1, 2), (2, 3), (3, 4)) if g == NBLK - 1 else ((0, 2), (2, 4))
             for j, (r0, r1) in enumerate(pieces):
                 logs(g, r0, r1)
-                dsub(g, r0, r1, nc.vector if (j % 2 == 1 and g < NBLK - 1) else nc.gpsimd)
+                dsub(g, r0, r1, nc.vector if j % 2 == 1 else nc.gpsimd)
                 sum_red(g, [("b", r) for r in range(r0, r1)], new=(j == 0))
             if g + 1 < NBLK:
                 imgt(g + 1)

@@ -20,7 +20,7 @@ HN = 512
 CH = 12288
 BLK = 512
 NBLK = CH // BLK
-BB = 8
+BB = 6
 NBATCH = NBLK // BB
 CHUNK = 1024
 NCHUNK = CH // CHUNK
@@ -30,9 +30,9 @@ SELU_ALPHA = 1.6732632423543772848170429916717
 SELU_SCALE = 1.0507009873554804934193349852946
 SA = SELU_SCALE * SELU_ALPHA
 
-UV_HALVES = ()
+UV_HALVES = (0,)
 UV_LAST = ()
-NLAST = 1
+NLAST = 2
 SL = 0
 DEFER = 2
 SBANKS = 2
@@ -52,10 +52,10 @@ def tile_decoder_kernel(tc, digits, styles, images, W_h, b_h, W1, b1, W2, b2, ou
     with ExitStack() as ctx:
         ctx.enter_context(tc.manual_schedule())
         const = ctx.enter_context(tc.tile_pool(name="const", bufs=1))
-        yp = ctx.enter_context(tc.tile_pool(name="yp", bufs=10))
+        yp = ctx.enter_context(tc.tile_pool(name="yp", bufs=8))
         bp = ctx.enter_context(tc.tile_pool(name="bp", bufs=5))
         rawp = ctx.enter_context(tc.tile_pool(name="rawp", bufs=3))
-        gp = ctx.enter_context(tc.tile_pool(name="gp", bufs=2))
+        gp = ctx.enter_context(tc.tile_pool(name="gp", bufs=3))
         cp = ctx.enter_context(tc.tile_pool(name="cp", bufs=BB + 2))
         imp = ctx.enter_context(tc.tile_pool(name="imp", bufs=3))
         pu = ctx.enter_context(tc.psum_pool(name="pu", bufs=3))
@@ -119,10 +119,11 @@ def tile_decoder_kernel(tc, digits, styles, images, W_h, b_h, W1, b1, W2, b2, ou
         def prep_copy(b, on_scalar=False):
             g2 = gp.tile([P, 4 * BLK], BF16, name="g2", tag="g2", align_bytes=64)
             lo = (b % 2) * BLK
-            dst = g2[:].rearrange("p (r q j) -> p r q j", r=4, j=4)
-            src = raws[b // 2][:, :, lo:lo + BLK].rearrange("p j (q r) -> p r q j", r=4)
+            dst = g2[:].rearrange("p (s e q j) -> p s q j e", s=2, e=2, j=4)
+            src = raws[b // 2][:, :, lo:lo + BLK].rearrange("p j (q s e) -> p s q j e", s=2, e=2)
             if on_scalar:
-                nc.scalar.copy(out=dst, in_=src)
+                for s in range(2):
+                    nc.scalar.copy(out=dst[:, s], in_=src[:, s])
             else:
                 nc.vector.tensor_copy(out=dst, in_=src)
             grouped[b] = g2
@@ -214,7 +215,7 @@ def tile_decoder_kernel(tc, digits, styles, images, W_h, b_h, W1, b1, W2, b2, ou
 
         def arrays(b):
             return ([("b", r) for r in range(4) if not is_uv(b, r)]
-                    + [("y", r) for r in (2, 3, 0, 1) if not is_uv(b, r)]
+                    + [("y", r) for r in range(4) if not is_uv(b, r)]
                     + [("y", r) for r in range(4) if is_uv(b, r)])
 
         def summ(b, picks=None):
@@ -229,7 +230,7 @@ def tile_decoder_kernel(tc, digits, styles, images, W_h, b_h, W1, b1, W2, b2, ou
                         out=stile[b][:, t * P:(t + 1) * P],
                         lhsT=src[:, r, t * P:(t + 1) * P],
                         rhs=ident_f[:],
-                        is_transpose=(done[b] % 6 != 6 - 1),
+                        is_transpose=True,
                         start=(done[b] == 0),
                         stop=(done[b] == total - 1),
                     )
@@ -328,13 +329,13 @@ def tile_decoder_kernel(tc, digits, styles, images, W_h, b_h, W1, b1, W2, b2, ou
         regroup(tg, t_sb)
         nc.scalar.activation(out=warm[:], in_=eps_b[:], func=ACT.Sigmoid)
         prep_quant(1)
+        prep_copy(2, on_scalar=True)
         t_codes = const.tile([P, TOK], U32, name="t_codes", align_bytes=64)
         t_plane = const.tile([P, TOK], U8, name="t_plane", align_bytes=64)
         nc.vector.quantize_mx(out=t_codes[:].bitcast(FP8X4), scales=t_plane[:], in_=tg[:])
-        for b in range(2, BB):
+        for b in range(3, BB):
             prep_copy(b)
-            if b > 2:
-                prep_quant(b - 1)
+            prep_quant(b - 1)
         prep_quant(BB - 1)
 
         res = const.tile([P, NT, CH // 64], F32, name="res")
@@ -375,15 +376,14 @@ def tile_decoder_kernel(tc, digits, styles, images, W_h, b_h, W1, b1, W2, b2, ou
                 if g >= NBLK - NLAST:
                     continue
                 logs(g)
-                dsub(g, 0, 2)
-                dsub(g, 2, 4, nc.vector)
+                dsub(g)
                 if k == BB - 3 and not last_batch:
                     for n in range(early):
                         mx(first + BB + n // 4, n % 4)
                 if k < BB - 1:
                     imgt(g + 1)
-                mul(g, 2, 4)
-                mul(g, 0, 2)
+                mul(g)
+                zsub(g)
                 h = g - SL
                 if h >= first and (last_batch or h < first + BB - DEFER):
                     sum_red(h)

@@ -20,7 +20,7 @@ HN = 512
 CH = 12288
 BLK = 512
 NBLK = CH // BLK
-BB = 6
+BB = 8
 NBATCH = NBLK // BB
 CHUNK = 1024
 NCHUNK = CH // CHUNK
@@ -30,9 +30,9 @@ SELU_ALPHA = 1.6732632423543772848170429916717
 SELU_SCALE = 1.0507009873554804934193349852946
 SA = SELU_SCALE * SELU_ALPHA
 
-UV_HALVES = (0,)
-UV_LAST = ()
-NLAST = 2
+UV_TILES = (0, 1)
+UV_LAST = (0, 1, 2, 3)
+NLAST = 1
 SL = 0
 DEFER = 2
 SBANKS = 2
@@ -52,7 +52,7 @@ def tile_decoder_kernel(tc, digits, styles, images, W_h, b_h, W1, b1, W2, b2, ou
     with ExitStack() as ctx:
         ctx.enter_context(tc.manual_schedule())
         const = ctx.enter_context(tc.tile_pool(name="const", bufs=1))
-        yp = ctx.enter_context(tc.tile_pool(name="yp", bufs=8))
+        yp = ctx.enter_context(tc.tile_pool(name="yp", bufs=10))
         bp = ctx.enter_context(tc.tile_pool(name="bp", bufs=5))
         rawp = ctx.enter_context(tc.tile_pool(name="rawp", bufs=3))
         gp = ctx.enter_context(tc.tile_pool(name="gp", bufs=3))
@@ -182,36 +182,41 @@ def tile_decoder_kernel(tc, digits, styles, images, W_h, b_h, W1, b1, W2, b2, ou
                 load_img(b // 2 + 3)
 
         def is_uv(b, r):
-            return r // 2 in (UV_LAST if b >= NBLK - NLAST else UV_HALVES)
+            return r in (UV_LAST if b >= NBLK - NLAST else UV_TILES)
+
+        def runs(b, r0, r1):
+            found = []
+            for r in range(r0, r1):
+                if found and found[-1][1] == r and r % 2 == 1 and is_uv(b, r) == found[-1][2]:
+                    found[-1] = (found[-1][0], r + 1, found[-1][2])
+                else:
+                    found.append((r, r + 1, is_uv(b, r)))
+            return found
 
         def dsub(b, r0=0, r1=4, eng=None):
-            for r in range(r0, r1, 2 if r1 - r0 > 1 else 1):
-                hi = min(r1, r + 2)
-                if not is_uv(b, r):
-                    (eng or nc.gpsimd).tensor_tensor(out=ytile[b][:, r:hi, :], in0=ytile[b][:, r:hi, :],
-                                                     in1=btile[b][:, r:hi, :], op=ALU.subtract)
+            for (lo, hi, uv) in runs(b, r0, r1):
+                if not uv:
+                    (eng or nc.gpsimd).tensor_tensor(out=ytile[b][:, lo:hi, :], in0=ytile[b][:, lo:hi, :],
+                                                     in1=btile[b][:, lo:hi, :], op=ALU.subtract)
 
         def mul(b, r0=0, r1=4):
-            for s in range(2):
-                lo = max(r0, 2 * s)
-                hi = min(r1, 2 * s + 2)
-                if lo < hi:
-                    iv = itile[(b, s)][:].bitcast(BF16).rearrange("p (t e) -> p e t", e=2)
-                    iv = iv[:, lo - 2 * s:hi - 2 * s, :]
-                    a_s = ytile[b][:, lo:hi, :]
-                    b_s = btile[b][:, lo:hi, :]
-                    nc.vector.scalar_tensor_tensor(out=a_s, in0=a_s, scalar=D_MIN, in1=iv,
-                                                   op0=ALU.max, op1=ALU.mult)
-                    if is_uv(b, lo):
-                        nc.vector.scalar_tensor_tensor(out=b_s, in0=iv, scalar=1.0, in1=b_s,
-                                                       op0=ALU.subtract, op1=ALU.mult)
+            for (lo, hi, uv) in runs(b, r0, r1):
+                s = lo // 2
+                iv = itile[(b, s)][:].bitcast(BF16).rearrange("p (t e) -> p e t", e=2)
+                iv = iv[:, lo - 2 * s:hi - 2 * s, :]
+                a_s = ytile[b][:, lo:hi, :]
+                b_s = btile[b][:, lo:hi, :]
+                nc.vector.scalar_tensor_tensor(out=a_s, in0=a_s, scalar=D_MIN, in1=iv,
+                                               op0=ALU.max, op1=ALU.mult)
+                if uv:
+                    nc.vector.scalar_tensor_tensor(out=b_s, in0=iv, scalar=1.0, in1=b_s,
+                                                   op0=ALU.subtract, op1=ALU.mult)
 
         def zsub(b, r0=0, r1=4, eng=None):
-            for r in range(r0, r1, 2 if r1 - r0 > 1 else 1):
-                hi = min(r1, r + 2)
-                if is_uv(b, r):
-                    (eng or nc.gpsimd).tensor_tensor(out=ytile[b][:, r:hi, :], in0=ytile[b][:, r:hi, :],
-                                                     in1=btile[b][:, r:hi, :], op=ALU.subtract)
+            for (lo, hi, uv) in runs(b, r0, r1):
+                if uv:
+                    (eng or nc.gpsimd).tensor_tensor(out=ytile[b][:, lo:hi, :], in0=ytile[b][:, lo:hi, :],
+                                                     in1=btile[b][:, lo:hi, :], op=ALU.subtract)
 
         def arrays(b):
             return ([("b", r) for r in range(4) if not is_uv(b, r)]
@@ -387,19 +392,13 @@ def tile_decoder_kernel(tc, digits, styles, images, W_h, b_h, W1, b1, W2, b2, ou
                 h = g - SL
                 if h >= first and (last_batch or h < first + BB - DEFER):
                     sum_red(h)
-        for h in range(NBLK - NLAST - SL, NBLK - NLAST):
-            sum_red(h)
-        for g in range(NBLK - NLAST, NBLK):
-            pieces = ((0, 1), (1, 2), (2, 3), (3, 4)) if g == NBLK - 1 else ((0, 2), (2, 4))
-            for j, (r0, r1) in enumerate(pieces):
-                logs(g, r0, r1)
-                dsub(g, r0, r1, nc.vector if j % 2 == 1 else nc.gpsimd)
-                sum_red(g, [("b", r) for r in range(r0, r1)], new=(j == 0))
-            if g + 1 < NBLK:
-                imgt(g + 1)
-            for (r0, r1) in (pieces if g == NBLK - 1 else pieces[::-1]):
-                mul(g, r0, r1)
-                sum_red(g, [("y", r) for r in range(r0, r1)], new=False)
+        nc.sync.dma_start(out=out_v[:, :, 0:8 * (NBLK - BB)], in_=res[:, :, 0:8 * (NBLK - BB)])
+        g = NBLK - 1
+        for r in range(4):
+            logs(g, r, r + 1)
+            mul(g, r, r + 1)
+            zsub(g, r, r + 1, nc.vector if r == 3 else nc.gpsimd)
+            sum_red(g, [("y", r)], new=(r == 0))
         while pending:
             red(pending.pop(0))
-        nc.sync.dma_start(out=out_v, in_=res[:])
+        nc.sync.dma_start(out=out_v[:, :, 8 * (NBLK - BB):], in_=res[:, :, 8 * (NBLK - BB):])

@@ -169,7 +169,10 @@ def tile_decoder_kernel(tc, digits, styles, images, W_h, b_h, W1, b1, W2, b2, ou
         def imgt(b):
             lo = (b % 2) * BLK
             for s in range(2):
-                it = pi.tile([P, TOK], F32, name="it", tag="it")
+                if b >= NBLK - BB and s == 1:
+                    it = pu.tile([P, TOK], F32, name="it_u", tag="u")
+                else:
+                    it = pi.tile([P, TOK], F32, name="it", tag="it")
                 for t in range(NT):
                     words = imgs[b // 2][:, t, lo:lo + BLK].bitcast(F32)
                     nc.tensor.transpose(
@@ -225,7 +228,10 @@ def tile_decoder_kernel(tc, digits, styles, images, W_h, b_h, W1, b1, W2, b2, ou
 
         def summ(b, picks=None):
             if b not in stile:
-                stile[b] = ps.tile([P, TOK], F32, name="st", tag="st")
+                if b == NBLK - 1:
+                    stile[b] = pu.tile([P, TOK], F32, name="st_last", tag="u")
+                else:
+                    stile[b] = ps.tile([P, TOK], F32, name="st", tag="st")
                 done[b] = 0
             total = len(arrays(b)) * NT
             for (which, r) in (arrays(b) if picks is None else picks):
@@ -373,6 +379,9 @@ def tile_decoder_kernel(tc, digits, styles, images, W_h, b_h, W1, b1, W2, b2, ou
             if not last_batch:
                 prep_quant(first + 2 * BB - 1)
             imgt(first)
+            if last_batch:
+                imgt(first + 1)
+                imgt(first + 2)
             if i > 0:
                 for late in range(first - DEFER, first):
                     sum_red(late)
@@ -385,7 +394,10 @@ def tile_decoder_kernel(tc, digits, styles, images, W_h, b_h, W1, b1, W2, b2, ou
                 if k == BB - 3 and not last_batch:
                     for n in range(early):
                         mx(first + BB + n // 4, n % 4)
-                if k < BB - 1:
+                if last_batch:
+                    if k < BB - 3:
+                        imgt(g + 3)
+                elif k < BB - 1:
                     imgt(g + 1)
                 mul(g)
                 zsub(g)
@@ -398,7 +410,8 @@ def tile_decoder_kernel(tc, digits, styles, images, W_h, b_h, W1, b1, W2, b2, ou
             logs(g, r, r + 1)
             mul(g, r, r + 1)
             zsub(g, r, r + 1, nc.vector if r == 3 else nc.gpsimd)
-            sum_red(g, [("y", r)], new=(r == 0))
+            summ(g, [("y", r)])
+        pending.append(g)
         while pending:
             red(pending.pop(0))
         nc.sync.dma_start(out=out_v[:, :, 8 * (NBLK - BB):], in_=res[:, :, 8 * (NBLK - BB):])

@@ -19,21 +19,26 @@ NT = 4
 HN = 512
 CH = 12288
 BLK = 512
+HALF = TOK // 2
 NBLK = CH // BLK
-BB = 8
+BB = 12
 NBATCH = NBLK // BB
-CHUNK = 1024
-NCHUNK = CH // CHUNK
+NRAW = 4
+NIMG = 4
+NCODE = 8
+NIDLE = 4
+AHEAD = 6
 EPS = 1e-9
 D_MIN = math.log(EPS) - 1e-3
 SELU_ALPHA = 1.6732632423543772848170429916717
 SELU_SCALE = 1.0507009873554804934193349852946
 SA = SELU_SCALE * SELU_ALPHA
 
-UV_TILES = (0, 1)
-UV_LAST = (0, 1, 2, 3)
-NLAST = 1
-SL = 0
+PRODS = (0,)
+DIFFS = ((2, 4), (1, 2))
+LATE_PRODS = (0, 1)
+LATE_DIFFS = ((2, 3), (3, 4))
+END_PRODS = (1, 2, 3)
 DEFER = 2
 SBANKS = 2
 
@@ -52,12 +57,13 @@ def tile_decoder_kernel(tc, digits, styles, images, W_h, b_h, W1, b1, W2, b2, ou
     with ExitStack() as ctx:
         ctx.enter_context(tc.manual_schedule())
         const = ctx.enter_context(tc.tile_pool(name="const", bufs=1))
-        yp = ctx.enter_context(tc.tile_pool(name="yp", bufs=10))
+        yp = ctx.enter_context(tc.tile_pool(name="yp", bufs=BB + DEFER))
         bp = ctx.enter_context(tc.tile_pool(name="bp", bufs=5))
-        rawp = ctx.enter_context(tc.tile_pool(name="rawp", bufs=3))
+        rawp = ctx.enter_context(tc.tile_pool(name="rawp", bufs=NRAW))
         gp = ctx.enter_context(tc.tile_pool(name="gp", bufs=3))
-        cp = ctx.enter_context(tc.tile_pool(name="cp", bufs=BB + 2))
-        imp = ctx.enter_context(tc.tile_pool(name="imp", bufs=3))
+        cp = ctx.enter_context(tc.tile_pool(name="cp", bufs=NCODE))
+        npool = ctx.enter_context(tc.tile_pool(name="npool", bufs=3))
+        imp = ctx.enter_context(tc.tile_pool(name="imp", bufs=NIMG))
         pu = ctx.enter_context(tc.psum_pool(name="pu", bufs=3))
         pi = ctx.enter_context(tc.psum_pool(name="pi", bufs=3))
         ps = ctx.enter_context(tc.psum_pool(name="ps", bufs=2))
@@ -71,8 +77,8 @@ def tile_decoder_kernel(tc, digits, styles, images, W_h, b_h, W1, b1, W2, b2, ou
         ytile = {}
         btile = {}
         itile = {}
+        ntile = {}
         stile = {}
-        done = {}
 
         ident_bf = const.tile([P, P], BF16, name="ident_bf")
         masks.make_identity(nc, ident_bf[:])
@@ -97,38 +103,37 @@ def tile_decoder_kernel(tc, digits, styles, images, W_h, b_h, W1, b1, W2, b2, ou
         nc.sync.dma_start(out=wh[:], in_=W_h)
         nc.sync.dma_start(out=brow[0:4, :], in_=b_h.rearrange("(j p) -> j p", p=P))
         nc.sync.dma_start(out=brow[4:8, :], in_=b1.rearrange("(j p) -> j p", p=P))
-        raw1 = const.tile([P, 4, HN], BF16, name="raw1")
+        raw1 = rawp.tile([P, 4, HN], BF16, name="raw1", tag="raw")
         nc.sync.dma_start(out=raw1[:], in_=w1_v)
         nc.sync.dma_start(out=b2rows[0:NBLK, :], in_=b2.rearrange("(b x) -> b x", x=BLK))
 
-        def load_w2(c):
-            raw = rawp.tile([P, 4, CHUNK], BF16, name="raw", tag="raw")
-            nc.sync.dma_start(out=raw[:], in_=w2_v[:, :, c * CHUNK:(c + 1) * CHUNK])
-            raws[c] = raw
+        def load_w2(b):
+            raw = rawp.tile([P, 4, BLK], BF16, name="raw", tag="raw")
+            nc.sync.dma_start(out=raw[:], in_=w2_v[:, :, b * BLK:(b + 1) * BLK])
+            raws[b] = raw
 
-        def load_img(c):
-            im = imp.tile([P, NT, CHUNK], BF16, name="im", tag="im")
-            nc.sync.dma_start(out=im[:], in_=img_v[:, :, c * CHUNK:(c + 1) * CHUNK])
-            imgs[c] = im
+        def load_img(b):
+            im = imp.tile([P, NT, BLK], BF16, name="im", tag="im")
+            nc.sync.dma_start(out=im[:], in_=img_v[:, :, b * BLK:(b + 1) * BLK])
+            imgs[b] = im
 
-        for c in range(3):
-            load_w2(c)
-        for c in range(3):
-            load_img(c)
+        for b in range(NRAW - 1):
+            load_w2(b)
+        for b in range(NIMG):
+            load_img(b)
 
         def prep_copy(b, on_scalar=False):
             g2 = gp.tile([P, 4 * BLK], BF16, name="g2", tag="g2", align_bytes=64)
-            lo = (b % 2) * BLK
             dst = g2[:].rearrange("p (s e q j) -> p s q j e", s=2, e=2, j=4)
-            src = raws[b // 2][:, :, lo:lo + BLK].rearrange("p j (q s e) -> p s q j e", s=2, e=2)
+            src = raws[b][:].rearrange("p j (q s e) -> p s q j e", s=2, e=2)
             if on_scalar:
                 for s in range(2):
                     nc.scalar.copy(out=dst[:, s], in_=src[:, s])
             else:
                 nc.vector.tensor_copy(out=dst, in_=src)
             grouped[b] = g2
-            if b % 2 == 1 and b // 2 + 3 < NCHUNK:
-                load_w2(b // 2 + 3)
+            if b + NRAW < NBLK:
+                load_w2(b + NRAW)
 
         def prep_quant(b):
             cd = cp.tile([P, BLK], U32, name="cd", tag="cd", align_bytes=64)
@@ -136,6 +141,12 @@ def tile_decoder_kernel(tc, digits, styles, images, W_h, b_h, W1, b1, W2, b2, ou
             nc.vector.quantize_mx(out=cd[:].bitcast(FP8X4), scales=pl[:], in_=grouped[b][:])
             codes[b] = cd
             planes[b] = pl
+
+        def prep_to(last):
+            for b in range(len(codes), min(last + 1, NBLK)):
+                if b + 1 < NBLK and b + 1 not in grouped:
+                    prep_copy(b + 1)
+                prep_quant(b)
 
         def mx(b, r):
             u = pu.tile([P, TOK], F32, name="u", tag="u")
@@ -158,94 +169,69 @@ def tile_decoder_kernel(tc, digits, styles, images, W_h, b_h, W1, b1, W2, b2, ou
                 bias=nb2[:, 4 * b + r:4 * b + r + 1], scale=-1.0,
             )
 
-        def logs(b, r0=0, r1=4):
+        def log_b(b, r0=0, r1=4):
             if r0 == 0:
                 btile[b] = bp.tile([P, 4, TOK], F32, name="bt", tag="bt")
             nc.scalar.activation(out=btile[b][:, r0:r1, :], in_=ytile[b][:, r0:r1, :], func=ACT.Ln,
                                  bias=eps_b[:, 0:1], scale=1.0)
+
+        def log_a(b, r0=0, r1=4):
             nc.scalar.activation(out=ytile[b][:, r0:r1, :], in_=ytile[b][:, r0:r1, :], func=ACT.Ln,
                                  bias=one_eps_b[:, 0:1], scale=-1.0)
 
         def imgt(b):
-            lo = (b % 2) * BLK
             for s in range(2):
                 if b >= NBLK - BB and s == 1:
                     it = pu.tile([P, TOK], F32, name="it_u", tag="u")
                 else:
                     it = pi.tile([P, TOK], F32, name="it", tag="it")
                 for t in range(NT):
-                    words = imgs[b // 2][:, t, lo:lo + BLK].bitcast(F32)
+                    words = imgs[b][:, t, :].bitcast(F32)
                     nc.tensor.transpose(
                         out=it[:, t * P:(t + 1) * P],
                         in_=words.rearrange("p (q s) -> p s q", s=2)[:, s, :],
                         identity=ident_f[:],
                     )
                 itile[(b, s)] = it
-            if b % 2 == 1 and b // 2 + 3 < NCHUNK:
-                load_img(b // 2 + 3)
+            if b + NIMG < NBLK:
+                load_img(b + NIMG)
 
-        def is_uv(b, r):
-            return r in (UV_LAST if b >= NBLK - NLAST else UV_TILES)
+        def image(b, r0, r1):
+            s = r0 // 2
+            iv = itile[(b, s)][:].bitcast(BF16).rearrange("p (t e) -> p e t", e=2)
+            return iv[:, r0 - 2 * s:r1 - 2 * s, :]
 
-        def runs(b, r0, r1):
-            found = []
-            for r in range(r0, r1):
-                if found and found[-1][1] == r and r % 2 == 1 and is_uv(b, r) == found[-1][2]:
-                    found[-1] = (found[-1][0], r + 1, found[-1][2])
-                else:
-                    found.append((r, r + 1, is_uv(b, r)))
-            return found
+        def diff(b, r0, r1):
+            nc.gpsimd.tensor_tensor(out=ytile[b][:, r0:r1, :], in0=ytile[b][:, r0:r1, :],
+                                    in1=btile[b][:, r0:r1, :], op=ALU.subtract)
 
-        def dsub(b, r0=0, r1=4, eng=None):
-            for (lo, hi, uv) in runs(b, r0, r1):
-                if not uv:
-                    (eng or nc.gpsimd).tensor_tensor(out=ytile[b][:, lo:hi, :], in0=ytile[b][:, lo:hi, :],
-                                                     in1=btile[b][:, lo:hi, :], op=ALU.subtract)
+        def mul(b, r0, r1):
+            nc.vector.scalar_tensor_tensor(out=ytile[b][:, r0:r1, :], in0=ytile[b][:, r0:r1, :],
+                                           scalar=D_MIN, in1=image(b, r0, r1),
+                                           op0=ALU.max, op1=ALU.mult)
 
-        def mul(b, r0=0, r1=4):
-            for (lo, hi, uv) in runs(b, r0, r1):
-                s = lo // 2
-                iv = itile[(b, s)][:].bitcast(BF16).rearrange("p (t e) -> p e t", e=2)
-                iv = iv[:, lo - 2 * s:hi - 2 * s, :]
-                a_s = ytile[b][:, lo:hi, :]
-                b_s = btile[b][:, lo:hi, :]
-                nc.vector.scalar_tensor_tensor(out=a_s, in0=a_s, scalar=D_MIN, in1=iv,
-                                               op0=ALU.max, op1=ALU.mult)
-                if uv:
-                    nc.vector.scalar_tensor_tensor(out=b_s, in0=iv, scalar=1.0, in1=b_s,
-                                                   op0=ALU.subtract, op1=ALU.mult)
+        def neg(b, r):
+            nt = npool.tile([P, 1, TOK], F32, name="nt", tag="nt")
+            nc.vector.scalar_tensor_tensor(out=nt[:], in0=btile[b][:, r:r + 1, :], scalar=-1.0,
+                                           in1=image(b, r, r + 1), op0=ALU.mult, op1=ALU.mult)
+            ntile[(b, r)] = nt
 
-        def zsub(b, r0=0, r1=4, eng=None):
-            for (lo, hi, uv) in runs(b, r0, r1):
-                if uv:
-                    (eng or nc.gpsimd).tensor_tensor(out=ytile[b][:, lo:hi, :], in0=ytile[b][:, lo:hi, :],
-                                                     in1=btile[b][:, lo:hi, :], op=ALU.subtract)
-
-        def arrays(b):
-            return ([("b", r) for r in range(4) if not is_uv(b, r)]
-                    + [("y", r) for r in range(4) if not is_uv(b, r)]
-                    + [("y", r) for r in range(4) if is_uv(b, r)])
-
-        def summ(b, picks=None):
-            if b not in stile:
+        def summ(b, arrays, first, last):
+            if first:
                 if b == NBLK - 1:
                     stile[b] = pu.tile([P, TOK], F32, name="st_last", tag="u")
                 else:
                     stile[b] = ps.tile([P, TOK], F32, name="st", tag="st")
-                done[b] = 0
-            total = len(arrays(b)) * NT
-            for (which, r) in (arrays(b) if picks is None else picks):
-                src = btile[b] if which == "b" else ytile[b]
+            for n, src in enumerate(arrays):
                 for t in range(NT):
                     nc.tensor.matmul(
                         out=stile[b][:, t * P:(t + 1) * P],
-                        lhsT=src[:, r, t * P:(t + 1) * P],
+                        lhsT=src[:, t * P:(t + 1) * P],
                         rhs=ident_f[:],
                         is_transpose=True,
-                        start=(done[b] == 0),
-                        stop=(done[b] == total - 1),
+                        start=(first and n == 0 and t == 0),
+                        stop=(last and n == len(arrays) - 1 and t == NT - 1),
                     )
-                    done[b] = done[b] + 1
 
         def red(b):
             nc.vector.tensor_reduce(
@@ -254,6 +240,11 @@ def tile_decoder_kernel(tc, digits, styles, images, W_h, b_h, W1, b1, W2, b2, ou
                 axis=AX.X, op=ALU.add, negate=True,
             )
 
+        idle = const.tile([P, TOK], BF16, name="idle")
+        nc.vector.memset(idle[:], 0.0)
+        idle_ps = pu.tile([P, TOK], F32, name="idle_ps", tag="u")
+        for n in range(NIDLE):
+            nc.tensor.matmul(out=idle_ps[:], lhsT=idle[:, 0:P], rhs=idle[:], start=True, stop=True)
         cat_ps = pi.tile([P, TOK], BF16, name="cat_ps", tag="it")
         for t in range(NT):
             nc.tensor.transpose(out=cat_ps[:, t * P:(t + 1) * P], in_=cat[:, t, :],
@@ -264,26 +255,10 @@ def tile_decoder_kernel(tc, digits, styles, images, W_h, b_h, W1, b1, W2, b2, ou
         nc.tensor.transpose(out=bias_ps[:], in_=brow[:], identity=ident_bf[:])
         bh = const.tile([P, 4], F32, name="bh")
         nc.vector.tensor_copy(out=bh[:], in_=bias_ps[:, 0:4])
+        b1c = const.tile([P, 4], F32, name="b1c")
+        nc.vector.tensor_copy(out=b1c[:], in_=bias_ps[:, 4:8])
         b1e = const.tile([P, 4], F32, name="b1e")
         nc.vector.tensor_scalar_add(out=b1e[:], in0=bias_ps[:, 4:8], scalar1=math.log(SA))
-        b1s = const.tile([P, 4], F32, name="b1s")
-        nc.vector.tensor_scalar_mul(out=b1s[:], in0=bias_ps[:, 4:8], scalar1=SELU_SCALE)
-
-        h_sb = bp.tile([P, 4, TOK], BF16, name="h_sb", tag="bt")
-        for j in range(4):
-            hp = pu.tile([P, TOK], F32, name="hp", tag="u")
-            nc.tensor.matmul(out=hp[:], lhsT=wh[:, j * P:(j + 1) * P], rhs=cat_t[:],
-                             start=True, stop=True)
-            nc.scalar.activation(out=h_sb[:, j, :], in_=hp[:], func=ACT.Relu,
-                                 bias=bh[:, j:j + 1], scale=1.0)
-
-        b2_ps = pi.tile([P, 2 * P], F32, name="b2_ps", tag="it")
-        for s in range(2):
-            nc.tensor.transpose(
-                out=b2_ps[:, s * P:(s + 1) * P],
-                in_=b2rows[:].bitcast(F32).rearrange("p (q s) -> p s q", s=2)[:, s, :],
-                identity=ident_f[:],
-            )
 
         def regroup(dst, src):
             nc.vector.tensor_copy(
@@ -293,6 +268,37 @@ def tile_decoder_kernel(tc, digits, styles, images, W_h, b_h, W1, b1, W2, b2, ou
 
         w1g = gp.tile([P, 4 * HN], BF16, name="w1g", tag="g2", align_bytes=64)
         regroup(w1g, raw1)
+        load_w2(NRAW - 1)
+        h_sb = bp.tile([P, 4, TOK], BF16, name="h_sb", tag="bt")
+        for j in range(4):
+            hp = pu.tile([P, TOK], F32, name="hp", tag="u")
+            nc.tensor.matmul(out=hp[:], lhsT=wh[:, j * P:(j + 1) * P], rhs=cat_t[:],
+                             start=True, stop=True)
+            if j < 3:
+                nc.scalar.activation(out=h_sb[:, j, :], in_=hp[:], func=ACT.Relu,
+                                     bias=bh[:, j:j + 1], scale=1.0)
+            else:
+                nc.vector.tensor_scalar(out=h_sb[:, j, :], in0=hp[:], scalar1=bh[:, j:j + 1],
+                                        scalar2=0.0, op0=ALU.add, op1=ALU.max)
+
+        w1_codes = cp.tile([P, HN], U32, name="w1_codes", tag="cd", align_bytes=64)
+        w1_plane = cp.tile([P, HN], U8, name="w1_plane", tag="pl", align_bytes=64)
+        nc.vector.quantize_mx(out=w1_codes[:].bitcast(FP8X4), scales=w1_plane[:], in_=w1g[:])
+
+        hg = gp.tile([P, 4 * TOK], BF16, name="hg", tag="g2", align_bytes=64)
+        regroup(hg, h_sb)
+        h_codes = cp.tile([P, TOK], U32, name="h_codes", tag="cd", align_bytes=64)
+        h_plane = cp.tile([P, TOK], U8, name="h_plane", tag="pl", align_bytes=64)
+        nc.vector.quantize_mx(out=h_codes[:].bitcast(FP8X4), scales=h_plane[:], in_=hg[:])
+
+        b2_ps = pi.tile([P, 2 * P], F32, name="b2_ps", tag="it")
+        for s in range(2):
+            nc.tensor.transpose(
+                out=b2_ps[:, s * P:(s + 1) * P],
+                in_=b2rows[:].bitcast(F32).rearrange("p (q s) -> p s q", s=2)[:, s, :],
+                identity=ident_f[:],
+            )
+
         nb2 = const.tile([P, 4 * NBLK], F32, name="nb2")
         nb2_v = nb2[:].rearrange("p (b s e) -> p b s e", s=2, e=2)
         for s in range(2):
@@ -301,65 +307,81 @@ def tile_decoder_kernel(tc, digits, styles, images, W_h, b_h, W1, b1, W2, b2, ou
                 in0=b2_ps[:, s * P:s * P + NBLK].bitcast(BF16).rearrange("p (b e) -> p b e", e=2),
                 scalar1=-1.0,
             )
-        w1_codes = const.tile([P, HN], U32, name="w1_codes", align_bytes=64)
-        w1_plane = const.tile([P, HN], U8, name="w1_plane", align_bytes=64)
-        nc.vector.quantize_mx(out=w1_codes[:].bitcast(FP8X4), scales=w1_plane[:], in_=w1g[:])
-
-        hg = gp.tile([P, 4 * TOK], BF16, name="hg", tag="g2", align_bytes=64)
-        regroup(hg, h_sb)
-        h_codes = const.tile([P, TOK], U32, name="h_codes", align_bytes=64)
-        h_plane = const.tile([P, TOK], U8, name="h_plane", align_bytes=64)
-        nc.vector.quantize_mx(out=h_codes[:].bitcast(FP8X4), scales=h_plane[:], in_=hg[:])
-
         prep_copy(0, on_scalar=True)
-        prep_copy(1)
-        prep_quant(0)
         e_sb = yp.tile([P, 4, TOK], F32, name="e_sb", tag="y")
         r_sb = bp.tile([P, 4, TOK], F32, name="r_sb", tag="bt")
-        t_sb = bp.tile([P, 4, TOK], BF16, name="t_sb", tag="bt")
-        for m in range(4):
-            tp = pu.tile([P, TOK], F32, name="tp", tag="u")
-            nc.tensor.matmul_mx(
-                out=tp[:],
-                lhsT=w1_codes[:, m * P:(m + 1) * P].bitcast(FP8X4),
-                lhsT_scale=w1_plane[:, m * P:(m + 1) * P],
-                rhs=h_codes[:].bitcast(FP8X4),
-                rhs_scale=h_plane[:],
-                start=True,
-                stop=True,
-            )
-            nc.scalar.activation(out=e_sb[:, m, :], in_=tp[:], func=ACT.Exp,
-                                 bias=b1e[:, m:m + 1], scale=1.0)
-            nc.scalar.activation(out=r_sb[:, m, :], in_=tp[:], func=ACT.Relu,
-                                 bias=b1s[:, m:m + 1], scale=SELU_SCALE)
-            nc.vector.tensor_scalar(out=e_sb[:, m, :], in0=e_sb[:, m, :], scalar1=SA,
-                                    scalar2=-SA, op0=ALU.min, op1=ALU.add)
-            nc.vector.tensor_tensor(out=t_sb[:, m, :], in0=e_sb[:, m, :], in1=r_sb[:, m, :],
-                                    op=ALU.add)
         tg = gp.tile([P, 4 * TOK], BF16, name="tg", tag="g2", align_bytes=64)
-        regroup(tg, t_sb)
-        nc.scalar.activation(out=warm[:], in_=eps_b[:], func=ACT.Sigmoid)
-        prep_quant(1)
-        prep_copy(2, on_scalar=True)
         t_codes = const.tile([P, TOK], U32, name="t_codes", align_bytes=64)
         t_plane = const.tile([P, TOK], U8, name="t_plane", align_bytes=64)
-        nc.vector.quantize_mx(out=t_codes[:].bitcast(FP8X4), scales=t_plane[:], in_=tg[:])
-        for b in range(3, BB):
-            prep_copy(b)
-            prep_quant(b - 1)
-        prep_quant(BB - 1)
+        halves = [slice(h * HALF, (h + 1) * HALF) for h in range(2)]
+        for h, cols in enumerate(halves):
+            pairs = [pu.tile([P, 2, HALF], F32, name="tp_a", tag="u"),
+                     pi.tile([P, 2, HALF], F32, name="tp_b", tag="it")]
+            for m in range(4):
+                nc.tensor.matmul_mx(
+                    out=pairs[m // 2][:, m % 2, :],
+                    lhsT=w1_codes[:, m * P:(m + 1) * P].bitcast(FP8X4),
+                    lhsT_scale=w1_plane[:, m * P:(m + 1) * P],
+                    rhs=h_codes[:, cols].bitcast(FP8X4),
+                    rhs_scale=h_plane[:, cols],
+                    start=True,
+                    stop=True,
+                )
+
+            def pre(m):
+                return pairs[m // 2][:, m % 2, :]
+
+            def expo(m):
+                nc.scalar.activation(out=e_sb[:, m, cols], in_=pre(m), func=ACT.Exp,
+                                     bias=b1e[:, m:m + 1], scale=1.0)
+                nc.gpsimd.tensor_scalar(out=e_sb[:, m, cols], in0=e_sb[:, m, cols], scalar1=SA,
+                                        scalar2=-SA, op0=ALU.min, op1=ALU.add)
+
+            nc.vector.tensor_scalar(out=r_sb[:, 0, cols], in0=pre(0), scalar1=b1c[:, 0:1],
+                                    scalar2=0.0, op0=ALU.add, op1=ALU.max)
+            nc.vector.tensor_scalar(out=r_sb[:, 1, cols], in0=pre(1), scalar1=b1c[:, 1:2],
+                                    scalar2=0.0, op0=ALU.add, op1=ALU.max)
+            expo(2)
+            expo(3)
+            nc.scalar.activation(out=r_sb[:, 3, cols], in_=pre(3), func=ACT.Relu,
+                                 bias=b1c[:, 3:4], scale=1.0)
+            expo(0)
+            expo(1)
+            nc.vector.tensor_scalar(out=r_sb[:, 2, cols], in0=pre(2), scalar1=b1c[:, 2:3],
+                                    scalar2=0.0, op0=ALU.add, op1=ALU.max)
+        nc.scalar.activation(out=warm[:], in_=eps_b[:], func=ACT.Sigmoid)
+        prep_quant(0)
+        for h, cols in enumerate(halves):
+            words = slice(4 * h * HALF, 4 * (h + 1) * HALF)
+            nc.vector.scalar_tensor_tensor(
+                out=tg[:, words].rearrange("p (c t) -> p c t", t=4),
+                in0=r_sb[:, :, cols].rearrange("p t c -> p c t"),
+                scalar=SELU_SCALE,
+                in1=e_sb[:, :, cols].rearrange("p t c -> p c t"),
+                op0=ALU.mult, op1=ALU.add)
+            nc.vector.quantize_mx(out=t_codes[:, cols].bitcast(FP8X4), scales=t_plane[:, cols],
+                                  in_=tg[:, words])
+        prep_copy(1)
+        prep_quant(1)
+        prep_copy(2)
+        prep_to(2)
 
         res = const.tile([P, NT, CH // 64], F32, name="res")
 
         early = 3
         pending = []
 
-        def sum_red(h, picks=None, new=True):
-            if new:
-                if len(pending) >= SBANKS:
-                    red(pending.pop(0))
-                pending.append(h)
-            summ(h, picks)
+        def open_sum(h):
+            if len(pending) >= SBANKS:
+                red(pending.pop(0))
+            pending.append(h)
+            summ(h, [btile[h][:, r, :] for r in range(4)], True, False)
+
+        def sum_red(h):
+            open_sum(h)
+            summ(h, [ntile[(h, r)][:, 0, :] for r in PRODS]
+                 + [ytile[h][:, r, :] for r in PRODS]
+                 + [ytile[h][:, r, :] for (r0, r1) in DIFFS for r in range(r0, r1)], False, True)
 
         for n in range(early):
             mx(n // 4, n % 4)
@@ -372,12 +394,8 @@ def tile_decoder_kernel(tc, digits, styles, images, W_h, b_h, W1, b1, W2, b2, ou
                 if n >= early:
                     mx(b, r)
                 sig(b, r)
-                if r == 3 and b + BB < NBLK:
-                    prep_copy(b + BB)
-                    if n // 4 > 0:
-                        prep_quant(b + BB - 1)
-            if not last_batch:
-                prep_quant(first + 2 * BB - 1)
+                if r == 3:
+                    prep_to(min(b + NCODE, BB + AHEAD - 1) if i == 0 else b + AHEAD)
             imgt(first)
             if last_batch:
                 imgt(first + 1)
@@ -387,10 +405,12 @@ def tile_decoder_kernel(tc, digits, styles, images, W_h, b_h, W1, b1, W2, b2, ou
                     sum_red(late)
             for k in range(BB):
                 g = first + k
-                if g >= NBLK - NLAST:
+                if g >= NBLK - 2:
                     continue
-                logs(g)
-                dsub(g)
+                log_b(g)
+                log_a(g)
+                for (r0, r1) in DIFFS:
+                    diff(g, r0, r1)
                 if k == BB - 3 and not last_batch:
                     for n in range(early):
                         mx(first + BB + n // 4, n % 4)
@@ -399,19 +419,46 @@ def tile_decoder_kernel(tc, digits, styles, images, W_h, b_h, W1, b1, W2, b2, ou
                         imgt(g + 3)
                 elif k < BB - 1:
                     imgt(g + 1)
-                mul(g)
-                zsub(g)
-                h = g - SL
-                if h >= first and (last_batch or h < first + BB - DEFER):
-                    sum_red(h)
+                for r in PRODS:
+                    neg(g, r)
+                    mul(g, r, r + 1)
+                for (r0, r1) in DIFFS:
+                    mul(g, r0, r1)
+                if last_batch or g < first + BB - DEFER:
+                    sum_red(g)
         nc.sync.dma_start(out=out_v[:, :, 0:8 * (NBLK - BB)], in_=res[:, :, 0:8 * (NBLK - BB)])
-        g = NBLK - 1
+        g = NBLK - 2
+        e = NBLK - 1
+        log_b(g)
+        log_a(g)
+        log_b(e)
         for r in range(4):
-            logs(g, r, r + 1)
+            log_a(e, r, r + 1)
+        for (r0, r1) in LATE_DIFFS:
+            diff(g, r0, r1)
+        diff(e, 0, 1)
+        for r in LATE_PRODS:
+            neg(g, r)
+        open_sum(g)
+        summ(g, [ntile[(g, r)][:, 0, :] for r in LATE_PRODS], False, False)
+        for r in LATE_PRODS:
             mul(g, r, r + 1)
-            zsub(g, r, r + 1, nc.vector if r == 3 else nc.gpsimd)
-            summ(g, [("y", r)])
-        pending.append(g)
+            summ(g, [ytile[g][:, r, :]], False, False)
+        mul(g, 2, 3)
+        summ(g, [ytile[g][:, 2, :]], False, False)
+        summ(e, [btile[e][:, r, :] for r in range(4)], True, False)
+        neg(e, 1)
+        mul(g, 3, 4)
+        summ(g, [ytile[g][:, 3, :]], False, True)
+        neg(e, 2)
+        neg(e, 3)
+        summ(e, [ntile[(e, r)][:, 0, :] for r in END_PRODS], False, False)
+        for r in (1, 0, 2):
+            mul(e, r, r + 1)
+            summ(e, [ytile[e][:, r, :]], False, False)
         while pending:
             red(pending.pop(0))
+        mul(e, 3, 4)
+        summ(e, [ytile[e][:, 3, :]], False, True)
+        red(e)
         nc.sync.dma_start(out=out_v[:, :, 8 * (NBLK - BB):], in_=res[:, :, 8 * (NBLK - BB):])

@@ -15,32 +15,33 @@ AX = mybir.AxisListType
 
 P = 128
 TOK = 512
+HALF = TOK // 2
 NT = 4
 HN = 512
 CH = 12288
 BLK = 512
-HALF = TOK // 2
 NBLK = CH // BLK
-BB = 12
-NBATCH = NBLK // BB
-NRAW = 4
-NIMG = 4
-NCODE = 8
-NIDLE = 4
-AHEAD = 6
 EPS = 1e-9
 D_MIN = math.log(EPS) - 1e-3
 SELU_ALPHA = 1.6732632423543772848170429916717
 SELU_SCALE = 1.0507009873554804934193349852946
 SA = SELU_SCALE * SELU_ALPHA
 
+NSLOT = NBLK + 3
+NCODE = 3
+RAW_SLOTS = (22, 23, 24, 25)
+GROUP_SLOTS = (21, 26)
+MX_BANKS = (0, 1, 2, 7)
+IMG_BANKS = ((3, 4), (5, 6), (0, 1))
+SUM_BANKS = (2, 7)
+
+FIRST_DIFFS = ((2, 4), (0, 2))
 PRODS = (0,)
 DIFFS = ((2, 4), (1, 2))
 LATE_PRODS = (0, 1)
 LATE_DIFFS = ((2, 3), (3, 4))
 END_PRODS = (1, 2, 3)
-DEFER = 2
-SBANKS = 2
+END_DIFFS = ((0, 1),)
 
 FLOPS = 2 * TOK * (128 * HN + HN * HN + HN * CH)
 
@@ -57,20 +58,21 @@ def tile_decoder_kernel(tc, digits, styles, images, W_h, b_h, W1, b1, W2, b2, ou
     with ExitStack() as ctx:
         ctx.enter_context(tc.manual_schedule())
         const = ctx.enter_context(tc.tile_pool(name="const", bufs=1))
-        yp = ctx.enter_context(tc.tile_pool(name="yp", bufs=BB + DEFER))
-        bp = ctx.enter_context(tc.tile_pool(name="bp", bufs=5))
-        rawp = ctx.enter_context(tc.tile_pool(name="rawp", bufs=NRAW))
-        gp = ctx.enter_context(tc.tile_pool(name="gp", bufs=3))
+        big = ctx.enter_context(tc.tile_pool(name="big", bufs=1))
         cp = ctx.enter_context(tc.tile_pool(name="cp", bufs=NCODE))
-        npool = ctx.enter_context(tc.tile_pool(name="npool", bufs=3))
-        imp = ctx.enter_context(tc.tile_pool(name="imp", bufs=NIMG))
-        pu = ctx.enter_context(tc.psum_pool(name="pu", bufs=3))
-        pi = ctx.enter_context(tc.psum_pool(name="pi", bufs=3))
-        ps = ctx.enter_context(tc.psum_pool(name="ps", bufs=2))
+        imp = ctx.enter_context(tc.tile_pool(name="imp", bufs=2))
+        psum = ctx.enter_context(tc.psum_pool(name="psum", bufs=1))
+
+        def slot(s, shape, dtype, name):
+            return big.tile(shape, dtype, name=name, tag="s%d" % s, align_bytes=64)
+
+        def bank(k, shape, dtype, name):
+            return psum.tile(shape, dtype, name=name, tag="b%d" % k)
 
         raws = {}
         imgs = {}
-        grouped = {}
+        groups = {}
+        grouped = set()
         codes = {}
         planes = {}
         ubank = {}
@@ -79,14 +81,19 @@ def tile_decoder_kernel(tc, digits, styles, images, W_h, b_h, W1, b1, W2, b2, ou
         itile = {}
         ntile = {}
         stile = {}
+        bslot = {}
+        nslot = {}
+        free = [24, 25, 26]
 
         ident_bf = const.tile([P, P], BF16, name="ident_bf")
         masks.make_identity(nc, ident_bf[:])
         ident_f = const.tile([P, P], F32, name="ident_f")
         masks.make_identity(nc, ident_f[:])
-        brow = const.tile([P, P], BF16, name="brow")
+        idle = slot(17, [P, TOK], BF16, "idle")
+        nc.vector.memset(idle[:], 0.0)
+        brow = slot(7, [P, P], BF16, "brow")
         nc.vector.memset(brow[:], 0.0)
-        b2rows = const.tile([P, BLK], BF16, name="b2rows")
+        b2rows = slot(8, [P, BLK], BF16, "b2rows")
         nc.vector.memset(b2rows[:], 0.0)
         eps_b = const.tile([P, 1], F32, name="eps_b")
         nc.vector.memset(eps_b[:], EPS)
@@ -96,49 +103,60 @@ def tile_decoder_kernel(tc, digits, styles, images, W_h, b_h, W1, b1, W2, b2, ou
         warm = const.tile([P, 1], F32, name="warm")
         nc.scalar.activation(out=warm[:], in_=eps_b[:], func=ACT.Relu)
 
-        cat = const.tile([P, NT, P], BF16, name="cat")
+        cat = slot(5, [P, NT, P], BF16, "cat")
         nc.sync.dma_start(out=cat[:, :, 0:32], in_=dig_v)
         nc.sync.dma_start(out=cat[:, :, 32:128], in_=sty_v)
-        wh = const.tile([P, HN], BF16, name="wh")
+        wh = slot(6, [P, HN], BF16, "wh")
         nc.sync.dma_start(out=wh[:], in_=W_h)
         nc.sync.dma_start(out=brow[0:4, :], in_=b_h.rearrange("(j p) -> j p", p=P))
         nc.sync.dma_start(out=brow[4:8, :], in_=b1.rearrange("(j p) -> j p", p=P))
-        raw1 = rawp.tile([P, 4, HN], BF16, name="raw1", tag="raw")
+        raw1 = slot(10, [P, 4, HN], BF16, "raw1")
         nc.sync.dma_start(out=raw1[:], in_=w1_v)
         nc.sync.dma_start(out=b2rows[0:NBLK, :], in_=b2.rearrange("(b x) -> b x", x=BLK))
 
-        def load_w2(b):
-            raw = rawp.tile([P, 4, BLK], BF16, name="raw", tag="raw")
-            nc.sync.dma_start(out=raw[:], in_=w2_v[:, :, b * BLK:(b + 1) * BLK])
-            raws[b] = raw
+        def load_w2(c, parts=1):
+            raw = slot(RAW_SLOTS[c % 4], [P, 4, 2 * BLK], BF16, "raw")
+            width = 2 * BLK // parts
+            for n in range(parts):
+                lo = n * width
+                nc.sync.dma_start(out=raw[:, :, lo:lo + width],
+                                  in_=w2_v[:, :, 2 * BLK * c + lo:2 * BLK * c + lo + width])
+            raws[c] = raw
 
         def load_img(b):
-            im = imp.tile([P, NT, BLK], BF16, name="im", tag="im")
+            if b < 2:
+                im = slot(18 + b, [P, NT, BLK], BF16, "im_first")
+            else:
+                im = imp.tile([P, NT, BLK], BF16, name="im", tag="im")
             nc.sync.dma_start(out=im[:], in_=img_v[:, :, b * BLK:(b + 1) * BLK])
             imgs[b] = im
 
-        for b in range(NRAW - 1):
-            load_w2(b)
-        for b in range(NIMG):
+        load_w2(0, parts=2)
+        for c in range(1, 4):
+            load_w2(c)
+        for b in range(4):
             load_img(b)
 
         def prep_copy(b, on_scalar=False):
-            g2 = gp.tile([P, 4 * BLK], BF16, name="g2", tag="g2", align_bytes=64)
-            dst = g2[:].rearrange("p (s e q j) -> p s q j e", s=2, e=2, j=4)
-            src = raws[b][:].rearrange("p j (q s e) -> p s q j e", s=2, e=2)
+            c = b // 2
+            if b % 2 == 0:
+                groups[c] = slot(GROUP_SLOTS[c % 2], [P, 2, 4 * BLK], BF16, "g2")
+            lo = (b % 2) * BLK
+            dst = groups[c][:, b % 2, :].rearrange("p (s e q j) -> p s q j e", s=2, e=2, j=4)
+            src = raws[c][:, :, lo:lo + BLK].rearrange("p j (q s e) -> p s q j e", s=2, e=2)
             if on_scalar:
                 for s in range(2):
                     nc.scalar.copy(out=dst[:, s], in_=src[:, s])
             else:
                 nc.vector.tensor_copy(out=dst, in_=src)
-            grouped[b] = g2
-            if b + NRAW < NBLK:
-                load_w2(b + NRAW)
+            grouped.add(b)
+            if b % 2 == 1 and c + 4 < NBLK // 2:
+                load_w2(c + 4)
 
         def prep_quant(b):
             cd = cp.tile([P, BLK], U32, name="cd", tag="cd", align_bytes=64)
             pl = cp.tile([P, BLK], U8, name="pl", tag="pl", align_bytes=64)
-            nc.vector.quantize_mx(out=cd[:].bitcast(FP8X4), scales=pl[:], in_=grouped[b][:])
+            nc.vector.quantize_mx(out=cd[:].bitcast(FP8X4), scales=pl[:], in_=groups[b // 2][:, b % 2, :])
             codes[b] = cd
             planes[b] = pl
 
@@ -149,7 +167,7 @@ def tile_decoder_kernel(tc, digits, styles, images, W_h, b_h, W1, b1, W2, b2, ou
                 prep_quant(b)
 
         def mx(b, r):
-            u = pu.tile([P, TOK], F32, name="u", tag="u")
+            u = bank(MX_BANKS[r], [P, TOK], F32, "u")
             nc.tensor.matmul_mx(
                 out=u[:],
                 lhsT=codes[b][:, r * P:(r + 1) * P].bitcast(FP8X4),
@@ -163,16 +181,16 @@ def tile_decoder_kernel(tc, digits, styles, images, W_h, b_h, W1, b1, W2, b2, ou
 
         def sig(b, r):
             if r == 0:
-                ytile[b] = yp.tile([P, 4, TOK], F32, name="y", tag="y")
+                ytile[b] = slot(b, [P, 4, TOK], F32, "y")
             nc.scalar.activation(
                 out=ytile[b][:, r, :], in_=ubank[(b, r)][:], func=ACT.Sigmoid,
                 bias=nb2[:, 4 * b + r:4 * b + r + 1], scale=-1.0,
             )
 
-        def log_b(b, r0=0, r1=4):
-            if r0 == 0:
-                btile[b] = bp.tile([P, 4, TOK], F32, name="bt", tag="bt")
-            nc.scalar.activation(out=btile[b][:, r0:r1, :], in_=ytile[b][:, r0:r1, :], func=ACT.Ln,
+        def log_b(b):
+            bslot[b] = free.pop(0)
+            btile[b] = slot(bslot[b], [P, 4, TOK], F32, "bt")
+            nc.scalar.activation(out=btile[b][:], in_=ytile[b][:], func=ACT.Ln,
                                  bias=eps_b[:, 0:1], scale=1.0)
 
         def log_a(b, r0=0, r1=4):
@@ -181,10 +199,7 @@ def tile_decoder_kernel(tc, digits, styles, images, W_h, b_h, W1, b1, W2, b2, ou
 
         def imgt(b):
             for s in range(2):
-                if b >= NBLK - BB and s == 1:
-                    it = pu.tile([P, TOK], F32, name="it_u", tag="u")
-                else:
-                    it = pi.tile([P, TOK], F32, name="it", tag="it")
+                it = bank(IMG_BANKS[b % 3][s], [P, TOK], F32, "it")
                 for t in range(NT):
                     words = imgs[b][:, t, :].bitcast(F32)
                     nc.tensor.transpose(
@@ -193,8 +208,8 @@ def tile_decoder_kernel(tc, digits, styles, images, W_h, b_h, W1, b1, W2, b2, ou
                         identity=ident_f[:],
                     )
                 itile[(b, s)] = it
-            if b + NIMG < NBLK:
-                load_img(b + NIMG)
+            if b >= 2 and b + 2 < NBLK:
+                load_img(b + 2)
 
         def image(b, r0, r1):
             s = r0 // 2
@@ -211,17 +226,16 @@ def tile_decoder_kernel(tc, digits, styles, images, W_h, b_h, W1, b1, W2, b2, ou
                                            op0=ALU.max, op1=ALU.mult)
 
         def neg(b, r):
-            nt = npool.tile([P, 1, TOK], F32, name="nt", tag="nt")
-            nc.vector.scalar_tensor_tensor(out=nt[:], in0=btile[b][:, r:r + 1, :], scalar=-1.0,
-                                           in1=image(b, r, r + 1), op0=ALU.mult, op1=ALU.mult)
-            ntile[(b, r)] = nt
+            if b not in ntile:
+                nslot[b] = free.pop(0)
+                ntile[b] = slot(nslot[b], [P, 4, TOK], F32, "nt")
+            nc.vector.scalar_tensor_tensor(out=ntile[b][:, r:r + 1, :], in0=btile[b][:, r:r + 1, :],
+                                           scalar=-1.0, in1=image(b, r, r + 1),
+                                           op0=ALU.mult, op1=ALU.mult)
 
         def summ(b, arrays, first, last):
             if first:
-                if b == NBLK - 1:
-                    stile[b] = pu.tile([P, TOK], F32, name="st_last", tag="u")
-                else:
-                    stile[b] = ps.tile([P, TOK], F32, name="st", tag="st")
+                stile[b] = bank(SUM_BANKS[b % 2], [P, TOK], F32, "st")
             for n, src in enumerate(arrays):
                 for t in range(NT):
                     nc.tensor.matmul(
@@ -232,6 +246,10 @@ def tile_decoder_kernel(tc, digits, styles, images, W_h, b_h, W1, b1, W2, b2, ou
                         start=(first and n == 0 and t == 0),
                         stop=(last and n == len(arrays) - 1 and t == NT - 1),
                     )
+            if last:
+                free.extend([b, bslot[b]])
+                if b in nslot:
+                    free.append(nslot[b])
 
         def red(b):
             nc.vector.tensor_reduce(
@@ -240,18 +258,20 @@ def tile_decoder_kernel(tc, digits, styles, images, W_h, b_h, W1, b1, W2, b2, ou
                 axis=AX.X, op=ALU.add, negate=True,
             )
 
-        idle = const.tile([P, TOK], BF16, name="idle")
-        nc.vector.memset(idle[:], 0.0)
-        idle_ps = pu.tile([P, TOK], F32, name="idle_ps", tag="u")
-        for n in range(NIDLE):
-            nc.tensor.matmul(out=idle_ps[:], lhsT=idle[:, 0:P], rhs=idle[:], start=True, stop=True)
-        cat_ps = pi.tile([P, TOK], BF16, name="cat_ps", tag="it")
+        idle_ps = bank(6, [P, TOK], F32, "idle_ps")
+
+        def idle_mm(count):
+            for n in range(count):
+                nc.tensor.matmul(out=idle_ps[:], lhsT=idle[:, 0:P], rhs=idle[:], start=True, stop=True)
+
+        idle_mm(4)
+        cat_ps = bank(3, [P, TOK], BF16, "cat_ps")
         for t in range(NT):
             nc.tensor.transpose(out=cat_ps[:, t * P:(t + 1) * P], in_=cat[:, t, :],
                                 identity=ident_bf[:])
-        cat_t = const.tile([P, TOK], BF16, name="cat_t")
+        cat_t = slot(9, [P, TOK], BF16, "cat_t")
         nc.vector.tensor_copy(out=cat_t[:], in_=cat_ps[:])
-        bias_ps = pi.tile([P, P], BF16, name="bias_ps", tag="it")
+        bias_ps = bank(4, [P, P], BF16, "bias_ps")
         nc.tensor.transpose(out=bias_ps[:], in_=brow[:], identity=ident_bf[:])
         bh = const.tile([P, 4], F32, name="bh")
         nc.vector.tensor_copy(out=bh[:], in_=bias_ps[:, 0:4])
@@ -266,12 +286,11 @@ def tile_decoder_kernel(tc, digits, styles, images, W_h, b_h, W1, b1, W2, b2, ou
                 in_=src[:].rearrange("p t (c i) -> p c t i", i=4),
             )
 
-        w1g = gp.tile([P, 4 * HN], BF16, name="w1g", tag="g2", align_bytes=64)
+        w1g = slot(11, [P, 4 * HN], BF16, "w1g")
         regroup(w1g, raw1)
-        load_w2(NRAW - 1)
-        h_sb = bp.tile([P, 4, TOK], BF16, name="h_sb", tag="bt")
+        h_sb = slot(12, [P, 4, TOK], BF16, "h_sb")
         for j in range(4):
-            hp = pu.tile([P, TOK], F32, name="hp", tag="u")
+            hp = bank((0, 1, 2, 7)[j], [P, TOK], F32, "hp")
             nc.tensor.matmul(out=hp[:], lhsT=wh[:, j * P:(j + 1) * P], rhs=cat_t[:],
                              start=True, stop=True)
             if j < 3:
@@ -285,20 +304,19 @@ def tile_decoder_kernel(tc, digits, styles, images, W_h, b_h, W1, b1, W2, b2, ou
         w1_plane = cp.tile([P, HN], U8, name="w1_plane", tag="pl", align_bytes=64)
         nc.vector.quantize_mx(out=w1_codes[:].bitcast(FP8X4), scales=w1_plane[:], in_=w1g[:])
 
-        hg = gp.tile([P, 4 * TOK], BF16, name="hg", tag="g2", align_bytes=64)
+        hg = slot(13, [P, 4 * TOK], BF16, "hg")
         regroup(hg, h_sb)
         h_codes = cp.tile([P, TOK], U32, name="h_codes", tag="cd", align_bytes=64)
         h_plane = cp.tile([P, TOK], U8, name="h_plane", tag="pl", align_bytes=64)
         nc.vector.quantize_mx(out=h_codes[:].bitcast(FP8X4), scales=h_plane[:], in_=hg[:])
 
-        b2_ps = pi.tile([P, 2 * P], F32, name="b2_ps", tag="it")
+        b2_ps = bank(5, [P, 2 * P], F32, "b2_ps")
         for s in range(2):
             nc.tensor.transpose(
                 out=b2_ps[:, s * P:(s + 1) * P],
                 in_=b2rows[:].bitcast(F32).rearrange("p (q s) -> p s q", s=2)[:, s, :],
                 identity=ident_f[:],
             )
-
         nb2 = const.tile([P, 4 * NBLK], F32, name="nb2")
         nb2_v = nb2[:].rearrange("p (b s e) -> p b s e", s=2, e=2)
         for s in range(2):
@@ -307,60 +325,50 @@ def tile_decoder_kernel(tc, digits, styles, images, W_h, b_h, W1, b1, W2, b2, ou
                 in0=b2_ps[:, s * P:s * P + NBLK].bitcast(BF16).rearrange("p (b e) -> p b e", e=2),
                 scalar1=-1.0,
             )
+
         prep_copy(0, on_scalar=True)
-        e_sb = yp.tile([P, 4, TOK], F32, name="e_sb", tag="y")
-        r_sb = bp.tile([P, 4, TOK], F32, name="r_sb", tag="bt")
-        tg = gp.tile([P, 4 * TOK], BF16, name="tg", tag="g2", align_bytes=64)
+        prep_quant(0)
+        e_sb = slot(14, [P, 4, TOK], F32, "e_sb")
+        r_sb = slot(15, [P, 4, TOK], F32, "r_sb")
+        tg = slot(16, [P, 4 * TOK], BF16, "tg")
         t_codes = const.tile([P, TOK], U32, name="t_codes", align_bytes=64)
         t_plane = const.tile([P, TOK], U8, name="t_plane", align_bytes=64)
-        halves = [slice(h * HALF, (h + 1) * HALF) for h in range(2)]
-        for h, cols in enumerate(halves):
-            pairs = [pu.tile([P, 2, HALF], F32, name="tp_a", tag="u"),
-                     pi.tile([P, 2, HALF], F32, name="tp_b", tag="it")]
-            for m in range(4):
-                nc.tensor.matmul_mx(
-                    out=pairs[m // 2][:, m % 2, :],
-                    lhsT=w1_codes[:, m * P:(m + 1) * P].bitcast(FP8X4),
-                    lhsT_scale=w1_plane[:, m * P:(m + 1) * P],
-                    rhs=h_codes[:, cols].bitcast(FP8X4),
-                    rhs_scale=h_plane[:, cols],
-                    start=True,
-                    stop=True,
-                )
-
-            def pre(m):
-                return pairs[m // 2][:, m % 2, :]
-
-            def expo(m):
-                nc.scalar.activation(out=e_sb[:, m, cols], in_=pre(m), func=ACT.Exp,
-                                     bias=b1e[:, m:m + 1], scale=1.0)
-                nc.gpsimd.tensor_scalar(out=e_sb[:, m, cols], in0=e_sb[:, m, cols], scalar1=SA,
-                                        scalar2=-SA, op0=ALU.min, op1=ALU.add)
-
-            nc.vector.tensor_scalar(out=r_sb[:, 0, cols], in0=pre(0), scalar1=b1c[:, 0:1],
-                                    scalar2=0.0, op0=ALU.add, op1=ALU.max)
-            nc.vector.tensor_scalar(out=r_sb[:, 1, cols], in0=pre(1), scalar1=b1c[:, 1:2],
-                                    scalar2=0.0, op0=ALU.add, op1=ALU.max)
-            expo(2)
-            expo(3)
-            nc.scalar.activation(out=r_sb[:, 3, cols], in_=pre(3), func=ACT.Relu,
-                                 bias=b1c[:, 3:4], scale=1.0)
-            expo(0)
-            expo(1)
-            nc.vector.tensor_scalar(out=r_sb[:, 2, cols], in0=pre(2), scalar1=b1c[:, 2:3],
-                                    scalar2=0.0, op0=ALU.add, op1=ALU.max)
+        idle_mm(6)
+        tps = [bank(MX_BANKS[m], [P, TOK], F32, "tp") for m in range(4)]
+        for m in range(4):
+            nc.tensor.matmul_mx(
+                out=tps[m][:],
+                lhsT=w1_codes[:, m * P:(m + 1) * P].bitcast(FP8X4),
+                lhsT_scale=w1_plane[:, m * P:(m + 1) * P],
+                rhs=h_codes[:].bitcast(FP8X4),
+                rhs_scale=h_plane[:],
+                start=True,
+                stop=True,
+            )
+        for m in range(4):
+            nc.scalar.activation(out=e_sb[:, m, :], in_=tps[m][:], func=ACT.Exp,
+                                 bias=b1e[:, m:m + 1], scale=1.0)
+        nc.scalar.activation(out=r_sb[:, 3, :], in_=tps[3][:], func=ACT.Relu,
+                             bias=b1c[:, 3:4], scale=1.0)
         nc.scalar.activation(out=warm[:], in_=eps_b[:], func=ACT.Sigmoid)
-        prep_quant(0)
-        for h, cols in enumerate(halves):
-            words = slice(4 * h * HALF, 4 * (h + 1) * HALF)
+        for m in (1, 2, 0):
+            nc.vector.tensor_scalar(out=r_sb[:, m, :], in0=tps[m][:], scalar1=b1c[:, m:m + 1],
+                                    scalar2=0.0, op0=ALU.add, op1=ALU.max)
+        for m in (0, 2):
+            nc.vector.tensor_scalar(out=e_sb[:, m:m + 2, :], in0=e_sb[:, m:m + 2, :], scalar1=SA,
+                                    scalar2=-SA, op0=ALU.min, op1=ALU.add)
+        for h in range(2):
+            cols = slice(h * HALF, (h + 1) * HALF)
             nc.vector.scalar_tensor_tensor(
-                out=tg[:, words].rearrange("p (c t) -> p c t", t=4),
+                out=tg[:, 4 * h * HALF:4 * (h + 1) * HALF].rearrange("p (c t) -> p c t", t=4),
                 in0=r_sb[:, :, cols].rearrange("p t c -> p c t"),
                 scalar=SELU_SCALE,
                 in1=e_sb[:, :, cols].rearrange("p t c -> p c t"),
                 op0=ALU.mult, op1=ALU.add)
+        for h in range(2):
+            cols = slice(h * HALF, (h + 1) * HALF)
             nc.vector.quantize_mx(out=t_codes[:, cols].bitcast(FP8X4), scales=t_plane[:, cols],
-                                  in_=tg[:, words])
+                                  in_=tg[:, 4 * h * HALF:4 * (h + 1) * HALF])
         prep_copy(1)
         prep_quant(1)
         prep_copy(2)
@@ -368,97 +376,67 @@ def tile_decoder_kernel(tc, digits, styles, images, W_h, b_h, W1, b1, W2, b2, ou
 
         res = const.tile([P, NT, CH // 64], F32, name="res")
 
-        early = 3
-        pending = []
+        forms = {}
+        for g in range(NBLK):
+            forms[g] = (PRODS, DIFFS)
+        for g in range(4):
+            forms[g] = ((), FIRST_DIFFS)
+        forms[NBLK - 2] = (LATE_PRODS, LATE_DIFFS)
+        forms[NBLK - 1] = (END_PRODS, END_DIFFS)
+
+        def negs(h):
+            for r in forms[h][0]:
+                neg(h, r)
 
         def open_sum(h):
-            if len(pending) >= SBANKS:
-                red(pending.pop(0))
-            pending.append(h)
-            summ(h, [btile[h][:, r, :] for r in range(4)], True, False)
+            summ(h, [btile[h][:, r, :] for r in range(4)]
+                 + [ntile[h][:, r, :] for r in forms[h][0]], True, False)
 
-        def sum_red(h):
-            open_sum(h)
-            summ(h, [ntile[(h, r)][:, 0, :] for r in PRODS]
-                 + [ytile[h][:, r, :] for r in PRODS]
-                 + [ytile[h][:, r, :] for (r0, r1) in DIFFS for r in range(r0, r1)], False, True)
-
-        for n in range(early):
-            mx(n // 4, n % 4)
-        for i in range(NBATCH):
-            first = i * BB
-            last_batch = first + BB >= NBLK
-            for n in range(4 * BB):
-                b = first + n // 4
-                r = n % 4
-                if n >= early:
-                    mx(b, r)
+        for b in range(NBLK):
+            for r in range(4):
+                mx(b, r)
                 sig(b, r)
-                if r == 3:
-                    prep_to(min(b + NCODE, BB + AHEAD - 1) if i == 0 else b + AHEAD)
-            imgt(first)
-            if last_batch:
-                imgt(first + 1)
-                imgt(first + 2)
-            if i > 0:
-                for late in range(first - DEFER, first):
-                    sum_red(late)
-            for k in range(BB):
-                g = first + k
-                if g >= NBLK - 2:
-                    continue
-                log_b(g)
-                log_a(g)
-                for (r0, r1) in DIFFS:
-                    diff(g, r0, r1)
-                if k == BB - 3 and not last_batch:
-                    for n in range(early):
-                        mx(first + BB + n // 4, n % 4)
-                if last_batch:
-                    if k < BB - 3:
-                        imgt(g + 3)
-                elif k < BB - 1:
-                    imgt(g + 1)
-                for r in PRODS:
-                    neg(g, r)
-                    mul(g, r, r + 1)
-                for (r0, r1) in DIFFS:
-                    mul(g, r0, r1)
-                if last_batch or g < first + BB - DEFER:
-                    sum_red(g)
-        nc.sync.dma_start(out=out_v[:, :, 0:8 * (NBLK - BB)], in_=res[:, :, 0:8 * (NBLK - BB)])
-        g = NBLK - 2
+            prep_to(b + NCODE)
+            if b in (3, 6):
+                imgt(b // 3 - 1)
+        imgt(2)
+
+        log_b(0)
+        negs(0)
+        open_sum(0)
+        for g in range(NBLK - 1):
+            prods, diffs = forms[g]
+            if g > 0:
+                log_b(g + 1)
+            log_a(g)
+            if g == 0:
+                log_b(1)
+            if g == NBLK - 2:
+                for r in range(4):
+                    log_a(NBLK - 1, r, r + 1)
+            for (r0, r1) in diffs:
+                diff(g, r0, r1)
+            negs(g + 1)
+            if g > 0:
+                red(g - 1)
+            for r in prods:
+                mul(g, r, r + 1)
+            for (r0, r1) in diffs:
+                mul(g, r0, r1)
+            open_sum(g + 1)
+            summ(g, [ytile[g][:, r, :] for r in prods]
+                 + [ytile[g][:, r, :] for (r0, r1) in diffs for r in range(r0, r1)], False, True)
+            if g + 3 < NBLK:
+                imgt(g + 3)
+            if g == NBLK // 2:
+                nc.sync.dma_start(out=out_v[:, :, 0:4 * NBLK], in_=res[:, :, 0:4 * NBLK])
         e = NBLK - 1
-        log_b(g)
-        log_a(g)
-        log_b(e)
-        for r in range(4):
-            log_a(e, r, r + 1)
-        for (r0, r1) in LATE_DIFFS:
-            diff(g, r0, r1)
         diff(e, 0, 1)
-        for r in LATE_PRODS:
-            neg(g, r)
-        open_sum(g)
-        summ(g, [ntile[(g, r)][:, 0, :] for r in LATE_PRODS], False, False)
-        for r in LATE_PRODS:
-            mul(g, r, r + 1)
-            summ(g, [ytile[g][:, r, :]], False, False)
-        mul(g, 2, 3)
-        summ(g, [ytile[g][:, 2, :]], False, False)
-        summ(e, [btile[e][:, r, :] for r in range(4)], True, False)
-        neg(e, 1)
-        mul(g, 3, 4)
-        summ(g, [ytile[g][:, 3, :]], False, True)
-        neg(e, 2)
-        neg(e, 3)
-        summ(e, [ntile[(e, r)][:, 0, :] for r in END_PRODS], False, False)
         for r in (1, 0, 2):
             mul(e, r, r + 1)
             summ(e, [ytile[e][:, r, :]], False, False)
-        while pending:
-            red(pending.pop(0))
+        red(e - 1)
         mul(e, 3, 4)
         summ(e, [ytile[e][:, 3, :]], False, True)
         red(e)
-        nc.sync.dma_start(out=out_v[:, :, 8 * (NBLK - BB):], in_=res[:, :, 8 * (NBLK - BB):])
+        nc.sync.dma_start(out=out_v[:, :, 4 * NBLK:], in_=res[:, :, 4 * NBLK:])

@@ -35,13 +35,11 @@ MX_BANKS = (0, 1, 2, 7)
 IMG_BANKS = ((3, 4), (5, 6), (0, 1))
 SUM_BANKS = (2, 7)
 
-FIRST_DIFFS = ((2, 4), (0, 2))
-PRODS = (0,)
-DIFFS = ((2, 4), (1, 2))
-LATE_PRODS = (0, 1)
-LATE_DIFFS = ((2, 3), (3, 4))
-END_PRODS = (1, 2, 3)
-END_DIFFS = ((0, 1),)
+EVEN = (((0, 2),), (), ((2, 4),))
+ODD = (((1, 2),), (0,), ((2, 4),))
+LATE = ((), (0, 1), ((2, 3), (3, 4)))
+LAST = ((), (1, 2, 3), ((0, 1),))
+PLAIN_EVERY = 5
 
 FLOPS = 2 * TOK * (128 * HN + HN * HN + HN * CH)
 
@@ -233,16 +231,24 @@ def tile_decoder_kernel(tc, digits, styles, images, W_h, b_h, W1, b1, W2, b2, ou
                                            scalar=-1.0, in1=image(b, r, r + 1),
                                            op0=ALU.mult, op1=ALU.mult)
 
+        def neg_rest(b, r0, r1):
+            nc.vector.scalar_tensor_tensor(out=btile[b][:, r0:r1, :], in0=image(b, r0, r1), scalar=1.0,
+                                           in1=btile[b][:, r0:r1, :],
+                                           op0=ALU.subtract, op1=ALU.mult)
+
+        passes = [0]
+
         def summ(b, arrays, first, last):
             if first:
                 stile[b] = bank(SUM_BANKS[b % 2], [P, TOK], F32, "st")
             for n, src in enumerate(arrays):
                 for t in range(NT):
+                    passes[0] = passes[0] + 1
                     nc.tensor.matmul(
                         out=stile[b][:, t * P:(t + 1) * P],
                         lhsT=src[:, t * P:(t + 1) * P],
                         rhs=ident_f[:],
-                        is_transpose=True,
+                        is_transpose=(passes[0] % PLAIN_EVERY != 0),
                         start=(first and n == 0 and t == 0),
                         stop=(last and n == len(arrays) - 1 and t == NT - 1),
                     )
@@ -264,7 +270,7 @@ def tile_decoder_kernel(tc, digits, styles, images, W_h, b_h, W1, b1, W2, b2, ou
             for n in range(count):
                 nc.tensor.matmul(out=idle_ps[:], lhsT=idle[:, 0:P], rhs=idle[:], start=True, stop=True)
 
-        idle_mm(4)
+        idle_mm(1)
         cat_ps = bank(3, [P, TOK], BF16, "cat_ps")
         for t in range(NT):
             nc.tensor.transpose(out=cat_ps[:, t * P:(t + 1) * P], in_=cat[:, t, :],
@@ -333,7 +339,7 @@ def tile_decoder_kernel(tc, digits, styles, images, W_h, b_h, W1, b1, W2, b2, ou
         tg = slot(16, [P, 4 * TOK], BF16, "tg")
         t_codes = const.tile([P, TOK], U32, name="t_codes", align_bytes=64)
         t_plane = const.tile([P, TOK], U8, name="t_plane", align_bytes=64)
-        idle_mm(6)
+        idle_mm(1)
         tps = [bank(MX_BANKS[m], [P, TOK], F32, "tp") for m in range(4)]
         for m in range(4):
             nc.tensor.matmul_mx(
@@ -378,19 +384,22 @@ def tile_decoder_kernel(tc, digits, styles, images, W_h, b_h, W1, b1, W2, b2, ou
 
         forms = {}
         for g in range(NBLK):
-            forms[g] = (PRODS, DIFFS)
-        for g in range(4):
-            forms[g] = ((), FIRST_DIFFS)
-        forms[NBLK - 2] = (LATE_PRODS, LATE_DIFFS)
-        forms[NBLK - 1] = (END_PRODS, END_DIFFS)
+            forms[g] = ODD if g % 2 == 1 and g > 4 else EVEN
+        forms[NBLK - 2] = LATE
+        forms[NBLK - 1] = LAST
 
-        def negs(h):
-            for r in forms[h][0]:
+        def early_products(h):
+            units, prods, diffs = forms[h]
+            for r in prods:
                 neg(h, r)
+            for (r0, r1) in units:
+                neg_rest(h, r0, r1)
 
         def open_sum(h):
-            summ(h, [btile[h][:, r, :] for r in range(4)]
-                 + [ntile[h][:, r, :] for r in forms[h][0]], True, False)
+            units, prods, diffs = forms[h]
+            summed = list(prods) + [r for (r0, r1) in diffs for r in range(r0, r1)]
+            summ(h, [btile[h][:, r, :] for r in summed]
+                 + [ntile[h][:, r, :] for r in prods], True, False)
 
         for b in range(NBLK):
             for r in range(4):
@@ -402,10 +411,10 @@ def tile_decoder_kernel(tc, digits, styles, images, W_h, b_h, W1, b1, W2, b2, ou
         imgt(2)
 
         log_b(0)
-        negs(0)
+        early_products(0)
         open_sum(0)
         for g in range(NBLK - 1):
-            prods, diffs = forms[g]
+            units, prods, diffs = forms[g]
             if g > 0:
                 log_b(g + 1)
             log_a(g)
@@ -416,16 +425,19 @@ def tile_decoder_kernel(tc, digits, styles, images, W_h, b_h, W1, b1, W2, b2, ou
                     log_a(NBLK - 1, r, r + 1)
             for (r0, r1) in diffs:
                 diff(g, r0, r1)
-            negs(g + 1)
+            early_products(g + 1)
             if g > 0:
                 red(g - 1)
+            for (r0, r1) in units:
+                mul(g, r0, r1)
+                diff(g, r0, r1)
             for r in prods:
                 mul(g, r, r + 1)
             for (r0, r1) in diffs:
                 mul(g, r0, r1)
             open_sum(g + 1)
-            summ(g, [ytile[g][:, r, :] for r in prods]
-                 + [ytile[g][:, r, :] for (r0, r1) in diffs for r in range(r0, r1)], False, True)
+            late = list(prods) + [r for (r0, r1) in diffs + units for r in range(r0, r1)]
+            summ(g, [ytile[g][:, r, :] for r in late], False, True)
             if g + 3 < NBLK:
                 imgt(g + 3)
             if g == NBLK // 2:

@@ -32,8 +32,8 @@ NCODE = 3
 RAW_SLOTS = (22, 23, 24, 25)
 GROUP_SLOTS = (21, 26)
 MX_BANKS = (0, 1, 2, 7)
-IMG_BANKS = ((3, 4), (5, 6), (0, 1))
-SUM_BANKS = (2, 7)
+IMG_BANKS = ((3, 4), (5, 6))
+SUM_BANKS = (0, 1, 2, 7)
 
 EVEN = (((0, 2),), (), ((2, 4),))
 ODD = (((1, 2),), (0,), ((2, 4),))
@@ -197,7 +197,7 @@ def tile_decoder_kernel(tc, digits, styles, images, W_h, b_h, W1, b1, W2, b2, ou
 
         def imgt(b):
             for s in range(2):
-                it = bank(IMG_BANKS[b % 3][s], [P, TOK], F32, "it")
+                it = bank(IMG_BANKS[b % 2][s], [P, TOK], F32, "it")
                 for t in range(NT):
                     words = imgs[b][:, t, :].bitcast(F32)
                     nc.tensor.transpose(
@@ -239,8 +239,10 @@ def tile_decoder_kernel(tc, digits, styles, images, W_h, b_h, W1, b1, W2, b2, ou
         passes = [0]
 
         def summ(b, arrays, first, last):
+            if not arrays:
+                return
             if first:
-                stile[b] = bank(SUM_BANKS[b % 2], [P, TOK], F32, "st")
+                stile[b] = bank(SUM_BANKS[b % 4], [P, TOK], F32, "st")
             for n, src in enumerate(arrays):
                 for t in range(NT):
                     passes[0] = passes[0] + 1
@@ -408,7 +410,12 @@ def tile_decoder_kernel(tc, digits, styles, images, W_h, b_h, W1, b1, W2, b2, ou
             prep_to(b + NCODE)
             if b in (3, 6):
                 imgt(b // 3 - 1)
-        imgt(2)
+
+        def spread(parts):
+            return [r for (r0, r1) in parts for r in range(r0, r1)]
+
+        def close_sum(h):
+            summ(h, [ytile[h][:, r, :] for r in spread(forms[h][0])], False, True)
 
         log_b(0)
         early_products(0)
@@ -425,28 +432,30 @@ def tile_decoder_kernel(tc, digits, styles, images, W_h, b_h, W1, b1, W2, b2, ou
                     log_a(NBLK - 1, r, r + 1)
             for (r0, r1) in diffs:
                 diff(g, r0, r1)
-            early_products(g + 1)
-            if g > 0:
-                red(g - 1)
             for (r0, r1) in units:
                 mul(g, r0, r1)
                 diff(g, r0, r1)
             for r in prods:
                 mul(g, r, r + 1)
+            if g > 1:
+                red(g - 2)
             for (r0, r1) in diffs:
                 mul(g, r0, r1)
+            early_products(g + 1)
+            if g > 0:
+                close_sum(g - 1)
+            summ(g, [ytile[g][:, r, :] for r in list(prods) + spread(diffs)], False, not units)
+            if g + 2 < NBLK:
+                imgt(g + 2)
             open_sum(g + 1)
-            late = list(prods) + [r for (r0, r1) in diffs + units for r in range(r0, r1)]
-            summ(g, [ytile[g][:, r, :] for r in late], False, True)
-            if g + 3 < NBLK:
-                imgt(g + 3)
-            if g == NBLK // 2:
+            if g == NBLK // 2 + 1:
                 nc.sync.dma_start(out=out_v[:, :, 0:4 * NBLK], in_=res[:, :, 0:4 * NBLK])
         e = NBLK - 1
         diff(e, 0, 1)
         for r in (1, 0, 2):
             mul(e, r, r + 1)
             summ(e, [ytile[e][:, r, :]], False, False)
+        red(e - 2)
         red(e - 1)
         mul(e, 3, 4)
         summ(e, [ytile[e][:, 3, :]], False, True)

@@ -39,7 +39,6 @@ EVEN = (((0, 2),), (), ((2, 4),))
 ODD = (((1, 2),), (0,), ((2, 4),))
 LATE = ((), (0, 1), ((2, 3), (3, 4)))
 LAST = ((), (1, 2, 3), ((0, 1),))
-PLAIN_EVERY = 5
 
 FLOPS = 2 * TOK * (128 * HN + HN * HN + HN * CH)
 
@@ -236,8 +235,6 @@ def tile_decoder_kernel(tc, digits, styles, images, W_h, b_h, W1, b1, W2, b2, ou
                                            in1=btile[b][:, r0:r1, :],
                                            op0=ALU.subtract, op1=ALU.mult)
 
-        passes = [0]
-
         def summ(b, arrays, first, last):
             if not arrays:
                 return
@@ -245,12 +242,11 @@ def tile_decoder_kernel(tc, digits, styles, images, W_h, b_h, W1, b1, W2, b2, ou
                 stile[b] = bank(SUM_BANKS[b % 4], [P, TOK], F32, "st")
             for n, src in enumerate(arrays):
                 for t in range(NT):
-                    passes[0] = passes[0] + 1
                     nc.tensor.matmul(
                         out=stile[b][:, t * P:(t + 1) * P],
                         lhsT=src[:, t * P:(t + 1) * P],
                         rhs=ident_f[:],
-                        is_transpose=(passes[0] % PLAIN_EVERY != 0),
+                        is_transpose=True,
                         start=(first and n == 0 and t == 0),
                         stop=(last and n == len(arrays) - 1 and t == NT - 1),
                     )
@@ -272,7 +268,7 @@ def tile_decoder_kernel(tc, digits, styles, images, W_h, b_h, W1, b1, W2, b2, ou
             for n in range(count):
                 nc.tensor.matmul(out=idle_ps[:], lhsT=idle[:, 0:P], rhs=idle[:], start=True, stop=True)
 
-        idle_mm(1)
+        idle_mm(4)
         cat_ps = bank(3, [P, TOK], BF16, "cat_ps")
         for t in range(NT):
             nc.tensor.transpose(out=cat_ps[:, t * P:(t + 1) * P], in_=cat[:, t, :],
@@ -341,7 +337,7 @@ def tile_decoder_kernel(tc, digits, styles, images, W_h, b_h, W1, b1, W2, b2, ou
         tg = slot(16, [P, 4 * TOK], BF16, "tg")
         t_codes = const.tile([P, TOK], U32, name="t_codes", align_bytes=64)
         t_plane = const.tile([P, TOK], U8, name="t_plane", align_bytes=64)
-        idle_mm(1)
+        idle_mm(6)
         tps = [bank(MX_BANKS[m], [P, TOK], F32, "tp") for m in range(4)]
         for m in range(4):
             nc.tensor.matmul_mx(

@@ -27,18 +27,12 @@ SELU_ALPHA = 1.6732632423543772848170429916717
 SELU_SCALE = 1.0507009873554804934193349852946
 SA = SELU_SCALE * SELU_ALPHA
 
-NSLOT = NBLK + 3
+BATCHES = ((0, 24),)
+NBIG = 27
 NCODE = 3
-RAW_SLOTS = (22, 23, 24, 25)
-GROUP_SLOTS = (21, 26)
-MX_BANKS = (0, 1, 2, 7)
-IMG_BANKS = ((3, 4), (5, 6))
-SUM_BANKS = (0, 1, 2, 7)
-
-EVEN = (((0, 2),), (), ((2, 4),))
-ODD = (((1, 2),), (0,), ((2, 4),))
-LATE = ((), (0, 1), ((2, 3), (3, 4)))
-LAST = ((), (1, 2, 3), ((0, 1),))
+AHEAD = 4
+LATE_FROM = 4
+TWO_SUMS = (7, 15, 23)
 
 FLOPS = 2 * TOK * (128 * HN + HN * HN + HN * CH)
 
@@ -59,12 +53,25 @@ def tile_decoder_kernel(tc, digits, styles, images, W_h, b_h, W1, b1, W2, b2, ou
         cp = ctx.enter_context(tc.tile_pool(name="cp", bufs=NCODE))
         imp = ctx.enter_context(tc.tile_pool(name="imp", bufs=2))
         psum = ctx.enter_context(tc.psum_pool(name="psum", bufs=1))
+        free_slots = list(range(NBIG))
+        free_banks = list(range(8))
+        mx_banks = []
+        slot_of = {}
+        bank_of = {}
 
-        def slot(s, shape, dtype, name):
-            return big.tile(shape, dtype, name=name, tag="s%d" % s, align_bytes=64)
+        def slot(key, shape, dtype, name):
+            slot_of[key] = free_slots.pop(0)
+            return big.tile(shape, dtype, name=name, tag="s%d" % slot_of[key], align_bytes=64)
 
-        def bank(k, shape, dtype, name):
-            return psum.tile(shape, dtype, name=name, tag="b%d" % k)
+        def slot_done(key):
+            free_slots.append(slot_of.pop(key))
+
+        def bank(key, shape, dtype, name, source=None):
+            bank_of[key] = (source or free_banks).pop(0)
+            return psum.tile(shape, dtype, name=name, tag="b%d" % bank_of[key])
+
+        def bank_done(key):
+            free_banks.append(bank_of.pop(key))
 
         raws = {}
         imgs = {}
@@ -76,21 +83,17 @@ def tile_decoder_kernel(tc, digits, styles, images, W_h, b_h, W1, b1, W2, b2, ou
         ytile = {}
         btile = {}
         itile = {}
-        ntile = {}
         stile = {}
-        bslot = {}
-        nslot = {}
-        free = [24, 25, 26]
 
         ident_bf = const.tile([P, P], BF16, name="ident_bf")
         masks.make_identity(nc, ident_bf[:])
         ident_f = const.tile([P, P], F32, name="ident_f")
         masks.make_identity(nc, ident_f[:])
-        idle = slot(17, [P, TOK], BF16, "idle")
+        idle = slot("idle", [P, TOK], BF16, "idle")
         nc.vector.memset(idle[:], 0.0)
-        brow = slot(7, [P, P], BF16, "brow")
+        brow = slot("brow", [P, P], BF16, "brow")
         nc.vector.memset(brow[:], 0.0)
-        b2rows = slot(8, [P, BLK], BF16, "b2rows")
+        b2rows = slot("b2rows", [P, BLK], BF16, "b2rows")
         nc.vector.memset(b2rows[:], 0.0)
         eps_b = const.tile([P, 1], F32, name="eps_b")
         nc.vector.memset(eps_b[:], EPS)
@@ -100,19 +103,19 @@ def tile_decoder_kernel(tc, digits, styles, images, W_h, b_h, W1, b1, W2, b2, ou
         warm = const.tile([P, 1], F32, name="warm")
         nc.scalar.activation(out=warm[:], in_=eps_b[:], func=ACT.Relu)
 
-        cat = slot(5, [P, NT, P], BF16, "cat")
+        cat = slot("cat", [P, NT, P], BF16, "cat")
         nc.sync.dma_start(out=cat[:, :, 0:32], in_=dig_v)
         nc.sync.dma_start(out=cat[:, :, 32:128], in_=sty_v)
-        wh = slot(6, [P, HN], BF16, "wh")
+        wh = slot("wh", [P, HN], BF16, "wh")
         nc.sync.dma_start(out=wh[:], in_=W_h)
         nc.sync.dma_start(out=brow[0:4, :], in_=b_h.rearrange("(j p) -> j p", p=P))
         nc.sync.dma_start(out=brow[4:8, :], in_=b1.rearrange("(j p) -> j p", p=P))
-        raw1 = slot(10, [P, 4, HN], BF16, "raw1")
+        raw1 = slot("raw1", [P, 4, HN], BF16, "raw1")
         nc.sync.dma_start(out=raw1[:], in_=w1_v)
         nc.sync.dma_start(out=b2rows[0:NBLK, :], in_=b2.rearrange("(b x) -> b x", x=BLK))
 
         def load_w2(c, parts=1):
-            raw = slot(RAW_SLOTS[c % 4], [P, 4, 2 * BLK], BF16, "raw")
+            raw = slot(("raw", c), [P, 4, 2 * BLK], BF16, "raw")
             width = 2 * BLK // parts
             for n in range(parts):
                 lo = n * width
@@ -121,23 +124,20 @@ def tile_decoder_kernel(tc, digits, styles, images, W_h, b_h, W1, b1, W2, b2, ou
             raws[c] = raw
 
         def load_img(b):
-            if b < 2:
-                im = slot(18 + b, [P, NT, BLK], BF16, "im_first")
-            else:
-                im = imp.tile([P, NT, BLK], BF16, name="im", tag="im")
+            im = imp.tile([P, NT, BLK], BF16, name="im", tag="im")
             nc.sync.dma_start(out=im[:], in_=img_v[:, :, b * BLK:(b + 1) * BLK])
             imgs[b] = im
 
         load_w2(0, parts=2)
-        for c in range(1, 4):
+        for c in range(1, AHEAD):
             load_w2(c)
-        for b in range(4):
+        for b in range(2):
             load_img(b)
 
         def prep_copy(b, on_scalar=False):
             c = b // 2
             if b % 2 == 0:
-                groups[c] = slot(GROUP_SLOTS[c % 2], [P, 2, 4 * BLK], BF16, "g2")
+                groups[c] = slot(("group", c), [P, 2, 4 * BLK], BF16, "g2")
             lo = (b % 2) * BLK
             dst = groups[c][:, b % 2, :].rearrange("p (s e q j) -> p s q j e", s=2, e=2, j=4)
             src = raws[c][:, :, lo:lo + BLK].rearrange("p j (q s e) -> p s q j e", s=2, e=2)
@@ -147,8 +147,10 @@ def tile_decoder_kernel(tc, digits, styles, images, W_h, b_h, W1, b1, W2, b2, ou
             else:
                 nc.vector.tensor_copy(out=dst, in_=src)
             grouped.add(b)
-            if b % 2 == 1 and c + 4 < NBLK // 2:
-                load_w2(c + 4)
+            if b % 2 == 1:
+                slot_done(("raw", c))
+                if c + AHEAD < NBLK // 2:
+                    load_w2(c + AHEAD)
 
         def prep_quant(b):
             cd = cp.tile([P, BLK], U32, name="cd", tag="cd", align_bytes=64)
@@ -156,6 +158,8 @@ def tile_decoder_kernel(tc, digits, styles, images, W_h, b_h, W1, b1, W2, b2, ou
             nc.vector.quantize_mx(out=cd[:].bitcast(FP8X4), scales=pl[:], in_=groups[b // 2][:, b % 2, :])
             codes[b] = cd
             planes[b] = pl
+            if b % 2 == 1:
+                slot_done(("group", b // 2))
 
         def prep_to(last):
             for b in range(len(codes), min(last + 1, NBLK)):
@@ -164,7 +168,7 @@ def tile_decoder_kernel(tc, digits, styles, images, W_h, b_h, W1, b1, W2, b2, ou
                 prep_quant(b)
 
         def mx(b, r):
-            u = bank(MX_BANKS[r], [P, TOK], F32, "u")
+            u = bank(("u", b, r), [P, TOK], F32, "u", mx_banks or free_banks)
             nc.tensor.matmul_mx(
                 out=u[:],
                 lhsT=codes[b][:, r * P:(r + 1) * P].bitcast(FP8X4),
@@ -176,17 +180,17 @@ def tile_decoder_kernel(tc, digits, styles, images, W_h, b_h, W1, b1, W2, b2, ou
             )
             ubank[(b, r)] = u
 
-        def sig(b, r):
+        def sig(b, r, ring):
             if r == 0:
-                ytile[b] = slot(b, [P, 4, TOK], F32, "y")
+                ytile[b] = slot(("y", b), [P, 4, TOK], F32, "y")
             nc.scalar.activation(
                 out=ytile[b][:, r, :], in_=ubank[(b, r)][:], func=ACT.Sigmoid,
                 bias=nb2[:, 4 * b + r:4 * b + r + 1], scale=-1.0,
             )
+            (mx_banks if ring else free_banks).append(bank_of.pop(("u", b, r)))
 
         def log_b(b):
-            bslot[b] = free.pop(0)
-            btile[b] = slot(bslot[b], [P, 4, TOK], F32, "bt")
+            btile[b] = slot(("b", b), [P, 4, TOK], F32, "bt")
             nc.scalar.activation(out=btile[b][:], in_=ytile[b][:], func=ACT.Ln,
                                  bias=eps_b[:, 0:1], scale=1.0)
 
@@ -194,18 +198,17 @@ def tile_decoder_kernel(tc, digits, styles, images, W_h, b_h, W1, b1, W2, b2, ou
             nc.scalar.activation(out=ytile[b][:, r0:r1, :], in_=ytile[b][:, r0:r1, :], func=ACT.Ln,
                                  bias=one_eps_b[:, 0:1], scale=-1.0)
 
-        def imgt(b):
-            for s in range(2):
-                it = bank(IMG_BANKS[b % 2][s], [P, TOK], F32, "it")
-                for t in range(NT):
-                    words = imgs[b][:, t, :].bitcast(F32)
-                    nc.tensor.transpose(
-                        out=it[:, t * P:(t + 1) * P],
-                        in_=words.rearrange("p (q s) -> p s q", s=2)[:, s, :],
-                        identity=ident_f[:],
-                    )
-                itile[(b, s)] = it
-            if b >= 2 and b + 2 < NBLK:
+        def imgt(b, s):
+            it = bank(("i", b, s), [P, TOK], F32, "it")
+            for t in range(NT):
+                words = imgs[b][:, t, :].bitcast(F32)
+                nc.tensor.transpose(
+                    out=it[:, t * P:(t + 1) * P],
+                    in_=words.rearrange("p (q s) -> p s q", s=2)[:, s, :],
+                    identity=ident_f[:],
+                )
+            itile[(b, s)] = it
+            if s == 1 and b + 2 < NBLK:
                 load_img(b + 2)
 
         def image(b, r0, r1):
@@ -222,60 +225,60 @@ def tile_decoder_kernel(tc, digits, styles, images, W_h, b_h, W1, b1, W2, b2, ou
                                            scalar=D_MIN, in1=image(b, r0, r1),
                                            op0=ALU.max, op1=ALU.mult)
 
-        def neg(b, r):
-            if b not in ntile:
-                nslot[b] = free.pop(0)
-                ntile[b] = slot(nslot[b], [P, 4, TOK], F32, "nt")
-            nc.vector.scalar_tensor_tensor(out=ntile[b][:, r:r + 1, :], in0=btile[b][:, r:r + 1, :],
-                                           scalar=-1.0, in1=image(b, r, r + 1),
-                                           op0=ALU.mult, op1=ALU.mult)
-
         def neg_rest(b, r0, r1):
             nc.vector.scalar_tensor_tensor(out=btile[b][:, r0:r1, :], in0=image(b, r0, r1), scalar=1.0,
                                            in1=btile[b][:, r0:r1, :],
                                            op0=ALU.subtract, op1=ALU.mult)
 
-        def summ(b, arrays, first, last):
-            if not arrays:
-                return
-            if first:
-                stile[b] = bank(SUM_BANKS[b % 4], [P, TOK], F32, "st")
+        def summ(b, arrays, sign="+", last=False):
+            fresh = (b, sign) not in stile
+            if fresh:
+                stile[(b, sign)] = bank(("s", b, sign), [P, TOK], F32, "st")
             for n, src in enumerate(arrays):
                 for t in range(NT):
                     nc.tensor.matmul(
-                        out=stile[b][:, t * P:(t + 1) * P],
+                        out=stile[(b, sign)][:, t * P:(t + 1) * P],
                         lhsT=src[:, t * P:(t + 1) * P],
                         rhs=ident_f[:],
                         is_transpose=True,
-                        start=(first and n == 0 and t == 0),
+                        start=(fresh and n == 0 and t == 0),
                         stop=(last and n == len(arrays) - 1 and t == NT - 1),
                     )
-            if last:
-                free.extend([b, bslot[b]])
-                if b in nslot:
-                    free.append(nslot[b])
 
-        def red(b):
+        def block_done(b):
+            slot_done(("y", b))
+            slot_done(("b", b))
+
+        def red(b, sign="+"):
+            dst = res[:, :, 8 * b:8 * b + 8] if sign == "+" else minus[:]
             nc.vector.tensor_reduce(
-                out=res[:, :, 8 * b:8 * b + 8],
-                in_=stile[b][:].rearrange("p (t g w) -> p t g w", t=NT, g=8),
-                axis=AX.X, op=ALU.add, negate=True,
+                out=dst,
+                in_=stile[(b, sign)][:].rearrange("p (t g w) -> p t g w", t=NT, g=8),
+                axis=AX.X, op=ALU.add, negate=(sign == "+"),
             )
+            bank_done(("s", b, sign))
 
-        idle_ps = bank(6, [P, TOK], F32, "idle_ps")
+        def red_all(b):
+            red(b)
+            if b in TWO_SUMS:
+                red(b, "-")
+                nc.vector.tensor_tensor(out=res[:, :, 8 * b:8 * b + 8], in0=res[:, :, 8 * b:8 * b + 8],
+                                        in1=minus[:], op=ALU.add)
+
+        idle_ps = bank("idle", [P, TOK], F32, "idle_ps")
 
         def idle_mm(count):
             for n in range(count):
                 nc.tensor.matmul(out=idle_ps[:], lhsT=idle[:, 0:P], rhs=idle[:], start=True, stop=True)
 
         idle_mm(4)
-        cat_ps = bank(3, [P, TOK], BF16, "cat_ps")
+        cat_ps = bank("cat", [P, TOK], BF16, "cat_ps")
         for t in range(NT):
             nc.tensor.transpose(out=cat_ps[:, t * P:(t + 1) * P], in_=cat[:, t, :],
                                 identity=ident_bf[:])
-        cat_t = slot(9, [P, TOK], BF16, "cat_t")
+        cat_t = slot("cat_t", [P, TOK], BF16, "cat_t")
         nc.vector.tensor_copy(out=cat_t[:], in_=cat_ps[:])
-        bias_ps = bank(4, [P, P], BF16, "bias_ps")
+        bias_ps = bank("bias", [P, P], BF16, "bias_ps")
         nc.tensor.transpose(out=bias_ps[:], in_=brow[:], identity=ident_bf[:])
         bh = const.tile([P, 4], F32, name="bh")
         nc.vector.tensor_copy(out=bh[:], in_=bias_ps[:, 0:4])
@@ -290,11 +293,11 @@ def tile_decoder_kernel(tc, digits, styles, images, W_h, b_h, W1, b1, W2, b2, ou
                 in_=src[:].rearrange("p t (c i) -> p c t i", i=4),
             )
 
-        w1g = slot(11, [P, 4 * HN], BF16, "w1g")
+        w1g = slot("w1g", [P, 4 * HN], BF16, "w1g")
         regroup(w1g, raw1)
-        h_sb = slot(12, [P, 4, TOK], BF16, "h_sb")
+        h_sb = slot("h_sb", [P, 4, TOK], BF16, "h_sb")
         for j in range(4):
-            hp = bank((0, 1, 2, 7)[j], [P, TOK], F32, "hp")
+            hp = bank(("h", j), [P, TOK], F32, "hp")
             nc.tensor.matmul(out=hp[:], lhsT=wh[:, j * P:(j + 1) * P], rhs=cat_t[:],
                              start=True, stop=True)
             if j < 3:
@@ -303,18 +306,19 @@ def tile_decoder_kernel(tc, digits, styles, images, W_h, b_h, W1, b1, W2, b2, ou
             else:
                 nc.vector.tensor_scalar(out=h_sb[:, j, :], in0=hp[:], scalar1=bh[:, j:j + 1],
                                         scalar2=0.0, op0=ALU.add, op1=ALU.max)
+            bank_done(("h", j))
 
         w1_codes = cp.tile([P, HN], U32, name="w1_codes", tag="cd", align_bytes=64)
         w1_plane = cp.tile([P, HN], U8, name="w1_plane", tag="pl", align_bytes=64)
         nc.vector.quantize_mx(out=w1_codes[:].bitcast(FP8X4), scales=w1_plane[:], in_=w1g[:])
 
-        hg = slot(13, [P, 4 * TOK], BF16, "hg")
+        hg = slot("hg", [P, 4 * TOK], BF16, "hg")
         regroup(hg, h_sb)
         h_codes = cp.tile([P, TOK], U32, name="h_codes", tag="cd", align_bytes=64)
         h_plane = cp.tile([P, TOK], U8, name="h_plane", tag="pl", align_bytes=64)
         nc.vector.quantize_mx(out=h_codes[:].bitcast(FP8X4), scales=h_plane[:], in_=hg[:])
 
-        b2_ps = bank(5, [P, 2 * P], F32, "b2_ps")
+        b2_ps = bank("b2", [P, 2 * P], F32, "b2_ps")
         for s in range(2):
             nc.tensor.transpose(
                 out=b2_ps[:, s * P:(s + 1) * P],
@@ -332,13 +336,15 @@ def tile_decoder_kernel(tc, digits, styles, images, W_h, b_h, W1, b1, W2, b2, ou
 
         prep_copy(0, on_scalar=True)
         prep_quant(0)
-        e_sb = slot(14, [P, 4, TOK], F32, "e_sb")
-        r_sb = slot(15, [P, 4, TOK], F32, "r_sb")
-        tg = slot(16, [P, 4 * TOK], BF16, "tg")
+        e_sb = slot("e_sb", [P, 4, TOK], F32, "e_sb")
+        r_sb = slot("r_sb", [P, 4, TOK], F32, "r_sb")
+        tg = slot("tg", [P, 4 * TOK], BF16, "tg")
         t_codes = const.tile([P, TOK], U32, name="t_codes", align_bytes=64)
         t_plane = const.tile([P, TOK], U8, name="t_plane", align_bytes=64)
         idle_mm(6)
-        tps = [bank(MX_BANKS[m], [P, TOK], F32, "tp") for m in range(4)]
+        for key in ("cat", "bias", "b2", "idle"):
+            bank_done(key)
+        tps = [bank(("t", m), [P, TOK], F32, "tp") for m in range(4)]
         for m in range(4):
             nc.tensor.matmul_mx(
                 out=tps[m][:],
@@ -373,87 +379,129 @@ def tile_decoder_kernel(tc, digits, styles, images, W_h, b_h, W1, b1, W2, b2, ou
             cols = slice(h * HALF, (h + 1) * HALF)
             nc.vector.quantize_mx(out=t_codes[:, cols].bitcast(FP8X4), scales=t_plane[:, cols],
                                   in_=tg[:, 4 * h * HALF:4 * (h + 1) * HALF])
+        for m in range(4):
+            bank_done(("t", m))
+        for key in ("idle", "brow", "b2rows", "cat", "wh", "raw1", "cat_t", "w1g", "h_sb", "hg", "e_sb", "r_sb", "tg"):
+            slot_done(key)
         prep_copy(1)
         prep_quant(1)
         prep_copy(2)
         prep_to(2)
 
         res = const.tile([P, NT, CH // 64], F32, name="res")
+        minus = const.tile([P, NT, 8], F32, name="minus")
 
-        forms = {}
-        for g in range(NBLK):
-            forms[g] = ODD if g % 2 == 1 and g > 4 else EVEN
-        forms[NBLK - 2] = LATE
-        forms[NBLK - 1] = LAST
+        end = NBLK - 1
 
-        def early_products(h):
-            units, prods, diffs = forms[h]
-            for r in prods:
-                neg(h, r)
-            for (r0, r1) in units:
-                neg_rest(h, r0, r1)
+        def rows(tiles, b, r0, r1):
+            return [tiles[b][:, r, :] for r in range(r0, r1)]
 
-        def open_sum(h):
-            units, prods, diffs = forms[h]
-            summed = list(prods) + [r for (r0, r1) in diffs for r in range(r0, r1)]
-            summ(h, [btile[h][:, r, :] for r in summed]
-                 + [ntile[h][:, r, :] for r in prods], True, False)
+        def early(h):
+            neg_rest(h, 0, 2)
+            if h in TWO_SUMS:
+                neg_rest(h, 2, 4)
 
-        for b in range(NBLK):
-            for r in range(4):
-                mx(b, r)
-                sig(b, r)
-            prep_to(b + NCODE)
-            if b in (3, 6):
-                imgt(b // 3 - 1)
+        def sum_early(h):
+            if h in TWO_SUMS:
+                summ(h, rows(btile, h, 0, 4), sign="-", last=True)
+            else:
+                summ(h, rows(btile, h, 2, 4))
 
-        def spread(parts):
-            return [r for (r0, r1) in parts for r in range(r0, r1)]
+        def sum_unit(h):
+            summ(h, rows(ytile, h, 0, 2), last=True)
+            block_done(h)
 
-        def close_sum(h):
-            summ(h, [ytile[h][:, r, :] for r in spread(forms[h][0])], False, True)
-
-        log_b(0)
-        early_products(0)
-        open_sum(0)
-        for g in range(NBLK - 1):
-            units, prods, diffs = forms[g]
-            if g > 0:
-                log_b(g + 1)
-            log_a(g)
-            if g == 0:
-                log_b(1)
-            if g == NBLK - 2:
+        issued = 0
+        late = []
+        for (lo, hi) in BATCHES:
+            for b in range(lo, hi):
                 for r in range(4):
-                    log_a(NBLK - 1, r, r + 1)
-            for (r0, r1) in diffs:
-                diff(g, r0, r1)
-            for (r0, r1) in units:
-                mul(g, r0, r1)
-                diff(g, r0, r1)
-            for r in prods:
-                mul(g, r, r + 1)
-            if g > 1:
-                red(g - 2)
-            for (r0, r1) in diffs:
-                mul(g, r0, r1)
-            early_products(g + 1)
-            if g > 0:
-                close_sum(g - 1)
-            summ(g, [ytile[g][:, r, :] for r in list(prods) + spread(diffs)], False, not units)
-            if g + 2 < NBLK:
-                imgt(g + 2)
-            open_sum(g + 1)
-            if g == NBLK // 2 + 1:
-                nc.sync.dma_start(out=out_v[:, :, 0:4 * NBLK], in_=res[:, :, 0:4 * NBLK])
-        e = NBLK - 1
-        diff(e, 0, 1)
-        for r in (1, 0, 2):
-            mul(e, r, r + 1)
-            summ(e, [ytile[e][:, r, :]], False, False)
-        red(e - 2)
-        red(e - 1)
-        mul(e, 3, 4)
-        summ(e, [ytile[e][:, 3, :]], False, True)
-        red(e)
-        nc.sync.dma_start(out=out_v[:, :, 4 * NBLK:], in_=res[:, :, 4 * NBLK:])
+                    if 4 * b + r >= issued:
+                        mx(b, r)
+                        issued = 4 * b + r + 1
+                    sig(b, r, late)
+                prep_to(min(b + NCODE, NBLK - 1))
+                if late and b >= lo + LATE_FROM:
+                    late.pop(0)()
+                    if not late:
+                        free_banks.extend(mx_banks)
+                        mx_banks.clear()
+                if b == hi - 3:
+                    imgt(lo, 0)
+                    imgt(lo, 1)
+                if b == hi - 2:
+                    imgt(lo + 1, 0)
+                    imgt(lo + 1, 1)
+            log_b(lo)
+            early(lo)
+            for g in range(lo, min(hi, end)):
+                if g > lo and g + 1 < hi:
+                    log_b(g + 1)
+                log_a(g)
+                if g == lo:
+                    log_b(g + 1)
+                if g == end - 1:
+                    for r in range(4):
+                        log_a(end, r, r + 1)
+                if g in TWO_SUMS:
+                    mul(g, 0, 2)
+                    bank_done(("i", g, 0))
+                    early(g + 1)
+                else:
+                    diff(g, 2, 4)
+                    mul(g, 0, 2)
+                    diff(g, 0, 2)
+                    bank_done(("i", g, 0))
+                    if g + 1 < hi:
+                        early(g + 1)
+                if g - 2 >= lo:
+                    red_all(g - 2)
+                if g == end - 1:
+                    mul(end, 0, 1)
+                    mul(end, 1, 2)
+                mul(g, 2, 4)
+                bank_done(("i", g, 1))
+                if hi < NBLK and g == hi - 1:
+                    late.append(lambda h=g: (sum_unit(h - 1), sum_early(h)))
+                    late.append(lambda h=g: (red_all(h - 1), summ(h, rows(ytile, h, 2, 4))))
+                    late.append(lambda h=g: sum_unit(h))
+                    late.append(lambda h=g: red_all(h))
+                    continue
+                if hi < NBLK and g == hi - 2:
+                    mx_banks.extend(free_banks[:3])
+                    for k in mx_banks:
+                        free_banks.remove(k)
+                    for r in range(3):
+                        mx(hi, r)
+                    issued = 4 * hi + 3
+                if g > lo:
+                    sum_unit(g - 1)
+                sum_early(g)
+                if g == end - 1:
+                    sum_early(end)
+                if g + 2 < hi:
+                    imgt(g + 2, 0)
+                if hi < NBLK and g == hi - 2:
+                    late.append(lambda h=g: summ(h, rows(ytile, h, 2, 4)))
+                else:
+                    summ(g, rows(ytile, g, 2, 4))
+                if g + 2 < hi:
+                    imgt(g + 2, 1)
+                if g == lo + 8 and lo == 0:
+                    nc.sync.dma_start(out=out_v[:, :, 0:48], in_=res[:, :, 0:48])
+                if g == lo + 16:
+                    nc.sync.dma_start(out=out_v[:, :, 48:8 * (g - 2)], in_=res[:, :, 48:8 * (g - 2)])
+                    stored = g - 2
+        summ(end, rows(ytile, end, 0, 2))
+        mul(end, 2, 3)
+        mul(end, 3, 4)
+        summ(end, rows(ytile, end, 2, 3))
+        sum_unit(end - 1)
+        red_all(end - 2)
+        red(end, "-")
+        summ(end, rows(ytile, end, 3, 4), last=True)
+        red(end - 1)
+        red(end)
+        nc.vector.tensor_tensor(out=res[:, :, 8 * end:8 * end + 8], in0=res[:, :, 8 * end:8 * end + 8],
+                                in1=minus[:], op=ALU.add)
+        nc.sync.dma_start(out=out_v[:, :, 8 * stored:], in_=res[:, :, 8 * stored:])

@@ -27,12 +27,11 @@ SELU_ALPHA = 1.6732632423543772848170429916717
 SELU_SCALE = 1.0507009873554804934193349852946
 SA = SELU_SCALE * SELU_ALPHA
 
-BATCHES = ((0, 24),)
-NBIG = 27
+NBIG = 28
 NCODE = 3
 AHEAD = 4
-LATE_FROM = 4
-TWO_SUMS = (7, 15, 23)
+FORMS = ["uudd", "uuud"] * 11 + ["uudd", "tttt"]
+LAG = 2
 
 FLOPS = 2 * TOK * (128 * HN + HN * HN + HN * CH)
 
@@ -50,12 +49,10 @@ def tile_decoder_kernel(tc, digits, styles, images, W_h, b_h, W1, b1, W2, b2, ou
         ctx.enter_context(tc.manual_schedule())
         const = ctx.enter_context(tc.tile_pool(name="const", bufs=1))
         big = ctx.enter_context(tc.tile_pool(name="big", bufs=1))
-        cp = ctx.enter_context(tc.tile_pool(name="cp", bufs=NCODE))
         imp = ctx.enter_context(tc.tile_pool(name="imp", bufs=2))
         psum = ctx.enter_context(tc.psum_pool(name="psum", bufs=1))
         free_slots = list(range(NBIG))
         free_banks = list(range(8))
-        mx_banks = []
         slot_of = {}
         bank_of = {}
 
@@ -84,8 +81,9 @@ def tile_decoder_kernel(tc, digits, styles, images, W_h, b_h, W1, b1, W2, b2, ou
         btile = {}
         itile = {}
         stile = {}
+        left = {}
 
-        ident_bf = const.tile([P, P], BF16, name="ident_bf")
+        ident_bf = slot("ident_bf", [P, P], BF16, "ident_bf")
         masks.make_identity(nc, ident_bf[:])
         ident_f = const.tile([P, P], F32, name="ident_f")
         masks.make_identity(nc, ident_f[:])
@@ -134,6 +132,13 @@ def tile_decoder_kernel(tc, digits, styles, images, W_h, b_h, W1, b1, W2, b2, ou
         for b in range(2):
             load_img(b)
 
+        code_words = slot("codes", [P, NCODE * BLK * 5 // 4], U32, "code_words")
+
+        def code_room(n):
+            words = code_words[:, n * BLK:(n + 1) * BLK]
+            lo = NCODE * BLK + n * BLK // 4
+            return words, code_words[:, lo:lo + BLK // 4].bitcast(U8)
+
         def prep_copy(b, on_scalar=False):
             c = b // 2
             if b % 2 == 0:
@@ -153,11 +158,8 @@ def tile_decoder_kernel(tc, digits, styles, images, W_h, b_h, W1, b1, W2, b2, ou
                     load_w2(c + AHEAD)
 
         def prep_quant(b):
-            cd = cp.tile([P, BLK], U32, name="cd", tag="cd", align_bytes=64)
-            pl = cp.tile([P, BLK], U8, name="pl", tag="pl", align_bytes=64)
-            nc.vector.quantize_mx(out=cd[:].bitcast(FP8X4), scales=pl[:], in_=groups[b // 2][:, b % 2, :])
-            codes[b] = cd
-            planes[b] = pl
+            codes[b], planes[b] = code_room(b % NCODE)
+            nc.vector.quantize_mx(out=codes[b].bitcast(FP8X4), scales=planes[b], in_=groups[b // 2][:, b % 2, :])
             if b % 2 == 1:
                 slot_done(("group", b // 2))
 
@@ -168,7 +170,7 @@ def tile_decoder_kernel(tc, digits, styles, images, W_h, b_h, W1, b1, W2, b2, ou
                 prep_quant(b)
 
         def mx(b, r):
-            u = bank(("u", b, r), [P, TOK], F32, "u", mx_banks or free_banks)
+            u = bank(("u", b, r), [P, TOK], F32, "u", free_banks)
             nc.tensor.matmul_mx(
                 out=u[:],
                 lhsT=codes[b][:, r * P:(r + 1) * P].bitcast(FP8X4),
@@ -180,18 +182,19 @@ def tile_decoder_kernel(tc, digits, styles, images, W_h, b_h, W1, b1, W2, b2, ou
             )
             ubank[(b, r)] = u
 
-        def sig(b, r, ring):
+        def sig(b, r):
             if r == 0:
                 ytile[b] = slot(("y", b), [P, 4, TOK], F32, "y")
             nc.scalar.activation(
                 out=ytile[b][:, r, :], in_=ubank[(b, r)][:], func=ACT.Sigmoid,
                 bias=nb2[:, 4 * b + r:4 * b + r + 1], scale=-1.0,
             )
-            (mx_banks if ring else free_banks).append(bank_of.pop(("u", b, r)))
+            bank_done(("u", b, r))
 
-        def log_b(b):
-            btile[b] = slot(("b", b), [P, 4, TOK], F32, "bt")
-            nc.scalar.activation(out=btile[b][:], in_=ytile[b][:], func=ACT.Ln,
+        def log_b(b, r0=0, r1=4):
+            if r0 == 0:
+                btile[b] = slot(("b", b), [P, 4, TOK], F32, "bt")
+            nc.scalar.activation(out=btile[b][:, r0:r1, :], in_=ytile[b][:, r0:r1, :], func=ACT.Ln,
                                  bias=eps_b[:, 0:1], scale=1.0)
 
         def log_a(b, r0=0, r1=4):
@@ -230,20 +233,33 @@ def tile_decoder_kernel(tc, digits, styles, images, W_h, b_h, W1, b1, W2, b2, ou
                                            in1=btile[b][:, r0:r1, :],
                                            op0=ALU.subtract, op1=ALU.mult)
 
-        def summ(b, arrays, sign="+", last=False):
-            fresh = (b, sign) not in stile
+        def sums(b, tiles, r0, r1, sign="+"):
+            fresh = (b, sign) not in stile and r0 < r1
             if fresh:
                 stile[(b, sign)] = bank(("s", b, sign), [P, TOK], F32, "st")
-            for n, src in enumerate(arrays):
+                left[(b, sign)] = NT * (units(b)[1] + 2 * (diffs(b)[1] - diffs(b)[0]) + (twos(b)[1] - twos(b)[0])
+                                        if sign == "+" else twos(b)[1] - twos(b)[0])
+            for r in range(r0, r1):
                 for t in range(NT):
+                    left[(b, sign)] = left[(b, sign)] - 1
                     nc.tensor.matmul(
                         out=stile[(b, sign)][:, t * P:(t + 1) * P],
-                        lhsT=src[:, t * P:(t + 1) * P],
+                        lhsT=tiles[b][:, r, t * P:(t + 1) * P],
                         rhs=ident_f[:],
                         is_transpose=True,
-                        start=(fresh and n == 0 and t == 0),
-                        stop=(last and n == len(arrays) - 1 and t == NT - 1),
+                        start=fresh,
+                        stop=(left[(b, sign)] == 0),
                     )
+                    fresh = False
+
+        def units(b):
+            return (0, FORMS[b].count("u"))
+
+        def diffs(b):
+            return (units(b)[1], units(b)[1] + FORMS[b].count("d"))
+
+        def twos(b):
+            return (diffs(b)[1], 4)
 
         def block_done(b):
             slot_done(("y", b))
@@ -260,10 +276,31 @@ def tile_decoder_kernel(tc, digits, styles, images, W_h, b_h, W1, b1, W2, b2, ou
 
         def red_all(b):
             red(b)
-            if b in TWO_SUMS:
+            if "t" in FORMS[b]:
                 red(b, "-")
                 nc.vector.tensor_tensor(out=res[:, :, 8 * b:8 * b + 8], in0=res[:, :, 8 * b:8 * b + 8],
                                         in1=minus[:], op=ALU.add)
+
+        def spans(r0, r1):
+            if r0 < 2 < r1:
+                return [(r0, 2), (2, r1)]
+            return [(r0, r1)] if r0 < r1 else []
+
+        def rests(b):
+            for (r0, r1) in spans(*units(b)) + spans(*twos(b)):
+                neg_rest(b, r0, r1)
+
+        def products(b):
+            for (r0, r1) in spans(*units(b)) + spans(*twos(b)):
+                mul(b, r0, r1)
+
+        def late_products(b):
+            for (r0, r1) in spans(*diffs(b)):
+                mul(b, r0, r1)
+
+        def subtract(b):
+            if diffs(b)[1] > 0:
+                diff(b, 0, diffs(b)[1])
 
         idle_ps = bank("idle", [P, TOK], F32, "idle_ps")
 
@@ -308,15 +345,13 @@ def tile_decoder_kernel(tc, digits, styles, images, W_h, b_h, W1, b1, W2, b2, ou
                                         scalar2=0.0, op0=ALU.add, op1=ALU.max)
             bank_done(("h", j))
 
-        w1_codes = cp.tile([P, HN], U32, name="w1_codes", tag="cd", align_bytes=64)
-        w1_plane = cp.tile([P, HN], U8, name="w1_plane", tag="pl", align_bytes=64)
-        nc.vector.quantize_mx(out=w1_codes[:].bitcast(FP8X4), scales=w1_plane[:], in_=w1g[:])
+        w1_codes, w1_plane = code_room(1)
+        nc.vector.quantize_mx(out=w1_codes.bitcast(FP8X4), scales=w1_plane, in_=w1g[:])
 
         hg = slot("hg", [P, 4 * TOK], BF16, "hg")
         regroup(hg, h_sb)
-        h_codes = cp.tile([P, TOK], U32, name="h_codes", tag="cd", align_bytes=64)
-        h_plane = cp.tile([P, TOK], U8, name="h_plane", tag="pl", align_bytes=64)
-        nc.vector.quantize_mx(out=h_codes[:].bitcast(FP8X4), scales=h_plane[:], in_=hg[:])
+        h_codes, h_plane = code_room(2)
+        nc.vector.quantize_mx(out=h_codes.bitcast(FP8X4), scales=h_plane, in_=hg[:])
 
         b2_ps = bank("b2", [P, 2 * P], F32, "b2_ps")
         for s in range(2):
@@ -350,8 +385,8 @@ def tile_decoder_kernel(tc, digits, styles, images, W_h, b_h, W1, b1, W2, b2, ou
                 out=tps[m][:],
                 lhsT=w1_codes[:, m * P:(m + 1) * P].bitcast(FP8X4),
                 lhsT_scale=w1_plane[:, m * P:(m + 1) * P],
-                rhs=h_codes[:].bitcast(FP8X4),
-                rhs_scale=h_plane[:],
+                rhs=h_codes.bitcast(FP8X4),
+                rhs_scale=h_plane,
                 start=True,
                 stop=True,
             )
@@ -381,7 +416,7 @@ def tile_decoder_kernel(tc, digits, styles, images, W_h, b_h, W1, b1, W2, b2, ou
                                   in_=tg[:, 4 * h * HALF:4 * (h + 1) * HALF])
         for m in range(4):
             bank_done(("t", m))
-        for key in ("idle", "brow", "b2rows", "cat", "wh", "raw1", "cat_t", "w1g", "h_sb", "hg", "e_sb", "r_sb", "tg"):
+        for key in ("ident_bf", "idle", "brow", "b2rows", "cat", "wh", "raw1", "cat_t", "w1g", "h_sb", "hg", "e_sb", "r_sb", "tg"):
             slot_done(key)
         prep_copy(1)
         prep_quant(1)
@@ -392,116 +427,80 @@ def tile_decoder_kernel(tc, digits, styles, images, W_h, b_h, W1, b1, W2, b2, ou
         minus = const.tile([P, NT, 8], F32, name="minus")
 
         end = NBLK - 1
+        for b in range(NBLK):
+            for r in range(4):
+                mx(b, r)
+                sig(b, r)
+            prep_to(min(b + NCODE, NBLK - 1))
+            if b == NBLK - 3:
+                imgt(0, 0)
+                imgt(0, 1)
+            if b == NBLK - 2:
+                imgt(1, 0)
+                imgt(1, 1)
+        slot_done("codes")
 
-        def rows(tiles, b, r0, r1):
-            return [tiles[b][:, r, :] for r in range(r0, r1)]
+        def products_late(h):
+            late_products(h)
+            if "d" in FORMS[h]:
+                bank_done(("i", h, 1))
 
-        def early(h):
-            neg_rest(h, 0, 2)
-            if h in TWO_SUMS:
-                neg_rest(h, 2, 4)
-
-        def sum_early(h):
-            if h in TWO_SUMS:
-                summ(h, rows(btile, h, 0, 4), sign="-", last=True)
-            else:
-                summ(h, rows(btile, h, 2, 4))
-
-        def sum_unit(h):
-            summ(h, rows(ytile, h, 0, 2), last=True)
+        def sums_of(h):
+            sums(h, btile, *diffs(h))
+            if "t" in FORMS[h]:
+                sums(h, btile, *twos(h), sign="-")
+            sums(h, ytile, *units(h))
+            sums(h, ytile, *twos(h))
+            sums(h, ytile, *diffs(h))
             block_done(h)
 
-        issued = 0
-        late = []
-        for (lo, hi) in BATCHES:
-            for b in range(lo, hi):
-                for r in range(4):
-                    if 4 * b + r >= issued:
-                        mx(b, r)
-                        issued = 4 * b + r + 1
-                    sig(b, r, late)
-                prep_to(min(b + NCODE, NBLK - 1))
-                if late and b >= lo + LATE_FROM:
-                    late.pop(0)()
-                    if not late:
-                        free_banks.extend(mx_banks)
-                        mx_banks.clear()
-                if b == hi - 3:
-                    imgt(lo, 0)
-                    imgt(lo, 1)
-                if b == hi - 2:
-                    imgt(lo + 1, 0)
-                    imgt(lo + 1, 1)
-            log_b(lo)
-            early(lo)
-            for g in range(lo, min(hi, end)):
-                if g > lo and g + 1 < hi:
-                    log_b(g + 1)
+        log_b(0, 0, 2)
+        log_b(0, 2, 4)
+        rests(0)
+        stored = 0
+        for g in range(NBLK + LAG):
+            if g == 0:
+                log_a(0, 0, 2)
+                log_a(0, 2, 4)
+                log_b(1)
+            elif g == 1:
+                log_a(1)
+                log_b(2)
+            elif g < end:
+                log_b(g + 1)
                 log_a(g)
-                if g == lo:
-                    log_b(g + 1)
-                if g == end - 1:
-                    for r in range(4):
-                        log_a(end, r, r + 1)
-                if g in TWO_SUMS:
-                    mul(g, 0, 2)
-                    bank_done(("i", g, 0))
-                    early(g + 1)
-                else:
-                    diff(g, 2, 4)
-                    mul(g, 0, 2)
-                    diff(g, 0, 2)
-                    bank_done(("i", g, 0))
-                    if g + 1 < hi:
-                        early(g + 1)
-                if g - 2 >= lo:
-                    red_all(g - 2)
-                if g == end - 1:
-                    mul(end, 0, 1)
-                    mul(end, 1, 2)
-                mul(g, 2, 4)
-                bank_done(("i", g, 1))
-                if hi < NBLK and g == hi - 1:
-                    late.append(lambda h=g: (sum_unit(h - 1), sum_early(h)))
-                    late.append(lambda h=g: (red_all(h - 1), summ(h, rows(ytile, h, 2, 4))))
-                    late.append(lambda h=g: sum_unit(h))
-                    late.append(lambda h=g: red_all(h))
-                    continue
-                if hi < NBLK and g == hi - 2:
-                    mx_banks.extend(free_banks[:3])
-                    for k in mx_banks:
-                        free_banks.remove(k)
-                    for r in range(3):
-                        mx(hi, r)
-                    issued = 4 * hi + 3
-                if g > lo:
-                    sum_unit(g - 1)
-                sum_early(g)
-                if g == end - 1:
-                    sum_early(end)
-                if g + 2 < hi:
-                    imgt(g + 2, 0)
-                if hi < NBLK and g == hi - 2:
-                    late.append(lambda h=g: summ(h, rows(ytile, h, 2, 4)))
-                else:
-                    summ(g, rows(ytile, g, 2, 4))
-                if g + 2 < hi:
-                    imgt(g + 2, 1)
-                if g == lo + 8 and lo == 0:
-                    nc.sync.dma_start(out=out_v[:, :, 0:48], in_=res[:, :, 0:48])
-                if g == lo + 16:
-                    nc.sync.dma_start(out=out_v[:, :, 48:8 * (g - 2)], in_=res[:, :, 48:8 * (g - 2)])
-                    stored = g - 2
-        summ(end, rows(ytile, end, 0, 2))
-        mul(end, 2, 3)
-        mul(end, 3, 4)
-        summ(end, rows(ytile, end, 2, 3))
-        sum_unit(end - 1)
-        red_all(end - 2)
-        red(end, "-")
-        summ(end, rows(ytile, end, 3, 4), last=True)
-        red(end - 1)
-        red(end)
-        nc.vector.tensor_tensor(out=res[:, :, 8 * end:8 * end + 8], in0=res[:, :, 8 * end:8 * end + 8],
-                                in1=minus[:], op=ALU.add)
+            elif g == end:
+                for r in range(4):
+                    log_a(g, r, r + 1)
+            h = g - LAG
+            if g == NBLK:
+                sums_of(end)
+            if 0 <= h < end:
+                products_late(h)
+            if g < end:
+                products(g)
+            elif g == end:
+                for r in range(4):
+                    mul(g, r, r + 1)
+            if g < NBLK:
+                subtract(g)
+                bank_done(("i", g, 0))
+                if "d" not in FORMS[g]:
+                    bank_done(("i", g, 1))
+            if g + 2 < NBLK:
+                imgt(g + 2, 0)
+            if g + 1 < NBLK:
+                rests(g + 1)
+            if 0 <= h < end:
+                sums_of(h)
+            if 0 < h < end:
+                red_all(h - 1)
+            if g == NBLK:
+                red_all(end)
+            if g + 2 < NBLK:
+                imgt(g + 2, 1)
+            if h in (10, 18):
+                nc.sync.dma_start(out=out_v[:, :, 8 * stored:8 * h], in_=res[:, :, 8 * stored:8 * h])
+                stored = h
+        red_all(end - 1)
         nc.sync.dma_start(out=out_v[:, :, 8 * stored:], in_=res[:, :, 8 * stored:])

@@ -30,8 +30,13 @@ SA = SELU_SCALE * SELU_ALPHA
 NBIG = 28
 NCODE = 3
 AHEAD = 4
-FORMS = ["uudd", "uuud"] * 11 + ["uudd", "tttt"]
+FORMS = ["uudd", "uuud"] * 10 + ["uudd", "uuuu", "uuuu", "tttt"]
 LAG = 2
+IDLE1 = 5
+IDLE2 = 6
+S_H0 = (2, 3)
+S_H1 = (0, 1, 2, 3)
+V_RELU = 1
 
 FLOPS = 2 * TOK * (128 * HN + HN * HN + HN * CH)
 
@@ -169,27 +174,26 @@ def tile_decoder_kernel(tc, digits, styles, images, W_h, b_h, W1, b1, W2, b2, ou
                     prep_copy(b + 1)
                 prep_quant(b)
 
-        def mx(b, r):
-            u = bank(("u", b, r), [P, TOK], F32, "u", free_banks)
+        def mx(b, r, t0=0, t1=TOK):
+            ubank[(b, r, t0)] = bank(("u", b, r, t0), [P, t1 - t0], F32, "u")
             nc.tensor.matmul_mx(
-                out=u[:],
+                out=ubank[(b, r, t0)][:],
                 lhsT=codes[b][:, r * P:(r + 1) * P].bitcast(FP8X4),
                 lhsT_scale=planes[b][:, r * P:(r + 1) * P],
-                rhs=t_codes[:].bitcast(FP8X4),
-                rhs_scale=t_plane[:],
+                rhs=t_codes[:, t0:t1].bitcast(FP8X4),
+                rhs_scale=t_plane[:, t0:t1],
                 start=True,
                 stop=True,
             )
-            ubank[(b, r)] = u
 
-        def sig(b, r):
-            if r == 0:
+        def sig(b, r, t0=0, t1=TOK):
+            if r == 0 and t0 == 0:
                 ytile[b] = slot(("y", b), [P, 4, TOK], F32, "y")
             nc.scalar.activation(
-                out=ytile[b][:, r, :], in_=ubank[(b, r)][:], func=ACT.Sigmoid,
+                out=ytile[b][:, r, t0:t1], in_=ubank[(b, r, t0)][:], func=ACT.Sigmoid,
                 bias=nb2[:, 4 * b + r:4 * b + r + 1], scale=-1.0,
             )
-            bank_done(("u", b, r))
+            bank_done(("u", b, r, t0))
 
         def log_b(b, r0=0, r1=4):
             if r0 == 0:
@@ -308,7 +312,13 @@ def tile_decoder_kernel(tc, digits, styles, images, W_h, b_h, W1, b1, W2, b2, ou
             for n in range(count):
                 nc.tensor.matmul(out=idle_ps[:], lhsT=idle[:, 0:P], rhs=idle[:], start=True, stop=True)
 
-        idle_mm(4)
+        def regroup(dst, src, c0=0, c1=TOK):
+            nc.vector.tensor_copy(
+                out=dst[:, 4 * c0:4 * c1].rearrange("p (c i t) -> p c t i", i=4, t=4),
+                in_=src[:, :, c0:c1].rearrange("p t (c i) -> p c t i", i=4),
+            )
+
+        idle_mm(IDLE1)
         cat_ps = bank("cat", [P, TOK], BF16, "cat_ps")
         for t in range(NT):
             nc.tensor.transpose(out=cat_ps[:, t * P:(t + 1) * P], in_=cat[:, t, :],
@@ -319,16 +329,6 @@ def tile_decoder_kernel(tc, digits, styles, images, W_h, b_h, W1, b1, W2, b2, ou
         nc.tensor.transpose(out=bias_ps[:], in_=brow[:], identity=ident_bf[:])
         bh = const.tile([P, 4], F32, name="bh")
         nc.vector.tensor_copy(out=bh[:], in_=bias_ps[:, 0:4])
-        b1c = const.tile([P, 4], F32, name="b1c")
-        nc.vector.tensor_copy(out=b1c[:], in_=bias_ps[:, 4:8])
-        b1e = const.tile([P, 4], F32, name="b1e")
-        nc.vector.tensor_scalar_add(out=b1e[:], in0=bias_ps[:, 4:8], scalar1=math.log(SA))
-
-        def regroup(dst, src):
-            nc.vector.tensor_copy(
-                out=dst[:].rearrange("p (c i t) -> p c t i", i=4, t=4),
-                in_=src[:].rearrange("p t (c i) -> p c t i", i=4),
-            )
 
         w1g = slot("w1g", [P, 4 * HN], BF16, "w1g")
         regroup(w1g, raw1)
@@ -337,7 +337,7 @@ def tile_decoder_kernel(tc, digits, styles, images, W_h, b_h, W1, b1, W2, b2, ou
             hp = bank(("h", j), [P, TOK], F32, "hp")
             nc.tensor.matmul(out=hp[:], lhsT=wh[:, j * P:(j + 1) * P], rhs=cat_t[:],
                              start=True, stop=True)
-            if j < 3:
+            if j != V_RELU:
                 nc.scalar.activation(out=h_sb[:, j, :], in_=hp[:], func=ACT.Relu,
                                      bias=bh[:, j:j + 1], scale=1.0)
             else:
@@ -347,12 +347,18 @@ def tile_decoder_kernel(tc, digits, styles, images, W_h, b_h, W1, b1, W2, b2, ou
 
         w1_codes, w1_plane = code_room(1)
         nc.vector.quantize_mx(out=w1_codes.bitcast(FP8X4), scales=w1_plane, in_=w1g[:])
+        b1c = const.tile([P, 4], F32, name="b1c")
+        nc.vector.tensor_copy(out=b1c[:], in_=bias_ps[:, 4:8])
+        b1e = const.tile([P, 4], F32, name="b1e")
+        nc.vector.tensor_scalar_add(out=b1e[:], in0=bias_ps[:, 4:8], scalar1=math.log(SA))
 
+        halves = [slice(0, HALF), slice(HALF, TOK)]
         hg = slot("hg", [P, 4 * TOK], BF16, "hg")
-        regroup(hg, h_sb)
         h_codes, h_plane = code_room(2)
-        nc.vector.quantize_mx(out=h_codes.bitcast(FP8X4), scales=h_plane, in_=hg[:])
-
+        for h in range(2):
+            regroup(hg, h_sb, h * HALF, (h + 1) * HALF)
+            nc.vector.quantize_mx(out=h_codes[:, halves[h]].bitcast(FP8X4), scales=h_plane[:, halves[h]],
+                                  in_=hg[:, 4 * h * HALF:4 * (h + 1) * HALF])
         b2_ps = bank("b2", [P, 2 * P], F32, "b2_ps")
         for s in range(2):
             nc.tensor.transpose(
@@ -368,69 +374,96 @@ def tile_decoder_kernel(tc, digits, styles, images, W_h, b_h, W1, b1, W2, b2, ou
                 in0=b2_ps[:, s * P:s * P + NBLK].bitcast(BF16).rearrange("p (b e) -> p b e", e=2),
                 scalar1=-1.0,
             )
-
         prep_copy(0, on_scalar=True)
-        prep_quant(0)
         e_sb = slot("e_sb", [P, 4, TOK], F32, "e_sb")
         r_sb = slot("r_sb", [P, 4, TOK], F32, "r_sb")
         tg = slot("tg", [P, 4 * TOK], BF16, "tg")
         t_codes = const.tile([P, TOK], U32, name="t_codes", align_bytes=64)
         t_plane = const.tile([P, TOK], U8, name="t_plane", align_bytes=64)
-        idle_mm(6)
+        idle_mm(IDLE2)
         for key in ("cat", "bias", "b2", "idle"):
             bank_done(key)
-        tps = [bank(("t", m), [P, TOK], F32, "tp") for m in range(4)]
-        for m in range(4):
-            nc.tensor.matmul_mx(
-                out=tps[m][:],
-                lhsT=w1_codes[:, m * P:(m + 1) * P].bitcast(FP8X4),
-                lhsT_scale=w1_plane[:, m * P:(m + 1) * P],
-                rhs=h_codes.bitcast(FP8X4),
-                rhs_scale=h_plane,
-                start=True,
-                stop=True,
-            )
-        for m in range(4):
-            nc.scalar.activation(out=e_sb[:, m, :], in_=tps[m][:], func=ACT.Exp,
-                                 bias=b1e[:, m:m + 1], scale=1.0)
-        nc.scalar.activation(out=r_sb[:, 3, :], in_=tps[3][:], func=ACT.Relu,
-                             bias=b1c[:, 3:4], scale=1.0)
-        nc.scalar.activation(out=warm[:], in_=eps_b[:], func=ACT.Sigmoid)
-        for m in (1, 2, 0):
-            nc.vector.tensor_scalar(out=r_sb[:, m, :], in0=tps[m][:], scalar1=b1c[:, m:m + 1],
-                                    scalar2=0.0, op0=ALU.add, op1=ALU.max)
-        for m in (0, 2):
-            nc.vector.tensor_scalar(out=e_sb[:, m:m + 2, :], in0=e_sb[:, m:m + 2, :], scalar1=SA,
-                                    scalar2=-SA, op0=ALU.min, op1=ALU.add)
+        tps = {}
         for h in range(2):
-            cols = slice(h * HALF, (h + 1) * HALF)
+            for m in range(4):
+                tps[(h, m)] = bank(("t", h, m), [P, HALF], F32, "tp")
+                nc.tensor.matmul_mx(
+                    out=tps[(h, m)][:],
+                    lhsT=w1_codes[:, m * P:(m + 1) * P].bitcast(FP8X4),
+                    lhsT_scale=w1_plane[:, m * P:(m + 1) * P],
+                    rhs=h_codes[:, halves[h]].bitcast(FP8X4),
+                    rhs_scale=h_plane[:, halves[h]],
+                    start=True,
+                    stop=True,
+                )
+
+        def exps(h):
+            for m in range(4):
+                nc.scalar.activation(out=e_sb[:, m, halves[h]], in_=tps[(h, m)][:], func=ACT.Exp,
+                                     bias=b1e[:, m:m + 1], scale=1.0)
+
+        def relus(h, on_scalar, on_vector):
+            for m in on_scalar:
+                nc.scalar.activation(out=r_sb[:, m, halves[h]], in_=tps[(h, m)][:], func=ACT.Relu,
+                                     bias=b1c[:, m:m + 1], scale=1.0)
+            for m in on_vector:
+                nc.vector.tensor_scalar(out=r_sb[:, m, halves[h]], in0=tps[(h, m)][:], scalar1=b1c[:, m:m + 1],
+                                        scalar2=0.0, op0=ALU.add, op1=ALU.max)
+
+        def clamp(h):
+            for m in (0, 2):
+                nc.vector.tensor_scalar(out=e_sb[:, m:m + 2, halves[h]], in0=e_sb[:, m:m + 2, halves[h]],
+                                        scalar1=SA, scalar2=-SA, op0=ALU.min, op1=ALU.add)
+
+        def add(h):
             nc.vector.scalar_tensor_tensor(
                 out=tg[:, 4 * h * HALF:4 * (h + 1) * HALF].rearrange("p (c t) -> p c t", t=4),
-                in0=r_sb[:, :, cols].rearrange("p t c -> p c t"),
+                in0=r_sb[:, :, halves[h]].rearrange("p t c -> p c t"),
                 scalar=SELU_SCALE,
-                in1=e_sb[:, :, cols].rearrange("p t c -> p c t"),
+                in1=e_sb[:, :, halves[h]].rearrange("p t c -> p c t"),
                 op0=ALU.mult, op1=ALU.add)
-        for h in range(2):
-            cols = slice(h * HALF, (h + 1) * HALF)
-            nc.vector.quantize_mx(out=t_codes[:, cols].bitcast(FP8X4), scales=t_plane[:, cols],
+
+        def t_quant(h):
+            nc.vector.quantize_mx(out=t_codes[:, halves[h]].bitcast(FP8X4), scales=t_plane[:, halves[h]],
                                   in_=tg[:, 4 * h * HALF:4 * (h + 1) * HALF])
-        for m in range(4):
-            bank_done(("t", m))
+
+        exps(0)
+        relus(0, S_H0, [m for m in range(4) if m not in S_H0])
+        clamp(0)
+        add(0)
+        exps(1)
+        relus(1, S_H1, [m for m in range(4) if m not in S_H1])
+        nc.scalar.activation(out=warm[:], in_=eps_b[:], func=ACT.Sigmoid)
+        prep_quant(0)
+        t_quant(0)
+        clamp(1)
+        add(1)
+        t_quant(1)
+        for h in range(2):
+            for m in range(4):
+                bank_done(("t", h, m))
         for key in ("ident_bf", "idle", "brow", "b2rows", "cat", "wh", "raw1", "cat_t", "w1g", "h_sb", "hg", "e_sb", "r_sb", "tg"):
             slot_done(key)
         prep_copy(1)
         prep_quant(1)
         prep_copy(2)
-        prep_to(2)
+        prep_quant(2)
+        prep_copy(3)
 
         res = const.tile([P, NT, CH // 64], F32, name="res")
         minus = const.tile([P, NT, 8], F32, name="minus")
 
         end = NBLK - 1
         for b in range(NBLK):
-            for r in range(4):
-                mx(b, r)
-                sig(b, r)
+            if b == 0:
+                for t0 in (0, HALF):
+                    for r in range(4):
+                        mx(b, r, t0, t0 + HALF)
+                        sig(b, r, t0, t0 + HALF)
+            else:
+                for r in range(4):
+                    mx(b, r)
+                    sig(b, r)
             prep_to(min(b + NCODE, NBLK - 1))
             if b == NBLK - 3:
                 imgt(0, 0)

@@ -30,7 +30,7 @@ SA = SELU_SCALE * SELU_ALPHA
 NBIG = 28
 NCODE = 3
 AHEAD = 4
-FORMS = ["uudd", "uuud"] * 10 + ["uudd", "uuuu", "uuuu", "tttt"]
+FORMS = ["uudd", "uuud", "uudd", "uuus"] * 5 + ["uudd", "uuuu", "uuuu", "ssss"]
 LAG = 2
 IDLE1 = 5
 IDLE2 = 6
@@ -224,35 +224,42 @@ def tile_decoder_kernel(tc, digits, styles, images, W_h, b_h, W1, b1, W2, b2, ou
             return iv[:, r0 - 2 * s:r1 - 2 * s, :]
 
         def diff(b, r0, r1):
-            nc.gpsimd.tensor_tensor(out=ytile[b][:, r0:r1, :], in0=ytile[b][:, r0:r1, :],
-                                    in1=btile[b][:, r0:r1, :], op=ALU.subtract)
+            first, second = (btile, ytile) if "s" in FORMS[b] else (ytile, btile)
+            nc.gpsimd.tensor_tensor(out=ytile[b][:, r0:r1, :], in0=first[b][:, r0:r1, :],
+                                    in1=second[b][:, r0:r1, :], op=ALU.subtract)
 
         def mul(b, r0, r1):
+            negated = FORMS[b][r0] == "s"
             nc.vector.scalar_tensor_tensor(out=ytile[b][:, r0:r1, :], in0=ytile[b][:, r0:r1, :],
-                                           scalar=D_MIN, in1=image(b, r0, r1),
-                                           op0=ALU.max, op1=ALU.mult)
+                                           scalar=-1.0 if negated else D_MIN, in1=image(b, r0, r1),
+                                           op0=ALU.mult if negated else ALU.max, op1=ALU.mult)
+
+        def below_one(b):
+            rows = ytile[b][:, pairs(b)[0]:4, :]
+            nc.vector.tensor_scalar_min(out=rows, in0=rows, scalar1=1.0 - 2.0 ** -24)
 
         def neg_rest(b, r0, r1):
             nc.vector.scalar_tensor_tensor(out=btile[b][:, r0:r1, :], in0=image(b, r0, r1), scalar=1.0,
                                            in1=btile[b][:, r0:r1, :],
                                            op0=ALU.subtract, op1=ALU.mult)
 
-        def sums(b, tiles, r0, r1, sign="+"):
-            fresh = (b, sign) not in stile and r0 < r1
+        def sums(b, tiles, r0, r1):
+            if r0 == r1:
+                return
+            fresh = b not in stile
             if fresh:
-                stile[(b, sign)] = bank(("s", b, sign), [P, TOK], F32, "st")
-                left[(b, sign)] = NT * (units(b)[1] + 2 * (diffs(b)[1] - diffs(b)[0]) + (twos(b)[1] - twos(b)[0])
-                                        if sign == "+" else twos(b)[1] - twos(b)[0])
+                stile[b] = bank(("s", b), [P, TOK], F32, "st")
+                left[b] = NT * (4 + FORMS[b].count("d") + FORMS[b].count("s"))
             for r in range(r0, r1):
                 for t in range(NT):
-                    left[(b, sign)] = left[(b, sign)] - 1
+                    left[b] = left[b] - 1
                     nc.tensor.matmul(
-                        out=stile[(b, sign)][:, t * P:(t + 1) * P],
+                        out=stile[b][:, t * P:(t + 1) * P],
                         lhsT=tiles[b][:, r, t * P:(t + 1) * P],
                         rhs=ident_f[:],
                         is_transpose=True,
                         start=fresh,
-                        stop=(left[(b, sign)] == 0),
+                        stop=(left[b] == 0),
                     )
                     fresh = False
 
@@ -262,28 +269,20 @@ def tile_decoder_kernel(tc, digits, styles, images, W_h, b_h, W1, b1, W2, b2, ou
         def diffs(b):
             return (units(b)[1], units(b)[1] + FORMS[b].count("d"))
 
-        def twos(b):
+        def pairs(b):
             return (diffs(b)[1], 4)
 
         def block_done(b):
             slot_done(("y", b))
             slot_done(("b", b))
 
-        def red(b, sign="+"):
-            dst = res[:, :, 8 * b:8 * b + 8] if sign == "+" else minus[:]
+        def red(b):
             nc.vector.tensor_reduce(
-                out=dst,
-                in_=stile[(b, sign)][:].rearrange("p (t g w) -> p t g w", t=NT, g=8),
-                axis=AX.X, op=ALU.add, negate=(sign == "+"),
+                out=res[:, :, 8 * b:8 * b + 8],
+                in_=stile[b][:].rearrange("p (t g w) -> p t g w", t=NT, g=8),
+                axis=AX.X, op=ALU.add, negate=("s" not in FORMS[b]),
             )
-            bank_done(("s", b, sign))
-
-        def red_all(b):
-            red(b)
-            if "t" in FORMS[b]:
-                red(b, "-")
-                nc.vector.tensor_tensor(out=res[:, :, 8 * b:8 * b + 8], in0=res[:, :, 8 * b:8 * b + 8],
-                                        in1=minus[:], op=ALU.add)
+            bank_done(("s", b))
 
         def spans(r0, r1):
             if r0 < 2 < r1:
@@ -291,11 +290,11 @@ def tile_decoder_kernel(tc, digits, styles, images, W_h, b_h, W1, b1, W2, b2, ou
             return [(r0, r1)] if r0 < r1 else []
 
         def rests(b):
-            for (r0, r1) in spans(*units(b)) + spans(*twos(b)):
+            for (r0, r1) in spans(*units(b)) + spans(*pairs(b)):
                 neg_rest(b, r0, r1)
 
         def products(b):
-            for (r0, r1) in spans(*units(b)) + spans(*twos(b)):
+            for (r0, r1) in spans(*units(b)) + spans(*pairs(b)):
                 mul(b, r0, r1)
 
         def late_products(b):
@@ -451,7 +450,6 @@ def tile_decoder_kernel(tc, digits, styles, images, W_h, b_h, W1, b1, W2, b2, ou
         prep_copy(3)
 
         res = const.tile([P, NT, CH // 64], F32, name="res")
-        minus = const.tile([P, NT, 8], F32, name="minus")
 
         end = NBLK - 1
         for b in range(NBLK):
@@ -465,6 +463,8 @@ def tile_decoder_kernel(tc, digits, styles, images, W_h, b_h, W1, b1, W2, b2, ou
                     mx(b, r)
                     sig(b, r)
             prep_to(min(b + NCODE, NBLK - 1))
+            if "s" in FORMS[b]:
+                below_one(b)
             if b == NBLK - 3:
                 imgt(0, 0)
                 imgt(0, 1)
@@ -480,10 +480,9 @@ def tile_decoder_kernel(tc, digits, styles, images, W_h, b_h, W1, b1, W2, b2, ou
 
         def sums_of(h):
             sums(h, btile, *diffs(h))
-            if "t" in FORMS[h]:
-                sums(h, btile, *twos(h), sign="-")
+            sums(h, btile, *pairs(h))
             sums(h, ytile, *units(h))
-            sums(h, ytile, *twos(h))
+            sums(h, ytile, *pairs(h))
             sums(h, ytile, *diffs(h))
             block_done(h)
 
@@ -527,13 +526,13 @@ def tile_decoder_kernel(tc, digits, styles, images, W_h, b_h, W1, b1, W2, b2, ou
             if 0 <= h < end:
                 sums_of(h)
             if 0 < h < end:
-                red_all(h - 1)
+                red(h - 1)
             if g == NBLK:
-                red_all(end)
+                red(end)
             if g + 2 < NBLK:
                 imgt(g + 2, 1)
             if h in (10, 18):
                 nc.sync.dma_start(out=out_v[:, :, 8 * stored:8 * h], in_=res[:, :, 8 * stored:8 * h])
                 stored = h
-        red_all(end - 1)
+        red(end - 1)
         nc.sync.dma_start(out=out_v[:, :, 8 * stored:], in_=res[:, :, 8 * stored:])

@@ -30,7 +30,7 @@ SA = SELU_SCALE * SELU_ALPHA
 NBIG = 28
 NCODE = 3
 AHEAD = 4
-FORMS = ["uudd", "uuud", "uudd", "uuus"] * 5 + ["uudd", "uuuu", "uuuu", "ssss"]
+FORMS = ["uudd", "uuud", "uudd", "uuus", "uudd", "uuuu"] * 3 + ["uudd", "uuud", "uudd"] + ["uuuu", "uuuu", "ssss"]
 LAG = 2
 IDLE1 = 5
 IDLE2 = 6

@@ -32,7 +32,7 @@ NCODE = 3
 AHEAD = 4
 FORMS = ["uudd", "uuud", "uudd", "uuus", "uudd", "uuuu"] * 3 + ["uudd", "uuud", "uudd"] + ["uuuu", "uuuu", "ssss"]
 LAG = 2
-IDLE1 = 5
+IDLE1 = 4
 IDLE2 = 6
 S_H0 = (2, 3)
 S_H1 = (0, 1, 2, 3)
@@ -144,18 +144,20 @@ def tile_decoder_kernel(tc, digits, styles, images, W_h, b_h, W1, b1, W2, b2, ou
             lo = NCODE * BLK + n * BLK // 4
             return words, code_words[:, lo:lo + BLK // 4].bitcast(U8)
 
-        def prep_copy(b, on_scalar=False):
+        def prep_copy(b, s0=0, s1=2, on_scalar=False):
             c = b // 2
-            if b % 2 == 0:
+            if c not in groups:
                 groups[c] = slot(("group", c), [P, 2, 4 * BLK], BF16, "g2")
             lo = (b % 2) * BLK
             dst = groups[c][:, b % 2, :].rearrange("p (s e q j) -> p s q j e", s=2, e=2, j=4)
             src = raws[c][:, :, lo:lo + BLK].rearrange("p j (q s e) -> p s q j e", s=2, e=2)
             if on_scalar:
-                for s in range(2):
+                for s in range(s0, s1):
                     nc.scalar.copy(out=dst[:, s], in_=src[:, s])
             else:
-                nc.vector.tensor_copy(out=dst, in_=src)
+                nc.vector.tensor_copy(out=dst[:, s0:s1], in_=src[:, s0:s1])
+            if s1 < 2:
+                return
             grouped.add(b)
             if b % 2 == 1:
                 slot_done(("raw", c))
@@ -436,6 +438,7 @@ def tile_decoder_kernel(tc, digits, styles, images, W_h, b_h, W1, b1, W2, b2, ou
         prep_quant(0)
         t_quant(0)
         clamp(1)
+        prep_copy(1, 0, 1)
         add(1)
         t_quant(1)
         for h in range(2):
@@ -443,7 +446,7 @@ def tile_decoder_kernel(tc, digits, styles, images, W_h, b_h, W1, b1, W2, b2, ou
                 bank_done(("t", h, m))
         for key in ("ident_bf", "idle", "brow", "b2rows", "cat", "wh", "raw1", "cat_t", "w1g", "h_sb", "hg", "e_sb", "r_sb", "tg"):
             slot_done(key)
-        prep_copy(1)
+        prep_copy(1, 1, 2)
         prep_quant(1)
         prep_copy(2)
         prep_quant(2)

import math
from contextlib import ExitStack

import concourse.masks as masks
import concourse.mybir as mybir

F32 = mybir.dt.float32
BF16 = mybir.dt.bfloat16
U32 = mybir.dt.uint32
U8 = mybir.dt.uint8
FP8X4 = mybir.dt.float8_e4m3fn_x4
ACT = mybir.ActivationFunctionType
ALU = mybir.AluOpType
AX = mybir.AxisListType

P = 128
TOK = 512
HALF = TOK // 2
NT = 4
HN = 512
CH = 12288
BLK = 512
NBLK = CH // BLK
EPS = 1e-9
D_MIN = math.log(EPS) - 1e-3
SELU_ALPHA = 1.6732632423543772848170429916717
SELU_SCALE = 1.0507009873554804934193349852946
SA = SELU_SCALE * SELU_ALPHA

NBIG = 28
NCODE = 3
AHEAD = 4
FORMS = ["uudd", "uuud", "uudd", "uuus", "uudd", "uuuu"] * 3 + ["uudd", "uuud", "uudd"] + ["uuuu", "uuuu", "ssss"]
LAG = 2
IDLE1 = 4
IDLE2 = 6
S_H0 = (2, 3)
S_H1 = (0, 1, 2, 3)
V_RELU = 1

FLOPS = 2 * TOK * (128 * HN + HN * HN + HN * CH)


def tile_decoder_kernel(tc, digits, styles, images, W_h, b_h, W1, b1, W2, b2, out):
    nc = tc.nc
    dig_v = digits.rearrange("s b c -> (s b) c").rearrange("(t p) c -> p t c", p=P)
    sty_v = styles.rearrange("s b c -> (s b) c").rearrange("(t p) c -> p t c", p=P)
    img_v = images.rearrange("s b c h w -> (s b) (c h w)").rearrange("(t p) n -> p t n", p=P)
    out_v = out.rearrange("s b c h -> (s b) (c h)").rearrange("(t p) g -> p t g", p=P)
    w1_v = W1.rearrange("(j p) n -> p j n", p=P)
    w2_v = W2.rearrange("(j p) n -> p j n", p=P)

    with ExitStack() as ctx:
        ctx.enter_context(tc.manual_schedule())
        const = ctx.enter_context(tc.tile_pool(name="const", bufs=1))
        big = ctx.enter_context(tc.tile_pool(name="big", bufs=1))
        imp = ctx.enter_context(tc.tile_pool(name="imp", bufs=2))
        psum = ctx.enter_context(tc.psum_pool(name="psum", bufs=1))
        free_slots = list(range(NBIG))
        free_banks = list(range(8))
        slot_of = {}
        bank_of = {}

        def slot(key, shape, dtype, name):
            slot_of[key] = free_slots.pop(0)
            return big.tile(shape, dtype, name=name, tag="s%d" % slot_of[key], align_bytes=64)

        def slot_done(key):
            free_slots.append(slot_of.pop(key))

        def bank(key, shape, dtype, name, source=None):
            bank_of[key] = (source or free_banks).pop(0)
            return psum.tile(shape, dtype, name=name, tag="b%d" % bank_of[key])

        def bank_done(key):
            free_banks.append(bank_of.pop(key))

        raws = {}
        imgs = {}
        groups = {}
        grouped = set()
        codes = {}
        planes = {}
        ubank = {}
        ytile = {}
        btile = {}
        itile = {}
        stile = {}
        left = {}

        ident_bf = slot("ident_bf", [P, P], BF16, "ident_bf")
        masks.make_identity(nc, ident_bf[:])
        ident_f = const.tile([P, P], F32, name="ident_f")
        masks.make_identity(nc, ident_f[:])
        idle = slot("idle", [P, TOK], BF16, "idle")
        nc.vector.memset(idle[:], 0.0)
        brow = slot("brow", [P, P], BF16, "brow")
        nc.vector.memset(brow[:], 0.0)
        b2rows = slot("b2rows", [P, BLK], BF16, "b2rows")
        nc.vector.memset(b2rows[:], 0.0)
        eps_b = const.tile([P, 1], F32, name="eps_b")
        nc.vector.memset(eps_b[:], EPS)
        one_eps_b = const.tile([P, 1], F32, name="one_eps_b")
        nc.vector.memset(one_eps_b[:], 1.0)
        nc.vector.tensor_scalar_add(out=one_eps_b[:], in0=one_eps_b[:], scalar1=EPS)
        warm = const.tile([P, 1], F32, name="warm")
        nc.scalar.activation(out=warm[:], in_=eps_b[:], func=ACT.Relu)

        cat = slot("cat", [P, NT, P], BF16, "cat")
        nc.sync.dma_start(out=cat[:, :, 0:32], in_=dig_v)
        nc.sync.dma_start(out=cat[:, :, 32:128], in_=sty_v)
        wh = slot("wh", [P, HN], BF16, "wh")
        nc.sync.dma_start(out=wh[:], in_=W_h)
        nc.sync.dma_start(out=brow[0:4, :], in_=b_h.rearrange("(j p) -> j p", p=P))
        nc.sync.dma_start(out=brow[4:8, :], in_=b1.rearrange("(j p) -> j p", p=P))
        raw1 = slot("raw1", [P, 4, HN], BF16, "raw1")
        nc.sync.dma_start(out=raw1[:], in_=w1_v)
        nc.sync.dma_start(out=b2rows[0:NBLK, :], in_=b2.rearrange("(b x) -> b x", x=BLK))

        def load_w2(c, parts=1):
            raw = slot(("raw", c), [P, 4, 2 * BLK], BF16, "raw")
            width = 2 * BLK // parts
            for n in range(parts):
                lo = n * width
                nc.sync.dma_start(out=raw[:, :, lo:lo + width],
                                  in_=w2_v[:, :, 2 * BLK * c + lo:2 * BLK * c + lo + width])
            raws[c] = raw

        def load_img(b):
            im = imp.tile([P, NT, BLK], BF16, name="im", tag="im")
            nc.sync.dma_start(out=im[:], in_=img_v[:, :, b * BLK:(b + 1) * BLK])
            imgs[b] = im

        load_w2(0, parts=2)
        for c in range(1, AHEAD):
            load_w2(c)
        for b in range(2):
            load_img(b)

        code_words = slot("codes", [P, NCODE * BLK * 5 // 4], U32, "code_words")

        def code_room(n):
            words = code_words[:, n * BLK:(n + 1) * BLK]
            lo = NCODE * BLK + n * BLK // 4
            return words, code_words[:, lo:lo + BLK // 4].bitcast(U8)

        def prep_copy(b, s0=0, s1=2, on_scalar=False):
            c = b // 2
            if c not in groups:
                groups[c] = slot(("group", c), [P, 2, 4 * BLK], BF16, "g2")
            lo = (b % 2) * BLK
            dst = groups[c][:, b % 2, :].rearrange("p (s e q j) -> p s q j e", s=2, e=2, j=4)
            src = raws[c][:, :, lo:lo + BLK].rearrange("p j (q s e) -> p s q j e", s=2, e=2)
            if on_scalar:
                for s in range(s0, s1):
                    nc.scalar.copy(out=dst[:, s], in_=src[:, s])
            else:
                nc.vector.tensor_copy(out=dst[:, s0:s1], in_=src[:, s0:s1])
            if s1 < 2:
                return
            grouped.add(b)
            if b % 2 == 1:
                slot_done(("raw", c))
                if c + AHEAD < NBLK // 2:
                    load_w2(c + AHEAD)

        def prep_quant(b):
            codes[b], planes[b] = code_room(b % NCODE)
            nc.vector.quantize_mx(out=codes[b].bitcast(FP8X4), scales=planes[b], in_=groups[b // 2][:, b % 2, :])
            if b % 2 == 1:
                slot_done(("group", b // 2))

        def prep_to(last):
            for b in range(len(codes), min(last + 1, NBLK)):
                if b + 1 < NBLK and b + 1 not in grouped:
                    prep_copy(b + 1)
                prep_quant(b)

        def mx(b, r, t0=0, t1=TOK):
            ubank[(b, r, t0)] = bank(("u", b, r, t0), [P, t1 - t0], F32, "u")
            nc.tensor.matmul_mx(
                out=ubank[(b, r, t0)][:],
                lhsT=codes[b][:, r * P:(r + 1) * P].bitcast(FP8X4),
                lhsT_scale=planes[b][:, r * P:(r + 1) * P],
                rhs=t_codes[:, t0:t1].bitcast(FP8X4),
                rhs_scale=t_plane[:, t0:t1],
                start=True,
                stop=True,
            )

        def sig(b, r, t0=0, t1=TOK):
            if r == 0 and t0 == 0:
                ytile[b] = slot(("y", b), [P, 4, TOK], F32, "y")
            nc.scalar.activation(
                out=ytile[b][:, r, t0:t1], in_=ubank[(b, r, t0)][:], func=ACT.Sigmoid,
                bias=nb2[:, 4 * b + r:4 * b + r + 1], scale=-1.0,
            )
            bank_done(("u", b, r, t0))

        def log_b(b, r0=0, r1=4):
            if r0 == 0:
                btile[b] = slot(("b", b), [P, 4, TOK], F32, "bt")
            nc.scalar.activation(out=btile[b][:, r0:r1, :], in_=ytile[b][:, r0:r1, :], func=ACT.Ln,
                                 bias=eps_b[:, 0:1], scale=1.0)

        def log_a(b, r0=0, r1=4):
            nc.scalar.activation(out=ytile[b][:, r0:r1, :], in_=ytile[b][:, r0:r1, :], func=ACT.Ln,
                                 bias=one_eps_b[:, 0:1], scale=-1.0)

        def imgt(b, s):
            it = bank(("i", b, s), [P, TOK], F32, "it")
            for t in range(NT):
                words = imgs[b][:, t, :].bitcast(F32)
                nc.tensor.transpose(
                    out=it[:, t * P:(t + 1) * P],
                    in_=words.rearrange("p (q s) -> p s q", s=2)[:, s, :],
                    identity=ident_f[:],
                )
            itile[(b, s)] = it
            if s == 1 and b + 2 < NBLK:
                load_img(b + 2)

        def image(b, r0, r1):
            s = r0 // 2
            iv = itile[(b, s)][:].bitcast(BF16).rearrange("p (t e) -> p e t", e=2)
            return iv[:, r0 - 2 * s:r1 - 2 * s, :]

        def diff(b, r0, r1):
            first, second = (btile, ytile) if "s" in FORMS[b] else (ytile, btile)
            nc.gpsimd.tensor_tensor(out=ytile[b][:, r0:r1, :], in0=first[b][:, r0:r1, :],
                                    in1=second[b][:, r0:r1, :], op=ALU.subtract)

        def mul(b, r0, r1):
            negated = FORMS[b][r0] == "s"
            nc.vector.scalar_tensor_tensor(out=ytile[b][:, r0:r1, :], in0=ytile[b][:, r0:r1, :],
                                           scalar=-1.0 if negated else D_MIN, in1=image(b, r0, r1),
                                           op0=ALU.mult if negated else ALU.max, op1=ALU.mult)

        def below_one(b):
            rows = ytile[b][:, pairs(b)[0]:4, :]
            nc.vector.tensor_scalar_min(out=rows, in0=rows, scalar1=1.0 - 2.0 ** -24)

        def neg_rest(b, r0, r1):
            nc.vector.scalar_tensor_tensor(out=btile[b][:, r0:r1, :], in0=image(b, r0, r1), scalar=1.0,
                                           in1=btile[b][:, r0:r1, :],
                                           op0=ALU.subtract, op1=ALU.mult)

        def sums(b, tiles, r0, r1):
            if r0 == r1:
                return
            fresh = b not in stile
            if fresh:
                stile[b] = bank(("s", b), [P, TOK], F32, "st")
                left[b] = NT * (4 + FORMS[b].count("d") + FORMS[b].count("s"))
            for r in range(r0, r1):
                for t in range(NT):
                    left[b] = left[b] - 1
                    nc.tensor.matmul(
                        out=stile[b][:, t * P:(t + 1) * P],
                        lhsT=tiles[b][:, r, t * P:(t + 1) * P],
                        rhs=ident_f[:],
                        is_transpose=True,
                        start=fresh,
                        stop=(left[b] == 0),
                    )
                    fresh = False

        def units(b):
            return (0, FORMS[b].count("u"))

        def diffs(b):
            return (units(b)[1], units(b)[1] + FORMS[b].count("d"))

        def pairs(b):
            return (diffs(b)[1], 4)

        def block_done(b):
            slot_done(("y", b))
            slot_done(("b", b))

        def red(b):
            nc.vector.tensor_reduce(
                out=res[:, :, 8 * b:8 * b + 8],
                in_=stile[b][:].rearrange("p (t g w) -> p t g w", t=NT, g=8),
                axis=AX.X, op=ALU.add, negate=("s" not in FORMS[b]),
            )
            bank_done(("s", b))

        def spans(r0, r1):
            if r0 < 2 < r1:
                return [(r0, 2), (2, r1)]
            return [(r0, r1)] if r0 < r1 else []

        def rests(b):
            for (r0, r1) in spans(*units(b)) + spans(*pairs(b)):
                neg_rest(b, r0, r1)

        def products(b):
            for (r0, r1) in spans(*units(b)) + spans(*pairs(b)):
                mul(b, r0, r1)

        def late_products(b):
            for (r0, r1) in spans(*diffs(b)):
                mul(b, r0, r1)

        def subtract(b):
            if diffs(b)[1] > 0:
                diff(b, 0, diffs(b)[1])

        idle_ps = bank("idle", [P, TOK], F32, "idle_ps")

        def idle_mm(count):
            for n in range(count):
                nc.tensor.matmul(out=idle_ps[:], lhsT=idle[:, 0:P], rhs=idle[:], start=True, stop=True)

        def regroup(dst, src, c0=0, c1=TOK):
            nc.vector.tensor_copy(
                out=dst[:, 4 * c0:4 * c1].rearrange("p (c i t) -> p c t i", i=4, t=4),
                in_=src[:, :, c0:c1].rearrange("p t (c i) -> p c t i", i=4),
            )

        idle_mm(IDLE1)
        cat_ps = bank("cat", [P, TOK], BF16, "cat_ps")
        for t in range(NT):
            nc.tensor.transpose(out=cat_ps[:, t * P:(t + 1) * P], in_=cat[:, t, :],
                                identity=ident_bf[:])
        cat_t = slot("cat_t", [P, TOK], BF16, "cat_t")
        nc.vector.tensor_copy(out=cat_t[:], in_=cat_ps[:])
        bias_ps = bank("bias", [P, P], BF16, "bias_ps")
        nc.tensor.transpose(out=bias_ps[:], in_=brow[:], identity=ident_bf[:])
        bh = const.tile([P, 4], F32, name="bh")
        nc.vector.tensor_copy(out=bh[:], in_=bias_ps[:, 0:4])

        w1g = slot("w1g", [P, 4 * HN], BF16, "w1g")
        regroup(w1g, raw1)
        h_sb = slot("h_sb", [P, 4, TOK], BF16, "h_sb")
        for j in range(4):
            hp = bank(("h", j), [P, TOK], F32, "hp")
            nc.tensor.matmul(out=hp[:], lhsT=wh[:, j * P:(j + 1) * P], rhs=cat_t[:],
                             start=True, stop=True)
            if j != V_RELU:
                nc.scalar.activation(out=h_sb[:, j, :], in_=hp[:], func=ACT.Relu,
                                     bias=bh[:, j:j + 1], scale=1.0)
            else:
                nc.vector.tensor_scalar(out=h_sb[:, j, :], in0=hp[:], scalar1=bh[:, j:j + 1],
                                        scalar2=0.0, op0=ALU.add, op1=ALU.max)
            bank_done(("h", j))

        w1_codes, w1_plane = code_room(1)
        nc.vector.quantize_mx(out=w1_codes.bitcast(FP8X4), scales=w1_plane, in_=w1g[:])
        b1c = const.tile([P, 4], F32, name="b1c")
        nc.vector.tensor_copy(out=b1c[:], in_=bias_ps[:, 4:8])
        b1e = const.tile([P, 4], F32, name="b1e")
        nc.vector.tensor_scalar_add(out=b1e[:], in0=bias_ps[:, 4:8], scalar1=math.log(SA))

        halves = [slice(0, HALF), slice(HALF, TOK)]
        hg = slot("hg", [P, 4 * TOK], BF16, "hg")
        h_codes, h_plane = code_room(2)
        for h in range(2):
            regroup(hg, h_sb, h * HALF, (h + 1) * HALF)
            nc.vector.quantize_mx(out=h_codes[:, halves[h]].bitcast(FP8X4), scales=h_plane[:, halves[h]],
                                  in_=hg[:, 4 * h * HALF:4 * (h + 1) * HALF])
        b2_ps = bank("b2", [P, 2 * P], F32, "b2_ps")
        for s in range(2):
            nc.tensor.transpose(
                out=b2_ps[:, s * P:(s + 1) * P],
                in_=b2rows[:].bitcast(F32).rearrange("p (q s) -> p s q", s=2)[:, s, :],
                identity=ident_f[:],
            )
        nb2 = const.tile([P, 4 * NBLK], F32, name="nb2")
        nb2_v = nb2[:].rearrange("p (b s e) -> p b s e", s=2, e=2)
        for s in range(2):
            nc.vector.tensor_scalar_mul(
                out=nb2_v[:, :, s, :],
                in0=b2_ps[:, s * P:s * P + NBLK].bitcast(BF16).rearrange("p (b e) -> p b e", e=2),
                scalar1=-1.0,
            )
        prep_copy(0, on_scalar=True)
        e_sb = slot("e_sb", [P, 4, TOK], F32, "e_sb")
        r_sb = slot("r_sb", [P, 4, TOK], F32, "r_sb")
        tg = slot("tg", [P, 4 * TOK], BF16, "tg")
        t_codes = const.tile([P, TOK], U32, name="t_codes", align_bytes=64)
        t_plane = const.tile([P, TOK], U8, name="t_plane", align_bytes=64)
        idle_mm(IDLE2)
        for key in ("cat", "bias", "b2", "idle"):
            bank_done(key)
        tps = {}
        for h in range(2):
            for m in range(4):
                tps[(h, m)] = bank(("t", h, m), [P, HALF], F32, "tp")
                nc.tensor.matmul_mx(
                    out=tps[(h, m)][:],
                    lhsT=w1_codes[:, m * P:(m + 1) * P].bitcast(FP8X4),
                    lhsT_scale=w1_plane[:, m * P:(m + 1) * P],
                    rhs=h_codes[:, halves[h]].bitcast(FP8X4),
                    rhs_scale=h_plane[:, halves[h]],
                    start=True,
                    stop=True,
                )

        def exps(h):
            for m in range(4):
                nc.scalar.activation(out=e_sb[:, m, halves[h]], in_=tps[(h, m)][:], func=ACT.Exp,
                                     bias=b1e[:, m:m + 1], scale=1.0)

        def relus(h, on_scalar, on_vector):
            for m in on_scalar:
                nc.scalar.activation(out=r_sb[:, m, halves[h]], in_=tps[(h, m)][:], func=ACT.Relu,
                                     bias=b1c[:, m:m + 1], scale=1.0)
            for m in on_vector:
                nc.vector.tensor_scalar(out=r_sb[:, m, halves[h]], in0=tps[(h, m)][:], scalar1=b1c[:, m:m + 1],
                                        scalar2=0.0, op0=ALU.add, op1=ALU.max)

        def clamp(h):
            for m in (0, 2):
                nc.vector.tensor_scalar(out=e_sb[:, m:m + 2, halves[h]], in0=e_sb[:, m:m + 2, halves[h]],
                                        scalar1=SA, scalar2=-SA, op0=ALU.min, op1=ALU.add)

        def add(h):
            nc.vector.scalar_tensor_tensor(
                out=tg[:, 4 * h * HALF:4 * (h + 1) * HALF].rearrange("p (c t) -> p c t", t=4),
                in0=r_sb[:, :, halves[h]].rearrange("p t c -> p c t"),
                scalar=SELU_SCALE,
                in1=e_sb[:, :, halves[h]].rearrange("p t c -> p c t"),
                op0=ALU.mult, op1=ALU.add)

        def t_quant(h):
            nc.vector.quantize_mx(out=t_codes[:, halves[h]].bitcast(FP8X4), scales=t_plane[:, halves[h]],
                                  in_=tg[:, 4 * h * HALF:4 * (h + 1) * HALF])

        exps(0)
        relus(0, S_H0, [m for m in range(4) if m not in S_H0])
        clamp(0)
        add(0)
        exps(1)
        relus(1, S_H1, [m for m in range(4) if m not in S_H1])
        nc.scalar.activation(out=warm[:], in_=eps_b[:], func=ACT.Sigmoid)
        prep_quant(0)
        t_quant(0)
        clamp(1)
        prep_copy(1, 0, 1)
        add(1)
        t_quant(1)
        for h in range(2):
            for m in range(4):
                bank_done(("t", h, m))
        for key in ("ident_bf", "idle", "brow", "b2rows", "cat", "wh", "raw1", "cat_t", "w1g", "h_sb", "hg", "e_sb", "r_sb", "tg"):
            slot_done(key)
        prep_copy(1, 1, 2)
        prep_quant(1)
        prep_copy(2)
        prep_quant(2)
        prep_copy(3)

        res = const.tile([P, NT, CH // 64], F32, name="res")

        end = NBLK - 1
        for b in range(NBLK):
            if b == 0:
                for t0 in (0, HALF):
                    for r in range(4):
                        mx(b, r, t0, t0 + HALF)
                        sig(b, r, t0, t0 + HALF)
            else:
                for r in range(4):
                    mx(b, r)
                    sig(b, r)
            prep_to(min(b + NCODE, NBLK - 1))
            if "s" in FORMS[b]:
                below_one(b)
            if b == NBLK - 3:
                imgt(0, 0)
                imgt(0, 1)
            if b == NBLK - 2:
                imgt(1, 0)
                imgt(1, 1)
        slot_done("codes")

        def products_late(h):
            late_products(h)
            if "d" in FORMS[h]:
                bank_done(("i", h, 1))

        def sums_of(h):
            sums(h, btile, *diffs(h))
            sums(h, btile, *pairs(h))
            sums(h, ytile, *units(h))
            sums(h, ytile, *pairs(h))
            sums(h, ytile, *diffs(h))
            block_done(h)

        log_b(0, 0, 2)
        log_b(0, 2, 4)
        rests(0)
        stored = 0
        for g in range(NBLK + LAG):
            if g == 0:
                log_a(0, 0, 2)
                log_a(0, 2, 4)
                log_b(1)
            elif g == 1:
                log_a(1)
                log_b(2)
            elif g < end:
                log_b(g + 1)
                log_a(g)
            elif g == end:
                for r in range(4):
                    log_a(g, r, r + 1)
            h = g - LAG
            if g == NBLK:
                sums_of(end)
            if 0 <= h < end:
                products_late(h)
            if g < end:
                products(g)
            elif g == end:
                for r in range(4):
                    mul(g, r, r + 1)
            if g < NBLK:
                subtract(g)
                bank_done(("i", g, 0))
                if "d" not in FORMS[g]:
                    bank_done(("i", g, 1))
            if g + 2 < NBLK:
                imgt(g + 2, 0)
            if g + 1 < NBLK:
                rests(g + 1)
            if 0 <= h < end:
                sums_of(h)
            if 0 < h < end:
                red(h - 1)
            if g == NBLK:
                red(end)
            if g + 2 < NBLK:
                imgt(g + 2, 1)
            if h in (10, 18):
                nc.sync.dma_start(out=out_v[:, :, 8 * stored:8 * h], in_=res[:, :, 8 * stored:8 * h])
                stored = h
        red(end - 1)
        nc.sync.dma_start(out=out_v[:, :, 8 * stored:], in_=res[:, :, 8 * stored:])
